import numpy as np
import ml_dtypes


def mxq(x, axis, fmt="e4m3"):
    dtype, down = {"e4m3": (ml_dtypes.float8_e4m3fn, 7), "e5m2": (ml_dtypes.float8_e5m2, 14)}[fmt]
    v = np.moveaxis(np.asarray(x, np.float32).astype(ml_dtypes.bfloat16).astype(np.float64), axis, -1)
    blocks = v.reshape(v.shape[:-1] + (-1, 32))
    amax = np.abs(blocks).max(-1, keepdims=True)
    byte = np.maximum(np.where(amax > 0, np.frexp(amax)[1] - 1 + 127, 0) - down, 1)
    scale = np.exp2(byte - 127.0)
    codes = (blocks / scale).astype(np.float32).astype(dtype).astype(np.float64)
    return np.moveaxis((codes * scale).reshape(v.shape), -1, axis)


WIDE = False


def mx_kscale(k):
    if not WIDE:
        return np.ones(k)
    levels = np.array([10, -10, 5, -5, 0])
    a = np.random.permutation(np.resize(levels, k // 512 * 4)).reshape(k // 512, 4)
    idx = np.arange(k)
    return np.exp2(a[idx // 512, idx % 128 // 32])


BF16 = ml_dtypes.bfloat16


def bf(x):
    return np.asarray(x, np.float32).astype(BF16)


def f64(x):
    return np.asarray(x).astype(np.float64)


B, SQ, SV, DV, DQ, DK, DO, H = 8, 512, 512, 1024, 640, 512, 512, 4
DHK = DK // H


def heads(x):
    b, s, d = x.shape
    return x.reshape(b, s, H, d // H).transpose(0, 2, 1, 3)


def sigmoid(a):
    return 1.0 / (1.0 + np.exp(-a))


def setup_inputs():
    s = mx_kscale(DV)
    kept = (np.random.uniform(size=(B, SV)) < 0.9).astype(np.float64)
    k_offset = np.random.standard_normal(DK) * 0.6
    return {"q": bf(np.random.standard_normal((B, SQ, DK)) * 1.5),
            "k": bf(np.random.standard_normal((B, SV, DK)) * 1.5 + k_offset),
            "pre_value_key": bf(np.random.standard_normal((B, SV, DV)) * s),
            "Wv": bf(np.random.standard_normal((DV, DO)) * 1.5 / np.sqrt(DV) / s[:, None]),
            "bv": bf(np.random.standard_normal(DO) * 0.3),
            "value_key_masks": bf(kept),
            "value_key_counts": bf(np.maximum(kept.sum(-1), 1.0)),
            "overall_gain": bf(1.0 + 0.2 * np.random.standard_normal((1, H, 1, 1))),
            "overall_bias": bf(-0.5 + 0.5 * np.random.standard_normal((1, H, 1, 1))),
            "pre_query": bf(np.random.standard_normal((B, SQ, DQ)))}


def reference(q, k, pre_value_key, Wv, bv, value_key_masks, value_key_counts, overall_gain, overall_bias, pre_query):
    qh, kh = heads(f64(q)), heads(f64(k))
    v = heads((mxq(f64(pre_value_key), 2, "e4m3") @ mxq(f64(Wv), 0, "e4m3")) + f64(bv))
    scores = qh @ kh.transpose(0, 1, 3, 2) / np.sqrt(DHK)
    mask = f64(value_key_masks)
    pooled = (scores * mask[:, None, None, :]).sum(-1, keepdims=True)
    pooled = pooled / f64(value_key_counts)[:, None, None, None]
    w = sigmoid(pooled * f64(overall_gain) + f64(overall_bias))
    sm = scores + np.where(mask == 0, -np.inf, 0.0)[:, None, None, :]
    e = np.exp(sm - sm.max(-1, keepdims=True))
    h = (mxq(e, 3, "e4m3") @ mxq(v, 2, "e4m3")) / e.sum(-1, keepdims=True)
    pq = f64(pre_query)
    mix = heads(pq[:, :, :DO]) * (1.0 - w) + h * w
    mix = mix.transpose(0, 2, 1, 3).reshape(B, SQ, DO)
    return np.concatenate([mix, pq[:, :, DO:]], axis=-1)

@@ -1,0 +1,400 @@
+import math
+from contextlib import ExitStack
+
+import concourse.mybir as mybir
+from concourse.masks import make_identity
+
+F32 = mybir.dt.float32
+BF16 = mybir.dt.bfloat16
+U32 = mybir.dt.uint32
+U8 = mybir.dt.uint8
+FP8X4 = mybir.dt.float8_e4m3fn_x4
+ALU = mybir.AluOpType
+ACT = mybir.ActivationFunctionType
+AXIS = mybir.AxisListType
+
+P = 128
+PACK = 4
+BATCH = 8
+SEQ = 512
+TILES = SEQ // P
+D_FEAT = 1024
+PASSES = D_FEAT // (P * PACK)
+HEADS = 4
+HEAD = 128
+D_MODEL = HEADS * HEAD
+D_OUT = 640
+INV_SQRT_HEAD = 1.0 / math.sqrt(HEAD)
+MASKED = -1.0e30
+
+FLOPS = 2 * BATCH * SEQ * D_FEAT * D_MODEL + 2 * 2 * BATCH * HEADS * SEQ * SEQ * HEAD
+
+
+def tile_multiheadedselfattention_pa_t_kernel(
+    tc,
+    q,
+    k,
+    pre_value_key,
+    Wv,
+    bv,
+    value_key_masks,
+    value_key_counts,
+    overall_gain,
+    overall_bias,
+    pre_query,
+    out,
+):
+    nc = tc.nc
+    with ExitStack() as stack:
+        const = stack.enter_context(tc.tile_pool(name="const", bufs=1))
+        loads = stack.enter_context(tc.tile_pool(name="loads", bufs=2))
+        per_batch = stack.enter_context(tc.tile_pool(name="per_batch", bufs=2))
+        per_head = stack.enter_context(tc.tile_pool(name="per_head", bufs=2))
+        psum_scores = stack.enter_context(tc.psum_pool(name="psum_scores", bufs=3))
+        psum_turn = stack.enter_context(tc.psum_pool(name="psum_turn", bufs=2))
+        psum_one = stack.enter_context(tc.psum_pool(name="psum_one", bufs=1))
+
+        loaded = {}
+        ready = {}
+        numerators = {}
+
+        def load_batch(b):
+            q_sb = loads.tile([P, TILES, D_MODEL], BF16)
+            nc.sync.dma_start(out=q_sb[:], in_=q[b].rearrange("(p r) c -> p r c", r=TILES))
+            k_sb = loads.tile([P, TILES, D_MODEL], BF16)
+            nc.sync.dma_start(out=k_sb[:], in_=k[b].rearrange("(p r) c -> p r c", r=TILES))
+            feat_sb = loads.tile([P, TILES, D_FEAT], BF16)
+            nc.sync.dma_start(
+                out=feat_sb[:], in_=pre_value_key[b].rearrange("(p r) c -> p r c", r=TILES)
+            )
+            stream_sb = loads.tile([P, TILES, D_OUT], BF16)
+            nc.sync.dma_start(
+                out=stream_sb[:], in_=pre_query[b].rearrange("(p r) c -> p r c", r=TILES)
+            )
+            loaded[b] = (q_sb, k_sb, feat_sb, stream_sb)
+
+        load_batch(0)
+
+        ident_bf = const.tile([P, P], BF16)
+        make_identity(nc, ident_bf[:])
+        ident_f = const.tile([P, P], F32)
+        make_identity(nc, ident_f[:])
+
+        w_raw = const.tile([P, PASSES, PACK, D_MODEL], BF16)
+        nc.sync.dma_start(
+            out=w_raw[:].rearrange("w g (u e) d -> w (g u) (e d)", u=2, e=2),
+            in_=Wv.rearrange("(g u w e) d -> w (g u) (e d)", g=PASSES, u=2, e=2),
+        )
+        load_batch(1)
+
+        mask_rows = const.tile([P, BATCH, SEQ], BF16)
+        nc.scalar.dma_start(
+            out=mask_rows[:].rearrange("p b s -> p (b s)"),
+            in_=value_key_masks.rearrange("b s -> (b s)").partition_broadcast(P),
+        )
+        mask_cols = const.tile([P, BATCH, TILES], BF16)
+        nc.scalar.dma_start(
+            out=mask_cols[:], in_=value_key_masks.rearrange("b (p a) -> p b a", a=TILES)
+        )
+        bv_rows = const.tile([P, D_MODEL], BF16)
+        nc.scalar.dma_start(out=bv_rows[:], in_=bv.partition_broadcast(P))
+        counts = const.tile([P, BATCH], BF16)
+        nc.scalar.dma_start(out=counts[:], in_=value_key_counts.partition_broadcast(P))
+        gain = const.tile([P, HEADS], BF16)
+        nc.scalar.dma_start(
+            out=gain[:], in_=overall_gain.rearrange("a h c d -> (a h c d)").partition_broadcast(P)
+        )
+        gate_bias = const.tile([P, HEADS], BF16)
+        nc.scalar.dma_start(
+            out=gate_bias[:],
+            in_=overall_bias.rearrange("a h c d -> (a h c d)").partition_broadcast(P),
+        )
+
+        inv_count = const.tile([P, BATCH], F32)
+        nc.vector.reciprocal(out=inv_count[:], in_=counts[:])
+        neg_gain = const.tile([P, HEADS], F32)
+        nc.vector.tensor_scalar_mul(out=neg_gain[:], in0=gain[:], scalar1=-INV_SQRT_HEAD)
+        neg_gate_bias = const.tile([P, HEADS], F32)
+        nc.vector.tensor_scalar_mul(out=neg_gate_bias[:], in0=gate_bias[:], scalar1=-1.0)
+
+        w_grouped = const.tile([P, PASSES, D_MODEL * PACK], BF16, align_bytes=64)
+        w_codes = const.tile([P, PASSES, D_MODEL], U32, align_bytes=64)
+        w_scales = const.tile([P, PASSES, D_MODEL], U8, align_bytes=64)
+        for g in range(PASSES):
+            nc.vector.tensor_copy(
+                out=w_grouped[:, g, :].rearrange("w (d t) -> w d t", t=PACK),
+                in_=w_raw[:, g, :, :].rearrange("w t d -> w d t"),
+            )
+        for g in range(PASSES):
+            nc.vector.quantize_mx(
+                out=w_codes[:, g, :].bitcast(FP8X4),
+                scales=w_scales[:, g, :],
+                in_=w_grouped[:, g, :],
+            )
+
+        def prepare_batch(b):
+            q_sb, k_sb, feat_sb, stream_sb = loaded[b]
+
+            mask_bias = per_batch.tile([P, TILES, P], BF16)
+            nc.vector.tensor_scalar(
+                out=mask_bias[:],
+                in0=mask_rows[:, b, :].rearrange("p (x a) -> p a x", a=TILES),
+                scalar1=0.0,
+                scalar2=MASKED,
+                op0=ALU.is_equal,
+                op1=ALU.mult,
+            )
+
+            q_turned = per_batch.tile([P, HEADS, TILES, P], BF16)
+            k_turned = per_batch.tile([P, HEADS, TILES, P], BF16)
+            for source, turned in ((q_sb, q_turned), (k_sb, k_turned)):
+                for n in range(HEADS):
+                    turn_bf = psum_turn.tile([P, TILES, P], BF16, tag="turn")
+                    for r in range(TILES):
+                        nc.tensor.transpose(
+                            out=turn_bf[:, r, :],
+                            in_=source[:, r, n * HEAD : (n + 1) * HEAD],
+                            identity=ident_bf[:],
+                        )
+                    nc.scalar.copy(out=turned[:, n, :, :], in_=turn_bf[:])
+
+            feat_words = feat_sb[:].bitcast(F32)
+            feat_grouped = per_batch.tile([P, TILES * PASSES * P * PACK], BF16, align_bytes=64)
+            feat_grouped_words = (
+                feat_grouped[:]
+                .bitcast(F32)
+                .rearrange("w (a g x u) -> w a g x u", a=TILES, g=PASSES, u=2)
+            )
+            for a in range(TILES):
+                turn_f = psum_turn.tile([P, PASSES, 2, P], F32, tag="turn")
+                for g in range(PASSES):
+                    for u in range(2):
+                        first = (2 * g + u) * P
+                        nc.tensor.transpose(
+                            out=turn_f[:, g, u, :],
+                            in_=feat_words[:, a, first : first + P],
+                            identity=ident_f[:],
+                        )
+                nc.scalar.copy(
+                    out=feat_grouped_words[:, a], in_=turn_f[:].rearrange("w g u x -> w g x u")
+                )
+            feat_codes = per_batch.tile([P, TILES * PASSES * P], U32, align_bytes=64)
+            feat_scales = per_batch.tile([P, TILES * PASSES * P], U8, align_bytes=64)
+            nc.vector.quantize_mx(
+                out=feat_codes[:].bitcast(FP8X4), scales=feat_scales[:], in_=feat_grouped[:]
+            )
+
+            v_grouped = per_batch.tile([P, D_MODEL * PACK], BF16, align_bytes=64)
+            for n in range(HEADS):
+                head_cols = slice(n * HEAD, (n + 1) * HEAD)
+                v_ps = psum_one.tile([P, TILES, HEAD], F32, tag="v")
+                for a in range(TILES):
+                    for g in range(PASSES):
+                        key_cols = slice((a * PASSES + g) * P, (a * PASSES + g + 1) * P)
+                        nc.tensor.matmul_mx(
+                            out=v_ps[:, a, :],
+                            lhsT=feat_codes[:, key_cols].bitcast(FP8X4),
+                            lhsT_scale=feat_scales[:, key_cols],
+                            rhs=w_codes[:, g, head_cols].bitcast(FP8X4),
+                            rhs_scale=w_scales[:, g, head_cols],
+                            start=(g == 0),
+                            stop=(g == PASSES - 1),
+                        )
+                nc.vector.tensor_tensor(
+                    out=v_grouped[:, n * HEAD * PACK : (n + 1) * HEAD * PACK].rearrange(
+                        "p (d a) -> p d a", a=PACK
+                    ),
+                    in0=v_ps[:].rearrange("p a d -> p d a"),
+                    in1=bv_rows[:, head_cols].unsqueeze(2).to_broadcast([P, HEAD, PACK]),
+                    op=ALU.add,
+                )
+            v_codes = per_batch.tile([P, D_MODEL], U32, align_bytes=64)
+            v_scales = per_batch.tile([P, D_MODEL], U8, align_bytes=64)
+            nc.vector.quantize_mx(
+                out=v_codes[:].bitcast(FP8X4), scales=v_scales[:], in_=v_grouped[:]
+            )
+
+            key_sum_ps = psum_one.tile([P, HEADS], F32, tag="small")
+            for n in range(HEADS):
+                for a in range(TILES):
+                    nc.tensor.matmul(
+                        out=key_sum_ps[:, n : n + 1],
+                        lhsT=k_sb[:, a, n * HEAD : (n + 1) * HEAD],
+                        rhs=mask_cols[:, b, a : a + 1],
+                        start=(a == 0),
+                        stop=(a == TILES - 1),
+                    )
+            key_sum = per_batch.tile([P, HEADS, 2], BF16)
+            nc.vector.tensor_copy(out=key_sum[:, :, 0], in_=key_sum_ps[:])
+            nc.vector.tensor_tensor(
+                out=key_sum[:, :, 1], in0=key_sum_ps[:], in1=key_sum[:, :, 0], op=ALU.subtract
+            )
+            pooled_ps = psum_one.tile([P, TILES, HEADS, 2], F32, tag="small")
+            for r in range(TILES):
+                for n in range(HEADS):
+                    nc.tensor.matmul(
+                        out=pooled_ps[:, r, n, :],
+                        lhsT=q_turned[:, n, r, :],
+                        rhs=key_sum[:, n, :],
+                        start=True,
+                        stop=True,
+                    )
+            pooled = per_batch.tile([P, TILES, HEADS], F32)
+            nc.vector.tensor_reduce(out=pooled[:], in_=pooled_ps[:], axis=AXIS.X, op=ALU.add)
+            neg_z = per_batch.tile([P, TILES, HEADS], F32)
+            nc.vector.scalar_tensor_tensor(
+                out=neg_z[:],
+                in0=pooled[:],
+                scalar=inv_count[:, b : b + 1],
+                in1=neg_gain[:].unsqueeze(1).to_broadcast([P, TILES, HEADS]),
+                op0=ALU.mult,
+                op1=ALU.mult,
+            )
+            nc.vector.tensor_tensor(
+                out=neg_z[:],
+                in0=neg_z[:],
+                in1=neg_gate_bias[:].unsqueeze(1).to_broadcast([P, TILES, HEADS]),
+                op=ALU.add,
+            )
+            gate = per_batch.tile([P, TILES, HEADS], F32)
+            nc.scalar.activation(out=gate[:], in_=neg_z[:], func=ACT.Exp)
+            nc.vector.tensor_scalar_add(out=gate[:], in0=gate[:], scalar1=1.0)
+            nc.vector.reciprocal(out=gate[:], in_=gate[:])
+            one_minus_gate = per_batch.tile([P, TILES, HEADS], F32)
+            nc.vector.tensor_scalar(
+                out=one_minus_gate[:],
+                in0=gate[:],
+                scalar1=-1.0,
+                scalar2=1.0,
+                op0=ALU.mult,
+                op1=ALU.add,
+            )
+
+            result = per_batch.tile([P, TILES, D_OUT], F32)
+            nc.gpsimd.tensor_tensor(
+                out=result[:, :, 0:D_MODEL].rearrange("p r (n d) -> p r n d", n=HEADS),
+                in0=stream_sb[:, :, 0:D_MODEL].rearrange("p r (n d) -> p r n d", n=HEADS),
+                in1=one_minus_gate[:].unsqueeze(3).to_broadcast([P, TILES, HEADS, HEAD]),
+                op=ALU.mult,
+            )
+            nc.gpsimd.tensor_scalar(
+                out=result[:, :, D_MODEL:D_OUT],
+                in0=stream_sb[:, :, D_MODEL:D_OUT],
+                scalar1=1.0,
+                scalar2=0.0,
+                op0=ALU.mult,
+                op1=ALU.add,
+            )
+            ready[b] = (mask_bias, q_turned, k_turned, v_codes, v_scales, gate, result)
+
+        def softmax_numerators(b, n):
+            mask_bias, q_turned, k_turned = ready[b][0:3]
+            masked_scores = per_head.tile([P, TILES, SEQ], F32)
+            for r in range(TILES):
+                scores_ps = psum_scores.tile([P, SEQ], F32, tag="scores")
+                nc.tensor.matmul(
+                    out=scores_ps[:],
+                    lhsT=q_turned[:, n, r, :],
+                    rhs=k_turned[:, n, :, :].rearrange("c a x -> c (a x)"),
+                    start=True,
+                    stop=True,
+                )
+                nc.vector.scalar_tensor_tensor(
+                    out=masked_scores[:, r, :],
+                    in0=scores_ps[:],
+                    scalar=INV_SQRT_HEAD,
+                    in1=mask_bias[:].rearrange("p a x -> p (a x)"),
+                    op0=ALU.mult,
+                    op1=ALU.add,
+                )
+            neg_max = per_head.tile([P, TILES], F32)
+            nc.vector.tensor_reduce(
+                out=neg_max[:], in_=masked_scores[:], axis=AXIS.X, op=ALU.max, negate=True
+            )
+            e_sb = per_head.tile([P, TILES, SEQ], BF16)
+            row_sum = per_head.tile([P, TILES], F32)
+            for r in range(TILES):
+                nc.scalar.activation(
+                    out=e_sb[:, r, :].rearrange("p (u w e) -> p u w e", u=2, e=2),
+                    in_=masked_scores[:, r, :].rearrange("p (u e w) -> p u w e", u=2, e=2),
+                    func=ACT.Exp,
+                    bias=neg_max[:, r : r + 1],
+                    scale=1.0,
+                    accum_out=row_sum[:, r : r + 1],
+                )
+            numerators[(b, n)] = (e_sb, row_sum)
+
+        def attend_and_blend(b, n):
+            v_codes, v_scales, gate, result = ready[b][3:7]
+            e_sb, row_sum = numerators[(b, n)]
+            head_cols = slice(n * HEAD, (n + 1) * HEAD)
+
+            e_words = e_sb[:].bitcast(F32)
+            e_grouped = per_head.tile([P, SEQ * PACK], BF16, align_bytes=64)
+            e_grouped_words = (
+                e_grouped[:].bitcast(F32).rearrange("w (r i u) -> w r i u", r=TILES, u=2)
+            )
+            for half in range(TILES // 2):
+                turn_e = psum_turn.tile([P, 2, 2, P], F32, tag="turn")
+                for rr in range(2):
+                    for u in range(2):
+                        nc.tensor.transpose(
+                            out=turn_e[:, rr, u, :],
+                            in_=e_words[:, 2 * half + rr, u * P : (u + 1) * P],
+                            identity=ident_f[:],
+                        )
+                nc.scalar.copy(
+                    out=e_grouped_words[:, 2 * half : 2 * half + 2],
+                    in_=turn_e[:].rearrange("w r u i -> w r i u"),
+                )
+            e_codes = per_head.tile([P, SEQ], U32, align_bytes=64)
+            e_scales = per_head.tile([P, SEQ], U8, align_bytes=64)
+            nc.vector.quantize_mx(
+                out=e_codes[:].bitcast(FP8X4), scales=e_scales[:], in_=e_grouped[:]
+            )
+
+            h_ps = psum_one.tile([P, TILES, HEAD], F32, tag="h")
+            for r in range(TILES):
+                query_cols = slice(r * P, (r + 1) * P)
+                nc.tensor.matmul_mx(
+                    out=h_ps[:, r, :],
+                    lhsT=e_codes[:, query_cols].bitcast(FP8X4),
+                    lhsT_scale=e_scales[:, query_cols],
+                    rhs=v_codes[:, head_cols].bitcast(FP8X4),
+                    rhs_scale=v_scales[:, head_cols],
+                    start=True,
+                    stop=True,
+                )
+
+            gate_over_sum = per_head.tile([P, TILES], F32)
+            nc.vector.reciprocal(out=gate_over_sum[:], in_=row_sum[:])
+            nc.vector.tensor_tensor(
+                out=gate_over_sum[:], in0=gate_over_sum[:], in1=gate[:, :, n], op=ALU.mult
+            )
+            h_gated = per_head.tile([P, TILES, HEAD], F32)
+            for r in range(TILES):
+                nc.scalar.activation(
+                    out=h_gated[:, r, :],
+                    in_=h_ps[:, r, :],
+                    func=ACT.Copy,
+                    scale=gate_over_sum[:, r : r + 1],
+                )
+            nc.gpsimd.tensor_tensor(
+                out=result[:, :, head_cols], in0=result[:, :, head_cols], in1=h_gated[:], op=ALU.add
+            )
+            if n == HEADS - 1:
+                nc.gpsimd.dma_start(
+                    out=out[b].rearrange("(p r) c -> p r c", r=TILES), in_=result[:]
+                )
+
+        heads = [(b, n) for b in range(BATCH) for n in range(HEADS)]
+        prepare_batch(0)
+        softmax_numerators(0, 0)
+        for position, (b, n) in enumerate(heads):
+            if n == 1 and b + 1 < BATCH:
+                prepare_batch(b + 1)
+                if b + 2 < BATCH:
+                    load_batch(b + 2)
+            if position + 1 < len(heads):
+                softmax_numerators(*heads[position + 1])
+            attend_and_blend(b, n)

@@ -52,7 +52,7 @@ def tile_multiheadedselfattention_pa_t_kernel(
         per_head = stack.enter_context(tc.tile_pool(name="per_head", bufs=2))
         psum_scores = stack.enter_context(tc.psum_pool(name="psum_scores", bufs=3))
         psum_turn = stack.enter_context(tc.psum_pool(name="psum_turn", bufs=2))
-        psum_one = stack.enter_context(tc.psum_pool(name="psum_one", bufs=1))
+        psum_sums = stack.enter_context(tc.psum_pool(name="psum_sums", bufs=3))
 
         loaded = {}
         ready = {}
@@ -87,11 +87,6 @@ def tile_multiheadedselfattention_pa_t_kernel(
         )
         load_batch(1)
 
-        mask_rows = const.tile([P, BATCH, SEQ], BF16)
-        nc.scalar.dma_start(
-            out=mask_rows[:].rearrange("p b s -> p (b s)"),
-            in_=value_key_masks.rearrange("b s -> (b s)").partition_broadcast(P),
-        )
         mask_cols = const.tile([P, BATCH, TILES], BF16)
         nc.scalar.dma_start(
             out=mask_cols[:], in_=value_key_masks.rearrange("b (p a) -> p b a", a=TILES)
@@ -108,6 +103,16 @@ def tile_multiheadedselfattention_pa_t_kernel(
         nc.scalar.dma_start(
             out=gate_bias[:],
             in_=overall_bias.rearrange("a h c d -> (a h c d)").partition_broadcast(P),
+        )
+
+        mask_bias = const.tile([P, BATCH, TILES], F32)
+        nc.vector.tensor_scalar(
+            out=mask_bias[:],
+            in0=mask_cols[:],
+            scalar1=0.0,
+            scalar2=MASKED,
+            op0=ALU.is_equal,
+            op1=ALU.mult,
         )
 
         inv_count = const.tile([P, BATCH], F32)
@@ -134,16 +139,6 @@ def tile_multiheadedselfattention_pa_t_kernel(
 
         def prepare_batch(b):
             q_sb, k_sb, feat_sb, stream_sb = loaded[b]
-
-            mask_bias = per_batch.tile([P, TILES, P], BF16)
-            nc.vector.tensor_scalar(
-                out=mask_bias[:],
-                in0=mask_rows[:, b, :].rearrange("p (x a) -> p a x", a=TILES),
-                scalar1=0.0,
-                scalar2=MASKED,
-                op0=ALU.is_equal,
-                op1=ALU.mult,
-            )
 
             q_turned = per_batch.tile([P, HEADS, TILES, P], BF16)
             k_turned = per_batch.tile([P, HEADS, TILES, P], BF16)
@@ -187,7 +182,7 @@ def tile_multiheadedselfattention_pa_t_kernel(
             v_grouped = per_batch.tile([P, D_MODEL * PACK], BF16, align_bytes=64)
             for n in range(HEADS):
                 head_cols = slice(n * HEAD, (n + 1) * HEAD)
-                v_ps = psum_one.tile([P, TILES, HEAD], F32, tag="v")
+                v_ps = psum_sums.tile([P, TILES, HEAD], F32, tag="sums")
                 for a in range(TILES):
                     for g in range(PASSES):
                         key_cols = slice((a * PASSES + g) * P, (a * PASSES + g + 1) * P)
@@ -214,7 +209,7 @@ def tile_multiheadedselfattention_pa_t_kernel(
                 out=v_codes[:].bitcast(FP8X4), scales=v_scales[:], in_=v_grouped[:]
             )
 
-            key_sum_ps = psum_one.tile([P, HEADS], F32, tag="small")
+            key_sum_ps = psum_sums.tile([P, HEADS], F32, tag="sums")
             for n in range(HEADS):
                 for a in range(TILES):
                     nc.tensor.matmul(
@@ -229,7 +224,7 @@ def tile_multiheadedselfattention_pa_t_kernel(
             nc.vector.tensor_tensor(
                 out=key_sum[:, :, 1], in0=key_sum_ps[:], in1=key_sum[:, :, 0], op=ALU.subtract
             )
-            pooled_ps = psum_one.tile([P, TILES, HEADS, 2], F32, tag="small")
+            pooled_ps = psum_sums.tile([P, TILES, HEADS, 2], F32, tag="sums")
             for r in range(TILES):
                 for n in range(HEADS):
                     nc.tensor.matmul(
@@ -285,47 +280,54 @@ def tile_multiheadedselfattention_pa_t_kernel(
                 op0=ALU.mult,
                 op1=ALU.add,
             )
-            ready[b] = (mask_bias, q_turned, k_turned, v_codes, v_scales, gate, result)
+            ready[b] = (q_turned, k_turned, v_codes, v_scales, gate, result)
 
         def softmax_numerators(b, n):
-            mask_bias, q_turned, k_turned = ready[b][0:3]
-            masked_scores = per_head.tile([P, TILES, SEQ], F32)
+            q_turned, k_turned = ready[b][0:2]
+            neg_scores = per_head.tile([P, TILES, SEQ], F32)
+            neg_max = per_head.tile([P, TILES], F32)
             for r in range(TILES):
-                scores_ps = psum_scores.tile([P, SEQ], F32, tag="scores")
+                scores_ps = psum_scores.tile([P, TILES, P], F32, tag="scores")
                 nc.tensor.matmul(
-                    out=scores_ps[:],
+                    out=scores_ps[:].rearrange("p a x -> p (a x)"),
                     lhsT=q_turned[:, n, r, :],
                     rhs=k_turned[:, n, :, :].rearrange("c a x -> c (a x)"),
                     start=True,
-                    stop=True,
+                    stop=False,
                 )
-                nc.vector.scalar_tensor_tensor(
-                    out=masked_scores[:, r, :],
-                    in0=scores_ps[:],
-                    scalar=INV_SQRT_HEAD,
-                    in1=mask_bias[:].rearrange("p a x -> p (a x)"),
+                for a in range(TILES):
+                    nc.tensor.matmul(
+                        out=scores_ps[:, a, :],
+                        lhsT=mask_bias[:, b, a : a + 1].to_broadcast([P, P]),
+                        rhs=ident_f[:],
+                        is_transpose=True,
+                        start=False,
+                        stop=(a == TILES - 1),
+                    )
+                nc.vector.tensor_scalar(
+                    out=neg_scores[:, r, :],
+                    in0=scores_ps[:].rearrange("p a x -> p (a x)"),
+                    scalar1=-INV_SQRT_HEAD,
+                    scalar2=None,
                     op0=ALU.mult,
-                    op1=ALU.add,
+                    op1=ALU.min,
+                    accum_out=neg_max[:, r : r + 1],
                 )
-            neg_max = per_head.tile([P, TILES], F32)
-            nc.vector.tensor_reduce(
-                out=neg_max[:], in_=masked_scores[:], axis=AXIS.X, op=ALU.max, negate=True
-            )
             e_sb = per_head.tile([P, TILES, SEQ], BF16)
             row_sum = per_head.tile([P, TILES], F32)
             for r in range(TILES):
                 nc.scalar.activation(
                     out=e_sb[:, r, :].rearrange("p (u w e) -> p u w e", u=2, e=2),
-                    in_=masked_scores[:, r, :].rearrange("p (u e w) -> p u w e", u=2, e=2),
+                    in_=neg_scores[:, r, :].rearrange("p (u e w) -> p u w e", u=2, e=2),
                     func=ACT.Exp,
                     bias=neg_max[:, r : r + 1],
-                    scale=1.0,
+                    scale=-1.0,
                     accum_out=row_sum[:, r : r + 1],
                 )
             numerators[(b, n)] = (e_sb, row_sum)
 
         def attend_and_blend(b, n):
-            v_codes, v_scales, gate, result = ready[b][3:7]
+            v_codes, v_scales, gate, result = ready[b][2:6]
             e_sb, row_sum = numerators[(b, n)]
             head_cols = slice(n * HEAD, (n + 1) * HEAD)
 
@@ -343,7 +345,8 @@ def tile_multiheadedselfattention_pa_t_kernel(
                             in_=e_words[:, 2 * half + rr, u * P : (u + 1) * P],
                             identity=ident_f[:],
                         )
-                nc.scalar.copy(
+                copy_out = nc.vector.tensor_copy if half == 0 else nc.scalar.copy
+                copy_out(
                     out=e_grouped_words[:, 2 * half : 2 * half + 2],
                     in_=turn_e[:].rearrange("w r u i -> w r i u"),
                 )
@@ -353,7 +356,7 @@ def tile_multiheadedselfattention_pa_t_kernel(
                 out=e_codes[:].bitcast(FP8X4), scales=e_scales[:], in_=e_grouped[:]
             )
 
-            h_ps = psum_one.tile([P, TILES, HEAD], F32, tag="h")
+            h_ps = psum_sums.tile([P, TILES, HEAD], F32, tag="sums")
             for r in range(TILES):
                 query_cols = slice(r * P, (r + 1) * P)
                 nc.tensor.matmul_mx(

@@ -49,10 +49,10 @@ def tile_multiheadedselfattention_pa_t_kernel(
         const = stack.enter_context(tc.tile_pool(name="const", bufs=1))
         loads = stack.enter_context(tc.tile_pool(name="loads", bufs=2))
         per_batch = stack.enter_context(tc.tile_pool(name="per_batch", bufs=2))
-        per_head = stack.enter_context(tc.tile_pool(name="per_head", bufs=2))
+        per_head = stack.enter_context(tc.tile_pool(name="per_head", bufs=3))
         psum_scores = stack.enter_context(tc.psum_pool(name="psum_scores", bufs=3))
         psum_turn = stack.enter_context(tc.psum_pool(name="psum_turn", bufs=2))
-        psum_sums = stack.enter_context(tc.psum_pool(name="psum_sums", bufs=3))
+        psum_one = stack.enter_context(tc.psum_pool(name="psum_one", bufs=1))
 
         loaded = {}
         ready = {}
@@ -87,6 +87,11 @@ def tile_multiheadedselfattention_pa_t_kernel(
         )
         load_batch(1)
 
+        mask_rows = const.tile([P, BATCH, SEQ], BF16)
+        nc.scalar.dma_start(
+            out=mask_rows[:].rearrange("p b s -> p (b s)"),
+            in_=value_key_masks.rearrange("b s -> (b s)").partition_broadcast(P),
+        )
         mask_cols = const.tile([P, BATCH, TILES], BF16)
         nc.scalar.dma_start(
             out=mask_cols[:], in_=value_key_masks.rearrange("b (p a) -> p b a", a=TILES)
@@ -105,20 +110,17 @@ def tile_multiheadedselfattention_pa_t_kernel(
             in_=overall_bias.rearrange("a h c d -> (a h c d)").partition_broadcast(P),
         )
 
-        mask_bias = const.tile([P, BATCH, TILES], F32)
-        nc.vector.tensor_scalar(
-            out=mask_bias[:],
-            in0=mask_cols[:],
-            scalar1=0.0,
-            scalar2=MASKED,
-            op0=ALU.is_equal,
-            op1=ALU.mult,
-        )
-
         inv_count = const.tile([P, BATCH], F32)
         nc.vector.reciprocal(out=inv_count[:], in_=counts[:])
         neg_gain = const.tile([P, HEADS], F32)
         nc.vector.tensor_scalar_mul(out=neg_gain[:], in0=gain[:], scalar1=-INV_SQRT_HEAD)
+        neg_gain_over_count = const.tile([P, BATCH, HEADS], F32)
+        nc.vector.tensor_tensor(
+            out=neg_gain_over_count[:],
+            in0=neg_gain[:].unsqueeze(1).to_broadcast([P, BATCH, HEADS]),
+            in1=inv_count[:].unsqueeze(2).to_broadcast([P, BATCH, HEADS]),
+            op=ALU.mult,
+        )
         neg_gate_bias = const.tile([P, HEADS], F32)
         nc.vector.tensor_scalar_mul(out=neg_gate_bias[:], in0=gate_bias[:], scalar1=-1.0)
 
@@ -139,6 +141,16 @@ def tile_multiheadedselfattention_pa_t_kernel(
 
         def prepare_batch(b):
             q_sb, k_sb, feat_sb, stream_sb = loaded[b]
+
+            mask_bias = per_batch.tile([P, TILES, P], BF16)
+            nc.gpsimd.tensor_scalar(
+                out=mask_bias[:],
+                in0=mask_rows[:, b, :].rearrange("p (x a) -> p a x", a=TILES),
+                scalar1=0.0,
+                scalar2=MASKED,
+                op0=ALU.is_equal,
+                op1=ALU.mult,
+            )
 
             q_turned = per_batch.tile([P, HEADS, TILES, P], BF16)
             k_turned = per_batch.tile([P, HEADS, TILES, P], BF16)
@@ -182,7 +194,7 @@ def tile_multiheadedselfattention_pa_t_kernel(
             v_grouped = per_batch.tile([P, D_MODEL * PACK], BF16, align_bytes=64)
             for n in range(HEADS):
                 head_cols = slice(n * HEAD, (n + 1) * HEAD)
-                v_ps = psum_sums.tile([P, TILES, HEAD], F32, tag="sums")
+                v_ps = psum_one.tile([P, TILES, HEAD], F32, tag="v")
                 for a in range(TILES):
                     for g in range(PASSES):
                         key_cols = slice((a * PASSES + g) * P, (a * PASSES + g + 1) * P)
@@ -209,7 +221,7 @@ def tile_multiheadedselfattention_pa_t_kernel(
                 out=v_codes[:].bitcast(FP8X4), scales=v_scales[:], in_=v_grouped[:]
             )
 
-            key_sum_ps = psum_sums.tile([P, HEADS], F32, tag="sums")
+            key_sum_ps = psum_one.tile([P, HEADS], F32, tag="small")
             for n in range(HEADS):
                 for a in range(TILES):
                     nc.tensor.matmul(
@@ -220,11 +232,13 @@ def tile_multiheadedselfattention_pa_t_kernel(
                         stop=(a == TILES - 1),
                     )
             key_sum = per_batch.tile([P, HEADS, 2], BF16)
-            nc.vector.tensor_copy(out=key_sum[:, :, 0], in_=key_sum_ps[:])
-            nc.vector.tensor_tensor(
-                out=key_sum[:, :, 1], in0=key_sum_ps[:], in1=key_sum[:, :, 0], op=ALU.subtract
+            key_sum_f = per_batch.tile([P, HEADS], F32)
+            nc.scalar.copy(out=key_sum[:, :, 0], in_=key_sum_ps[:])
+            nc.scalar.copy(out=key_sum_f[:], in_=key_sum_ps[:])
+            nc.gpsimd.tensor_tensor(
+                out=key_sum[:, :, 1], in0=key_sum_f[:], in1=key_sum[:, :, 0], op=ALU.subtract
             )
-            pooled_ps = psum_sums.tile([P, TILES, HEADS, 2], F32, tag="sums")
+            pooled_ps = psum_one.tile([P, TILES, HEADS, 2], F32, tag="small")
             for r in range(TILES):
                 for n in range(HEADS):
                     nc.tensor.matmul(
@@ -234,18 +248,19 @@ def tile_multiheadedselfattention_pa_t_kernel(
                         start=True,
                         stop=True,
                     )
-            pooled = per_batch.tile([P, TILES, HEADS], F32)
-            nc.vector.tensor_reduce(out=pooled[:], in_=pooled_ps[:], axis=AXIS.X, op=ALU.add)
+            pooled_parts = per_batch.tile([P, TILES, HEADS, 2], F32)
+            nc.scalar.copy(out=pooled_parts[:], in_=pooled_ps[:])
             neg_z = per_batch.tile([P, TILES, HEADS], F32)
-            nc.vector.scalar_tensor_tensor(
-                out=neg_z[:],
-                in0=pooled[:],
-                scalar=inv_count[:, b : b + 1],
-                in1=neg_gain[:].unsqueeze(1).to_broadcast([P, TILES, HEADS]),
-                op0=ALU.mult,
-                op1=ALU.mult,
+            nc.gpsimd.tensor_tensor(
+                out=neg_z[:], in0=pooled_parts[:, :, :, 0], in1=pooled_parts[:, :, :, 1], op=ALU.add
             )
-            nc.vector.tensor_tensor(
+            nc.gpsimd.tensor_tensor(
+                out=neg_z[:],
+                in0=neg_z[:],
+                in1=neg_gain_over_count[:, b, :].unsqueeze(1).to_broadcast([P, TILES, HEADS]),
+                op=ALU.mult,
+            )
+            nc.gpsimd.tensor_tensor(
                 out=neg_z[:],
                 in0=neg_z[:],
                 in1=neg_gate_bias[:].unsqueeze(1).to_broadcast([P, TILES, HEADS]),
@@ -253,10 +268,10 @@ def tile_multiheadedselfattention_pa_t_kernel(
             )
             gate = per_batch.tile([P, TILES, HEADS], F32)
             nc.scalar.activation(out=gate[:], in_=neg_z[:], func=ACT.Exp)
-            nc.vector.tensor_scalar_add(out=gate[:], in0=gate[:], scalar1=1.0)
+            nc.gpsimd.tensor_scalar_add(out=gate[:], in0=gate[:], scalar1=1.0)
             nc.vector.reciprocal(out=gate[:], in_=gate[:])
             one_minus_gate = per_batch.tile([P, TILES, HEADS], F32)
-            nc.vector.tensor_scalar(
+            nc.gpsimd.tensor_scalar(
                 out=one_minus_gate[:],
                 in0=gate[:],
                 scalar1=-1.0,
@@ -280,54 +295,51 @@ def tile_multiheadedselfattention_pa_t_kernel(
                 op0=ALU.mult,
                 op1=ALU.add,
             )
-            ready[b] = (q_turned, k_turned, v_codes, v_scales, gate, result)
+            ready[b] = (mask_bias, q_turned, k_turned, v_codes, v_scales, gate, result)
 
         def softmax_numerators(b, n):
-            q_turned, k_turned = ready[b][0:2]
-            neg_scores = per_head.tile([P, TILES, SEQ], F32)
+            mask_bias, q_turned, k_turned = ready[b][0:3]
+            masked_scores = per_head.tile([P, TILES, SEQ], F32)
             neg_max = per_head.tile([P, TILES], F32)
             for r in range(TILES):
-                scores_ps = psum_scores.tile([P, TILES, P], F32, tag="scores")
+                scores_ps = psum_scores.tile([P, SEQ], F32, tag="scores")
                 nc.tensor.matmul(
-                    out=scores_ps[:].rearrange("p a x -> p (a x)"),
+                    out=scores_ps[:],
                     lhsT=q_turned[:, n, r, :],
                     rhs=k_turned[:, n, :, :].rearrange("c a x -> c (a x)"),
                     start=True,
-                    stop=False,
+                    stop=True,
                 )
-                for a in range(TILES):
-                    nc.tensor.matmul(
-                        out=scores_ps[:, a, :],
-                        lhsT=mask_bias[:, b, a : a + 1].to_broadcast([P, P]),
-                        rhs=ident_f[:],
-                        is_transpose=True,
-                        start=False,
-                        stop=(a == TILES - 1),
-                    )
-                nc.vector.tensor_scalar(
-                    out=neg_scores[:, r, :],
-                    in0=scores_ps[:].rearrange("p a x -> p (a x)"),
-                    scalar1=-INV_SQRT_HEAD,
-                    scalar2=None,
+                nc.vector.scalar_tensor_tensor(
+                    out=masked_scores[:, r, :],
+                    in0=scores_ps[:],
+                    scalar=INV_SQRT_HEAD,
+                    in1=mask_bias[:].rearrange("p a x -> p (a x)"),
                     op0=ALU.mult,
-                    op1=ALU.min,
-                    accum_out=neg_max[:, r : r + 1],
+                    op1=ALU.add,
+                )
+                nc.vector.tensor_reduce(
+                    out=neg_max[:, r : r + 1],
+                    in_=masked_scores[:, r, :],
+                    axis=AXIS.X,
+                    op=ALU.max,
+                    negate=True,
                 )
             e_sb = per_head.tile([P, TILES, SEQ], BF16)
             row_sum = per_head.tile([P, TILES], F32)
             for r in range(TILES):
                 nc.scalar.activation(
                     out=e_sb[:, r, :].rearrange("p (u w e) -> p u w e", u=2, e=2),
-                    in_=neg_scores[:, r, :].rearrange("p (u e w) -> p u w e", u=2, e=2),
+                    in_=masked_scores[:, r, :].rearrange("p (u e w) -> p u w e", u=2, e=2),
                     func=ACT.Exp,
                     bias=neg_max[:, r : r + 1],
-                    scale=-1.0,
+                    scale=1.0,
                     accum_out=row_sum[:, r : r + 1],
                 )
             numerators[(b, n)] = (e_sb, row_sum)
 
         def attend_and_blend(b, n):
-            v_codes, v_scales, gate, result = ready[b][2:6]
+            v_codes, v_scales, gate, result = ready[b][3:7]
             e_sb, row_sum = numerators[(b, n)]
             head_cols = slice(n * HEAD, (n + 1) * HEAD)
 
@@ -345,8 +357,7 @@ def tile_multiheadedselfattention_pa_t_kernel(
                             in_=e_words[:, 2 * half + rr, u * P : (u + 1) * P],
                             identity=ident_f[:],
                         )
-                copy_out = nc.vector.tensor_copy if half == 0 else nc.scalar.copy
-                copy_out(
+                nc.scalar.copy(
                     out=e_grouped_words[:, 2 * half : 2 * half + 2],
                     in_=turn_e[:].rearrange("w r u i -> w r i u"),
                 )
@@ -356,7 +367,7 @@ def tile_multiheadedselfattention_pa_t_kernel(
                 out=e_codes[:].bitcast(FP8X4), scales=e_scales[:], in_=e_grouped[:]
             )
 
-            h_ps = psum_sums.tile([P, TILES, HEAD], F32, tag="sums")
+            h_ps = psum_one.tile([P, TILES, HEAD], F32, tag="h")
             for r in range(TILES):
                 query_cols = slice(r * P, (r + 1) * P)
                 nc.tensor.matmul_mx(
@@ -371,7 +382,7 @@ def tile_multiheadedselfattention_pa_t_kernel(
 
             gate_over_sum = per_head.tile([P, TILES], F32)
             nc.vector.reciprocal(out=gate_over_sum[:], in_=row_sum[:])
-            nc.vector.tensor_tensor(
+            nc.gpsimd.tensor_tensor(
                 out=gate_over_sum[:], in0=gate_over_sum[:], in1=gate[:, :, n], op=ALU.mult
             )
             h_gated = per_head.tile([P, TILES, HEAD], F32)

@@ -53,6 +53,7 @@ def tile_multiheadedselfattention_pa_t_kernel(
         psum_scores = stack.enter_context(tc.psum_pool(name="psum_scores", bufs=3))
         psum_turn = stack.enter_context(tc.psum_pool(name="psum_turn", bufs=2))
         psum_one = stack.enter_context(tc.psum_pool(name="psum_one", bufs=1))
+        psum_h = stack.enter_context(tc.psum_pool(name="psum_h", bufs=2))
 
         loaded = {}
         ready = {}
@@ -194,7 +195,7 @@ def tile_multiheadedselfattention_pa_t_kernel(
             v_grouped = per_batch.tile([P, D_MODEL * PACK], BF16, align_bytes=64)
             for n in range(HEADS):
                 head_cols = slice(n * HEAD, (n + 1) * HEAD)
-                v_ps = psum_one.tile([P, TILES, HEAD], F32, tag="v")
+                v_ps = psum_one.tile([P, TILES, HEAD], F32, tag="sums")
                 for a in range(TILES):
                     for g in range(PASSES):
                         key_cols = slice((a * PASSES + g) * P, (a * PASSES + g + 1) * P)
@@ -221,7 +222,7 @@ def tile_multiheadedselfattention_pa_t_kernel(
                 out=v_codes[:].bitcast(FP8X4), scales=v_scales[:], in_=v_grouped[:]
             )
 
-            key_sum_ps = psum_one.tile([P, HEADS], F32, tag="small")
+            key_sum_ps = psum_one.tile([P, HEADS], F32, tag="sums")
             for n in range(HEADS):
                 for a in range(TILES):
                     nc.tensor.matmul(
@@ -238,7 +239,7 @@ def tile_multiheadedselfattention_pa_t_kernel(
             nc.gpsimd.tensor_tensor(
                 out=key_sum[:, :, 1], in0=key_sum_f[:], in1=key_sum[:, :, 0], op=ALU.subtract
             )
-            pooled_ps = psum_one.tile([P, TILES, HEADS, 2], F32, tag="small")
+            pooled_ps = psum_one.tile([P, TILES, HEADS, 2], F32, tag="sums")
             for r in range(TILES):
                 for n in range(HEADS):
                     nc.tensor.matmul(
@@ -367,19 +368,6 @@ def tile_multiheadedselfattention_pa_t_kernel(
                 out=e_codes[:].bitcast(FP8X4), scales=e_scales[:], in_=e_grouped[:]
             )
 
-            h_ps = psum_one.tile([P, TILES, HEAD], F32, tag="h")
-            for r in range(TILES):
-                query_cols = slice(r * P, (r + 1) * P)
-                nc.tensor.matmul_mx(
-                    out=h_ps[:, r, :],
-                    lhsT=e_codes[:, query_cols].bitcast(FP8X4),
-                    lhsT_scale=e_scales[:, query_cols],
-                    rhs=v_codes[:, head_cols].bitcast(FP8X4),
-                    rhs_scale=v_scales[:, head_cols],
-                    start=True,
-                    stop=True,
-                )
-
             gate_over_sum = per_head.tile([P, TILES], F32)
             nc.vector.reciprocal(out=gate_over_sum[:], in_=row_sum[:])
             nc.gpsimd.tensor_tensor(
@@ -387,9 +375,20 @@ def tile_multiheadedselfattention_pa_t_kernel(
             )
             h_gated = per_head.tile([P, TILES, HEAD], F32)
             for r in range(TILES):
+                query_cols = slice(r * P, (r + 1) * P)
+                h_ps = psum_h.tile([P, D_MODEL], F32, tag="h")
+                nc.tensor.matmul_mx(
+                    out=h_ps[:],
+                    lhsT=e_codes[:, query_cols].bitcast(FP8X4),
+                    lhsT_scale=e_scales[:, query_cols],
+                    rhs=v_codes[:].bitcast(FP8X4),
+                    rhs_scale=v_scales[:],
+                    start=True,
+                    stop=True,
+                )
                 nc.scalar.activation(
                     out=h_gated[:, r, :],
-                    in_=h_ps[:, r, :],
+                    in_=h_ps[:, head_cols],
                     func=ACT.Copy,
                     scale=gate_over_sum[:, r : r + 1],
                 )

@@ -24,6 +24,7 @@ HEADS = 4
 HEAD = 128
 D_MODEL = HEADS * HEAD
 D_OUT = 640
+UNITS = BATCH * HEADS
 INV_SQRT_HEAD = 1.0 / math.sqrt(HEAD)
 MASKED = -1.0e30
 
@@ -46,56 +47,57 @@ def tile_multiheadedselfattention_pa_t_kernel(
 ):
     nc = tc.nc
     with ExitStack() as stack:
+        stack.enter_context(tc.manual_schedule())
         const = stack.enter_context(tc.tile_pool(name="const", bufs=1))
-        loads = stack.enter_context(tc.tile_pool(name="loads", bufs=2))
-        per_batch = stack.enter_context(tc.tile_pool(name="per_batch", bufs=2))
-        per_head = stack.enter_context(tc.tile_pool(name="per_head", bufs=3))
+        two = stack.enter_context(tc.tile_pool(name="two", bufs=2))
+        three = stack.enter_context(tc.tile_pool(name="three", bufs=3))
+        five = stack.enter_context(tc.tile_pool(name="five", bufs=5))
         psum_scores = stack.enter_context(tc.psum_pool(name="psum_scores", bufs=3))
         psum_turn = stack.enter_context(tc.psum_pool(name="psum_turn", bufs=2))
         psum_one = stack.enter_context(tc.psum_pool(name="psum_one", bufs=1))
-        psum_h = stack.enter_context(tc.psum_pool(name="psum_h", bufs=2))
 
-        loaded = {}
-        ready = {}
-        numerators = {}
+        kept = {}
+
+        def live(u):
+            return 0 <= u < UNITS
+
+        def head_columns(u):
+            return slice((u % HEADS) * HEAD, (u % HEADS + 1) * HEAD)
 
         def load_batch(b):
-            q_sb = loads.tile([P, TILES, D_MODEL], BF16)
+            q_sb = three.tile([P, TILES, D_MODEL], BF16)
             nc.sync.dma_start(out=q_sb[:], in_=q[b].rearrange("(p r) c -> p r c", r=TILES))
-            k_sb = loads.tile([P, TILES, D_MODEL], BF16)
+            k_sb = three.tile([P, TILES, D_MODEL], BF16)
             nc.sync.dma_start(out=k_sb[:], in_=k[b].rearrange("(p r) c -> p r c", r=TILES))
-            feat_sb = loads.tile([P, TILES, D_FEAT], BF16)
+            feat_sb = two.tile([P, TILES, D_FEAT], BF16)
             nc.sync.dma_start(
                 out=feat_sb[:], in_=pre_value_key[b].rearrange("(p r) c -> p r c", r=TILES)
             )
-            stream_sb = loads.tile([P, TILES, D_OUT], BF16)
+            stream_sb = three.tile([P, TILES, D_OUT], BF16)
             nc.sync.dma_start(
                 out=stream_sb[:], in_=pre_query[b].rearrange("(p r) c -> p r c", r=TILES)
             )
-            loaded[b] = (q_sb, k_sb, feat_sb, stream_sb)
-
-        load_batch(0)
-
-        ident_bf = const.tile([P, P], BF16)
-        make_identity(nc, ident_bf[:])
-        ident_f = const.tile([P, P], F32)
-        make_identity(nc, ident_f[:])
+            kept[("q", b)] = q_sb
+            kept[("k", b)] = k_sb
+            kept[("feat", b)] = feat_sb
+            kept[("stream", b)] = stream_sb
 
         w_raw = const.tile([P, PASSES, PACK, D_MODEL], BF16)
         nc.sync.dma_start(
             out=w_raw[:].rearrange("w g (u e) d -> w (g u) (e d)", u=2, e=2),
             in_=Wv.rearrange("(g u w e) d -> w (g u) (e d)", g=PASSES, u=2, e=2),
         )
+        load_batch(0)
         load_batch(1)
 
+        mask_cols = const.tile([P, BATCH, TILES], BF16)
+        nc.scalar.dma_start(
+            out=mask_cols[:], in_=value_key_masks.rearrange("b (p a) -> p b a", a=TILES)
+        )
         mask_rows = const.tile([P, BATCH, SEQ], BF16)
         nc.scalar.dma_start(
             out=mask_rows[:].rearrange("p b s -> p (b s)"),
             in_=value_key_masks.rearrange("b s -> (b s)").partition_broadcast(P),
-        )
-        mask_cols = const.tile([P, BATCH, TILES], BF16)
-        nc.scalar.dma_start(
-            out=mask_cols[:], in_=value_key_masks.rearrange("b (p a) -> p b a", a=TILES)
         )
         bv_rows = const.tile([P, D_MODEL], BF16)
         nc.scalar.dma_start(out=bv_rows[:], in_=bv.partition_broadcast(P))
@@ -111,10 +113,39 @@ def tile_multiheadedselfattention_pa_t_kernel(
             in_=overall_bias.rearrange("a h c d -> (a h c d)").partition_broadcast(P),
         )
 
+        ident_bf = const.tile([P, P], BF16)
+        make_identity(nc, ident_bf[:])
+        ident_f = const.tile([P, P], F32)
+        make_identity(nc, ident_f[:])
+
+        def prepare_masks(b):
+            kept_keys = two.tile([P, TILES, P], BF16)
+            nc.gpsimd.tensor_tensor(
+                out=kept_keys[:],
+                in0=ident_bf[:].unsqueeze(1).to_broadcast([P, TILES, P]),
+                in1=mask_cols[:, b, :].unsqueeze(2).to_broadcast([P, TILES, P]),
+                op=ALU.mult,
+            )
+            mask_bias = two.tile([P, TILES, P], BF16)
+            nc.gpsimd.tensor_scalar(
+                out=mask_bias[:],
+                in0=mask_rows[:, b, :].rearrange("p (x a) -> p a x", a=TILES),
+                scalar1=0.0,
+                scalar2=MASKED,
+                op0=ALU.is_equal,
+                op1=ALU.mult,
+            )
+            kept[("kept_keys", b)] = kept_keys
+            kept[("mask_bias", b)] = mask_bias
+
+        prepare_masks(0)
+
         inv_count = const.tile([P, BATCH], F32)
         nc.vector.reciprocal(out=inv_count[:], in_=counts[:])
         neg_gain = const.tile([P, HEADS], F32)
         nc.vector.tensor_scalar_mul(out=neg_gain[:], in0=gain[:], scalar1=-INV_SQRT_HEAD)
+        neg_gate_bias = const.tile([P, HEADS], F32)
+        nc.vector.tensor_scalar_mul(out=neg_gate_bias[:], in0=gate_bias[:], scalar1=-1.0)
         neg_gain_over_count = const.tile([P, BATCH, HEADS], F32)
         nc.vector.tensor_tensor(
             out=neg_gain_over_count[:],
@@ -122,8 +153,6 @@ def tile_multiheadedselfattention_pa_t_kernel(
             in1=inv_count[:].unsqueeze(2).to_broadcast([P, BATCH, HEADS]),
             op=ALU.mult,
         )
-        neg_gate_bias = const.tile([P, HEADS], F32)
-        nc.vector.tensor_scalar_mul(out=neg_gate_bias[:], in0=gate_bias[:], scalar1=-1.0)
 
         w_grouped = const.tile([P, PASSES, D_MODEL * PACK], BF16, align_bytes=64)
         w_codes = const.tile([P, PASSES, D_MODEL], U32, align_bytes=64)
@@ -140,274 +169,354 @@ def tile_multiheadedselfattention_pa_t_kernel(
                 in_=w_grouped[:, g, :],
             )
 
-        def prepare_batch(b):
-            q_sb, k_sb, feat_sb, stream_sb = loaded[b]
-
-            mask_bias = per_batch.tile([P, TILES, P], BF16)
-            nc.gpsimd.tensor_scalar(
-                out=mask_bias[:],
-                in0=mask_rows[:, b, :].rearrange("p (x a) -> p a x", a=TILES),
-                scalar1=0.0,
-                scalar2=MASKED,
-                op0=ALU.is_equal,
-                op1=ALU.mult,
-            )
-
-            q_turned = per_batch.tile([P, HEADS, TILES, P], BF16)
-            k_turned = per_batch.tile([P, HEADS, TILES, P], BF16)
-            for source, turned in ((q_sb, q_turned), (k_sb, k_turned)):
-                for n in range(HEADS):
-                    turn_bf = psum_turn.tile([P, TILES, P], BF16, tag="turn")
-                    for r in range(TILES):
-                        nc.tensor.transpose(
-                            out=turn_bf[:, r, :],
-                            in_=source[:, r, n * HEAD : (n + 1) * HEAD],
-                            identity=ident_bf[:],
-                        )
-                    nc.scalar.copy(out=turned[:, n, :, :], in_=turn_bf[:])
-
-            feat_words = feat_sb[:].bitcast(F32)
-            feat_grouped = per_batch.tile([P, TILES * PASSES * P * PACK], BF16, align_bytes=64)
-            feat_grouped_words = (
-                feat_grouped[:]
-                .bitcast(F32)
-                .rearrange("w (a g x u) -> w a g x u", a=TILES, g=PASSES, u=2)
-            )
-            for a in range(TILES):
-                turn_f = psum_turn.tile([P, PASSES, 2, P], F32, tag="turn")
-                for g in range(PASSES):
-                    for u in range(2):
-                        first = (2 * g + u) * P
-                        nc.tensor.transpose(
-                            out=turn_f[:, g, u, :],
-                            in_=feat_words[:, a, first : first + P],
-                            identity=ident_f[:],
-                        )
-                nc.scalar.copy(
-                    out=feat_grouped_words[:, a], in_=turn_f[:].rearrange("w g u x -> w g x u")
-                )
-            feat_codes = per_batch.tile([P, TILES * PASSES * P], U32, align_bytes=64)
-            feat_scales = per_batch.tile([P, TILES * PASSES * P], U8, align_bytes=64)
-            nc.vector.quantize_mx(
-                out=feat_codes[:].bitcast(FP8X4), scales=feat_scales[:], in_=feat_grouped[:]
-            )
-
-            v_grouped = per_batch.tile([P, D_MODEL * PACK], BF16, align_bytes=64)
-            for n in range(HEADS):
-                head_cols = slice(n * HEAD, (n + 1) * HEAD)
-                v_ps = psum_one.tile([P, TILES, HEAD], F32, tag="sums")
-                for a in range(TILES):
-                    for g in range(PASSES):
-                        key_cols = slice((a * PASSES + g) * P, (a * PASSES + g + 1) * P)
-                        nc.tensor.matmul_mx(
-                            out=v_ps[:, a, :],
-                            lhsT=feat_codes[:, key_cols].bitcast(FP8X4),
-                            lhsT_scale=feat_scales[:, key_cols],
-                            rhs=w_codes[:, g, head_cols].bitcast(FP8X4),
-                            rhs_scale=w_scales[:, g, head_cols],
-                            start=(g == 0),
-                            stop=(g == PASSES - 1),
-                        )
-                nc.vector.tensor_tensor(
-                    out=v_grouped[:, n * HEAD * PACK : (n + 1) * HEAD * PACK].rearrange(
-                        "p (d a) -> p d a", a=PACK
-                    ),
-                    in0=v_ps[:].rearrange("p a d -> p d a"),
-                    in1=bv_rows[:, head_cols].unsqueeze(2).to_broadcast([P, HEAD, PACK]),
-                    op=ALU.add,
-                )
-            v_codes = per_batch.tile([P, D_MODEL], U32, align_bytes=64)
-            v_scales = per_batch.tile([P, D_MODEL], U8, align_bytes=64)
-            nc.vector.quantize_mx(
-                out=v_codes[:].bitcast(FP8X4), scales=v_scales[:], in_=v_grouped[:]
-            )
-
-            key_sum_ps = psum_one.tile([P, HEADS], F32, tag="sums")
-            for n in range(HEADS):
-                for a in range(TILES):
-                    nc.tensor.matmul(
-                        out=key_sum_ps[:, n : n + 1],
-                        lhsT=k_sb[:, a, n * HEAD : (n + 1) * HEAD],
-                        rhs=mask_cols[:, b, a : a + 1],
-                        start=(a == 0),
-                        stop=(a == TILES - 1),
+        def turn_features(piece):
+            b, a = piece // TILES, piece % TILES
+            feat_words = kept[("feat", b)][:].bitcast(F32)
+            turn_f = psum_turn.tile([P, PASSES, 2, P], F32, tag="turn")
+            for g in range(PASSES):
+                for u in range(2):
+                    first = (2 * g + u) * P
+                    nc.tensor.transpose(
+                        out=turn_f[:, g, u, :],
+                        in_=feat_words[:, a, first : first + P],
+                        identity=ident_f[:],
                     )
-            key_sum = per_batch.tile([P, HEADS, 2], BF16)
-            key_sum_f = per_batch.tile([P, HEADS], F32)
-            nc.scalar.copy(out=key_sum[:, :, 0], in_=key_sum_ps[:])
-            nc.scalar.copy(out=key_sum_f[:], in_=key_sum_ps[:])
-            nc.gpsimd.tensor_tensor(
-                out=key_sum[:, :, 1], in0=key_sum_f[:], in1=key_sum[:, :, 0], op=ALU.subtract
+            feat_grouped = two.tile([P, PASSES * P * PACK], BF16, align_bytes=64)
+            nc.scalar.copy(
+                out=feat_grouped[:].bitcast(F32).rearrange("w (g x u) -> w g x u", g=PASSES, u=2),
+                in_=turn_f[:].rearrange("w g u x -> w g x u"),
             )
-            pooled_ps = psum_one.tile([P, TILES, HEADS, 2], F32, tag="sums")
+            kept[("feat_grouped", piece)] = feat_grouped
+
+        def quantise_features(piece):
+            b, a = piece // TILES, piece % TILES
+            if a == 0:
+                feat_codes = two.tile([P, TILES, PASSES * P], U32, align_bytes=64)
+                feat_scales = two.tile([P, TILES, PASSES * P], U8, align_bytes=64)
+                kept[("feat_codes", b)] = feat_codes
+                kept[("feat_scales", b)] = feat_scales
+            nc.vector.quantize_mx(
+                out=kept[("feat_codes", b)][:, a, :].bitcast(FP8X4),
+                scales=kept[("feat_scales", b)][:, a, :],
+                in_=kept[("feat_grouped", piece)][:],
+            )
+
+        def turn_q_and_k(u):
+            b = u // HEADS
+            turn_qk = psum_turn.tile([P, 2, TILES, P], BF16, tag="turn")
             for r in range(TILES):
-                for n in range(HEADS):
-                    nc.tensor.matmul(
-                        out=pooled_ps[:, r, n, :],
-                        lhsT=q_turned[:, n, r, :],
-                        rhs=key_sum[:, n, :],
-                        start=True,
-                        stop=True,
-                    )
-            pooled_parts = per_batch.tile([P, TILES, HEADS, 2], F32)
-            nc.scalar.copy(out=pooled_parts[:], in_=pooled_ps[:])
-            neg_z = per_batch.tile([P, TILES, HEADS], F32)
-            nc.gpsimd.tensor_tensor(
-                out=neg_z[:], in0=pooled_parts[:, :, :, 0], in1=pooled_parts[:, :, :, 1], op=ALU.add
+                nc.tensor.transpose(
+                    out=turn_qk[:, 0, r, :],
+                    in_=kept[("q", b)][:, r, head_columns(u)],
+                    identity=ident_bf[:],
+                )
+            for a in range(TILES):
+                nc.tensor.transpose(
+                    out=turn_qk[:, 1, a, :],
+                    in_=kept[("k", b)][:, a, head_columns(u)],
+                    identity=kept[("kept_keys", b)][:, a, :],
+                )
+            q_turned = three.tile([P, TILES, P], BF16)
+            nc.scalar.copy(out=q_turned[:], in_=turn_qk[:, 0, :, :])
+            k_turned = three.tile([P, TILES, P], BF16)
+            key_sum_f = three.tile([P, 1], F32)
+            nc.scalar.activation(
+                out=k_turned[:], in_=turn_qk[:, 1, :, :], func=ACT.Copy, accum_out=key_sum_f[:]
             )
-            nc.gpsimd.tensor_tensor(
-                out=neg_z[:],
-                in0=neg_z[:],
-                in1=neg_gain_over_count[:, b, :].unsqueeze(1).to_broadcast([P, TILES, HEADS]),
-                op=ALU.mult,
-            )
-            nc.gpsimd.tensor_tensor(
-                out=neg_z[:],
-                in0=neg_z[:],
-                in1=neg_gate_bias[:].unsqueeze(1).to_broadcast([P, TILES, HEADS]),
-                op=ALU.add,
-            )
-            gate = per_batch.tile([P, TILES, HEADS], F32)
-            nc.scalar.activation(out=gate[:], in_=neg_z[:], func=ACT.Exp)
-            nc.gpsimd.tensor_scalar_add(out=gate[:], in0=gate[:], scalar1=1.0)
-            nc.vector.reciprocal(out=gate[:], in_=gate[:])
-            one_minus_gate = per_batch.tile([P, TILES, HEADS], F32)
+            key_sum = three.tile([P, 2], BF16)
             nc.gpsimd.tensor_scalar(
-                out=one_minus_gate[:],
-                in0=gate[:],
-                scalar1=-1.0,
-                scalar2=1.0,
-                op0=ALU.mult,
-                op1=ALU.add,
-            )
-
-            result = per_batch.tile([P, TILES, D_OUT], F32)
-            nc.gpsimd.tensor_tensor(
-                out=result[:, :, 0:D_MODEL].rearrange("p r (n d) -> p r n d", n=HEADS),
-                in0=stream_sb[:, :, 0:D_MODEL].rearrange("p r (n d) -> p r n d", n=HEADS),
-                in1=one_minus_gate[:].unsqueeze(3).to_broadcast([P, TILES, HEADS, HEAD]),
-                op=ALU.mult,
-            )
-            nc.gpsimd.tensor_scalar(
-                out=result[:, :, D_MODEL:D_OUT],
-                in0=stream_sb[:, :, D_MODEL:D_OUT],
+                out=key_sum[:, 0:1],
+                in0=key_sum_f[:],
                 scalar1=1.0,
                 scalar2=0.0,
                 op0=ALU.mult,
                 op1=ALU.add,
             )
-            ready[b] = (mask_bias, q_turned, k_turned, v_codes, v_scales, gate, result)
+            nc.gpsimd.tensor_tensor(
+                out=key_sum[:, 1:2], in0=key_sum_f[:], in1=key_sum[:, 0:1], op=ALU.subtract
+            )
+            kept[("q_turned", u)] = q_turned
+            kept[("k_turned", u)] = k_turned
+            kept[("key_sum", u)] = key_sum
 
-        def softmax_numerators(b, n):
-            mask_bias, q_turned, k_turned = ready[b][0:3]
-            masked_scores = per_head.tile([P, TILES, SEQ], F32)
-            neg_max = per_head.tile([P, TILES], F32)
+        def pooled_matmuls(u):
+            pooled_ps = psum_one.tile([P, TILES, 2], F32, tag="pooled")
             for r in range(TILES):
-                scores_ps = psum_scores.tile([P, SEQ], F32, tag="scores")
                 nc.tensor.matmul(
-                    out=scores_ps[:],
-                    lhsT=q_turned[:, n, r, :],
-                    rhs=k_turned[:, n, :, :].rearrange("c a x -> c (a x)"),
+                    out=pooled_ps[:, r, :],
+                    lhsT=kept[("q_turned", u)][:, r, :],
+                    rhs=kept[("key_sum", u)][:],
                     start=True,
                     stop=True,
                 )
-                nc.vector.scalar_tensor_tensor(
-                    out=masked_scores[:, r, :],
-                    in0=scores_ps[:],
-                    scalar=INV_SQRT_HEAD,
-                    in1=mask_bias[:].rearrange("p a x -> p (a x)"),
+            kept[("pooled_ps", u)] = pooled_ps
+
+        def pooled_sum(u):
+            pooled = three.tile([P, TILES], F32)
+            nc.vector.tensor_reduce(
+                out=pooled[:], in_=kept[("pooled_ps", u)][:], axis=AXIS.X, op=ALU.add
+            )
+            kept[("pooled", u)] = pooled
+
+        def gate_denominator(u):
+            b, n = u // HEADS, u % HEADS
+            denominator = three.tile([P, TILES], F32)
+            nc.scalar.activation(
+                out=denominator[:],
+                in_=kept[("pooled", u)][:],
+                func=ACT.Exp,
+                scale=neg_gain_over_count[:, b, n : n + 1],
+                bias=neg_gate_bias[:, n : n + 1],
+            )
+            nc.gpsimd.tensor_scalar_add(out=denominator[:], in0=denominator[:], scalar1=1.0)
+            kept[("denominator", u)] = denominator
+
+        def invert(u_gate, u_sum):
+            if live(u_gate):
+                gate = five.tile([P, TILES], F32)
+                nc.vector.reciprocal(out=gate[:], in_=kept[("denominator", u_gate)][:])
+                kept[("gate", u_gate)] = gate
+            if live(u_sum):
+                inv_sum = three.tile([P, TILES], F32)
+                nc.vector.reciprocal(out=inv_sum[:], in_=kept[("row_sum", u_sum)][:])
+                kept[("inv_sum", u_sum)] = inv_sum
+
+        def start_result(u):
+            b, n = u // HEADS, u % HEADS
+            stream_sb = kept[("stream", b)]
+            if n == 0:
+                result = three.tile([P, TILES, D_OUT], F32)
+                nc.gpsimd.tensor_scalar(
+                    out=result[:, :, D_MODEL:D_OUT],
+                    in0=stream_sb[:, :, D_MODEL:D_OUT],
+                    scalar1=1.0,
+                    scalar2=0.0,
                     op0=ALU.mult,
                     op1=ALU.add,
                 )
-                nc.vector.tensor_reduce(
-                    out=neg_max[:, r : r + 1],
-                    in_=masked_scores[:, r, :],
-                    axis=AXIS.X,
-                    op=ALU.max,
-                    negate=True,
-                )
-            e_sb = per_head.tile([P, TILES, SEQ], BF16)
-            row_sum = per_head.tile([P, TILES], F32)
+                kept[("result", b)] = result
+            one_minus_gate = three.tile([P, TILES], F32)
+            nc.gpsimd.tensor_scalar(
+                out=one_minus_gate[:],
+                in0=kept[("gate", u)][:],
+                scalar1=-1.0,
+                scalar2=1.0,
+                op0=ALU.mult,
+                op1=ALU.add,
+            )
+            nc.gpsimd.tensor_tensor(
+                out=kept[("result", b)][:, :, head_columns(u)],
+                in0=stream_sb[:, :, head_columns(u)],
+                in1=one_minus_gate[:].unsqueeze(2).to_broadcast([P, TILES, HEAD]),
+                op=ALU.mult,
+            )
+
+        def score_matmul(u, r):
+            scores_ps = psum_scores.tile([P, SEQ], F32, tag="scores")
+            nc.tensor.matmul(
+                out=scores_ps[:],
+                lhsT=kept[("q_turned", u)][:, r, :],
+                rhs=kept[("k_turned", u)][:].rearrange("c a x -> c (a x)"),
+                start=True,
+                stop=True,
+            )
+            kept[("scores_ps", u, r)] = scores_ps
+
+        def add_mask(u, r):
+            if r == 0:
+                masked_scores = three.tile([P, TILES, SEQ], F32)
+                neg_max = three.tile([P, TILES], F32)
+                kept[("masked_scores", u)] = masked_scores
+                kept[("neg_max", u)] = neg_max
+            nc.vector.scalar_tensor_tensor(
+                out=kept[("masked_scores", u)][:, r, :],
+                in0=kept[("scores_ps", u, r)][:],
+                scalar=INV_SQRT_HEAD,
+                in1=kept[("mask_bias", u // HEADS)][:].rearrange("p a x -> p (a x)"),
+                op0=ALU.mult,
+                op1=ALU.add,
+            )
+
+        def row_max(u, r):
+            nc.vector.tensor_reduce(
+                out=kept[("neg_max", u)][:, r : r + 1],
+                in_=kept[("masked_scores", u)][:, r, :],
+                axis=AXIS.X,
+                op=ALU.max,
+                negate=True,
+            )
+
+        def exponentials(u):
+            e_sb = two.tile([P, TILES, SEQ], BF16)
+            row_sum = three.tile([P, TILES], F32)
             for r in range(TILES):
                 nc.scalar.activation(
                     out=e_sb[:, r, :].rearrange("p (u w e) -> p u w e", u=2, e=2),
-                    in_=masked_scores[:, r, :].rearrange("p (u e w) -> p u w e", u=2, e=2),
+                    in_=kept[("masked_scores", u)][:, r, :].rearrange(
+                        "p (u e w) -> p u w e", u=2, e=2
+                    ),
                     func=ACT.Exp,
-                    bias=neg_max[:, r : r + 1],
+                    bias=kept[("neg_max", u)][:, r : r + 1],
                     scale=1.0,
                     accum_out=row_sum[:, r : r + 1],
                 )
-            numerators[(b, n)] = (e_sb, row_sum)
+            kept[("e_sb", u)] = e_sb
+            kept[("row_sum", u)] = row_sum
 
-        def attend_and_blend(b, n):
-            v_codes, v_scales, gate, result = ready[b][3:7]
-            e_sb, row_sum = numerators[(b, n)]
-            head_cols = slice(n * HEAD, (n + 1) * HEAD)
-
-            e_words = e_sb[:].bitcast(F32)
-            e_grouped = per_head.tile([P, SEQ * PACK], BF16, align_bytes=64)
+        def turn_e(u):
+            e_words = kept[("e_sb", u)][:].bitcast(F32)
+            e_grouped = two.tile([P, SEQ * PACK], BF16, align_bytes=64)
             e_grouped_words = (
                 e_grouped[:].bitcast(F32).rearrange("w (r i u) -> w r i u", r=TILES, u=2)
             )
             for half in range(TILES // 2):
-                turn_e = psum_turn.tile([P, 2, 2, P], F32, tag="turn")
+                turn_half = psum_turn.tile([P, 2, 2, P], F32, tag="turn")
                 for rr in range(2):
-                    for u in range(2):
+                    for u2 in range(2):
                         nc.tensor.transpose(
-                            out=turn_e[:, rr, u, :],
-                            in_=e_words[:, 2 * half + rr, u * P : (u + 1) * P],
+                            out=turn_half[:, rr, u2, :],
+                            in_=e_words[:, 2 * half + rr, u2 * P : (u2 + 1) * P],
                             identity=ident_f[:],
                         )
                 nc.scalar.copy(
                     out=e_grouped_words[:, 2 * half : 2 * half + 2],
-                    in_=turn_e[:].rearrange("w r u i -> w r i u"),
+                    in_=turn_half[:].rearrange("w r u i -> w r i u"),
                 )
-            e_codes = per_head.tile([P, SEQ], U32, align_bytes=64)
-            e_scales = per_head.tile([P, SEQ], U8, align_bytes=64)
-            nc.vector.quantize_mx(
-                out=e_codes[:].bitcast(FP8X4), scales=e_scales[:], in_=e_grouped[:]
-            )
+            kept[("e_grouped", u)] = e_grouped
 
-            gate_over_sum = per_head.tile([P, TILES], F32)
-            nc.vector.reciprocal(out=gate_over_sum[:], in_=row_sum[:])
-            nc.gpsimd.tensor_tensor(
-                out=gate_over_sum[:], in0=gate_over_sum[:], in1=gate[:, :, n], op=ALU.mult
+        def project_values(u):
+            b = u // HEADS
+            v_ps = psum_one.tile([P, TILES, HEAD], F32, tag="v")
+            for a in range(TILES):
+                for g in range(PASSES):
+                    key_cols = slice(g * P, (g + 1) * P)
+                    nc.tensor.matmul_mx(
+                        out=v_ps[:, a, :],
+                        lhsT=kept[("feat_codes", b)][:, a, key_cols].bitcast(FP8X4),
+                        lhsT_scale=kept[("feat_scales", b)][:, a, key_cols],
+                        rhs=w_codes[:, g, head_columns(u)].bitcast(FP8X4),
+                        rhs_scale=w_scales[:, g, head_columns(u)],
+                        start=(g == 0),
+                        stop=(g == PASSES - 1),
+                    )
+            kept[("v_ps", u)] = v_ps
+
+        def add_value_bias(u):
+            v_grouped = two.tile([P, HEAD * PACK], BF16, align_bytes=64)
+            nc.vector.tensor_tensor(
+                out=v_grouped[:].rearrange("p (d a) -> p d a", a=PACK),
+                in0=kept[("v_ps", u)][:].rearrange("p a d -> p d a"),
+                in1=bv_rows[:, head_columns(u)].unsqueeze(2).to_broadcast([P, HEAD, PACK]),
+                op=ALU.add,
             )
-            h_gated = per_head.tile([P, TILES, HEAD], F32)
+            kept[("v_grouped", u)] = v_grouped
+
+        def quantise_e_and_v(u):
+            e_codes = two.tile([P, SEQ], U32, align_bytes=64)
+            e_scales = two.tile([P, SEQ], U8, align_bytes=64)
+            nc.vector.quantize_mx(
+                out=e_codes[:].bitcast(FP8X4), scales=e_scales[:], in_=kept[("e_grouped", u)][:]
+            )
+            v_codes = two.tile([P, HEAD], U32, align_bytes=64)
+            v_scales = two.tile([P, HEAD], U8, align_bytes=64)
+            nc.vector.quantize_mx(
+                out=v_codes[:].bitcast(FP8X4), scales=v_scales[:], in_=kept[("v_grouped", u)][:]
+            )
+            kept[("e_codes", u)] = e_codes
+            kept[("e_scales", u)] = e_scales
+            kept[("v_codes", u)] = v_codes
+            kept[("v_scales", u)] = v_scales
+
+        def attend(u):
+            h_ps = psum_one.tile([P, TILES, HEAD], F32, tag="h")
             for r in range(TILES):
                 query_cols = slice(r * P, (r + 1) * P)
-                h_ps = psum_h.tile([P, D_MODEL], F32, tag="h")
                 nc.tensor.matmul_mx(
-                    out=h_ps[:],
-                    lhsT=e_codes[:, query_cols].bitcast(FP8X4),
-                    lhsT_scale=e_scales[:, query_cols],
-                    rhs=v_codes[:].bitcast(FP8X4),
-                    rhs_scale=v_scales[:],
+                    out=h_ps[:, r, :],
+                    lhsT=kept[("e_codes", u)][:, query_cols].bitcast(FP8X4),
+                    lhsT_scale=kept[("e_scales", u)][:, query_cols],
+                    rhs=kept[("v_codes", u)][:].bitcast(FP8X4),
+                    rhs_scale=kept[("v_scales", u)][:],
                     start=True,
                     stop=True,
                 )
+            kept[("h_ps", u)] = h_ps
+
+        def gate_over_row_sum(u):
+            gate_over_sum = three.tile([P, TILES], F32)
+            nc.gpsimd.tensor_tensor(
+                out=gate_over_sum[:],
+                in0=kept[("inv_sum", u)][:],
+                in1=kept[("gate", u)][:],
+                op=ALU.mult,
+            )
+            kept[("gate_over_sum", u)] = gate_over_sum
+
+        def blend(u):
+            b, n = u // HEADS, u % HEADS
+            h_gated = two.tile([P, TILES, HEAD], F32)
+            for r in range(TILES):
                 nc.scalar.activation(
                     out=h_gated[:, r, :],
-                    in_=h_ps[:, head_cols],
+                    in_=kept[("h_ps", u)][:, r, :],
                     func=ACT.Copy,
-                    scale=gate_over_sum[:, r : r + 1],
+                    scale=kept[("gate_over_sum", u)][:, r : r + 1],
                 )
+            result = kept[("result", b)]
             nc.gpsimd.tensor_tensor(
-                out=result[:, :, head_cols], in0=result[:, :, head_cols], in1=h_gated[:], op=ALU.add
+                out=result[:, :, head_columns(u)],
+                in0=result[:, :, head_columns(u)],
+                in1=h_gated[:],
+                op=ALU.add,
             )
             if n == HEADS - 1:
                 nc.gpsimd.dma_start(
                     out=out[b].rearrange("(p r) c -> p r c", r=TILES), in_=result[:]
                 )
 
-        heads = [(b, n) for b in range(BATCH) for n in range(HEADS)]
-        prepare_batch(0)
-        softmax_numerators(0, 0)
-        for position, (b, n) in enumerate(heads):
-            if n == 1 and b + 1 < BATCH:
-                prepare_batch(b + 1)
-                if b + 2 < BATCH:
-                    load_batch(b + 2)
-            if position + 1 < len(heads):
-                softmax_numerators(*heads[position + 1])
-            attend_and_blend(b, n)
+        for i in range(-3, UNITS + 5):
+            if live(i - 4):
+                blend(i - 4)
+            if live(i - 3):
+                quantise_e_and_v(i - 3)
+                gate_over_row_sum(i - 3)
+            if live(i - 1):
+                start_result(i - 1)
+            if live(i - 2):
+                turn_e(i - 2)
+            if live(i + 2):
+                turn_q_and_k(i + 2)
+            if live(i + 3):
+                turn_features(i + 3)
+            if live(i):
+                for r in range(TILES):
+                    add_mask(i, r)
+                    if r == 0:
+                        score_matmul(i, TILES - 1)
+                    else:
+                        row_max(i, r - 1)
+            if live(i + 2):
+                quantise_features(i + 2)
+            if live(i):
+                row_max(i, TILES - 1)
+                gate_denominator(i)
+            if live(i + 1):
+                pooled_matmuls(i + 1)
+            if live(i - 2):
+                project_values(i - 2)
+                add_value_bias(i - 2)
+            if live(i - 3):
+                attend(i - 3)
+            if live(i + 1):
+                pooled_sum(i + 1)
+            invert(i, i - 2)
+            if live(i - 1):
+                exponentials(i - 1)
+            if live(i + 1):
+                for r in range(TILES - 1):
+                    score_matmul(i + 1, r)
+            if i >= 0 and i % HEADS == 0:
+                if i // HEADS + 1 < BATCH:
+                    prepare_masks(i // HEADS + 1)
+                if i // HEADS + 2 < BATCH:
+                    load_batch(i // HEADS + 2)

@@ -51,6 +51,7 @@ def tile_multiheadedselfattention_pa_t_kernel(
         const = stack.enter_context(tc.tile_pool(name="const", bufs=1))
         two = stack.enter_context(tc.tile_pool(name="two", bufs=2))
         three = stack.enter_context(tc.tile_pool(name="three", bufs=3))
+        four = stack.enter_context(tc.tile_pool(name="four", bufs=4))
         five = stack.enter_context(tc.tile_pool(name="five", bufs=5))
         psum_scores = stack.enter_context(tc.psum_pool(name="psum_scores", bufs=3))
         psum_turn = stack.enter_context(tc.psum_pool(name="psum_turn", bufs=2))
@@ -65,15 +66,15 @@ def tile_multiheadedselfattention_pa_t_kernel(
             return slice((u % HEADS) * HEAD, (u % HEADS + 1) * HEAD)
 
         def load_batch(b):
-            q_sb = three.tile([P, TILES, D_MODEL], BF16)
-            nc.sync.dma_start(out=q_sb[:], in_=q[b].rearrange("(p r) c -> p r c", r=TILES))
-            k_sb = three.tile([P, TILES, D_MODEL], BF16)
-            nc.sync.dma_start(out=k_sb[:], in_=k[b].rearrange("(p r) c -> p r c", r=TILES))
             feat_sb = two.tile([P, TILES, D_FEAT], BF16)
             nc.sync.dma_start(
                 out=feat_sb[:], in_=pre_value_key[b].rearrange("(p r) c -> p r c", r=TILES)
             )
-            stream_sb = three.tile([P, TILES, D_OUT], BF16)
+            q_sb = three.tile([P, TILES, D_MODEL], BF16)
+            nc.sync.dma_start(out=q_sb[:], in_=q[b].rearrange("(p r) c -> p r c", r=TILES))
+            k_sb = three.tile([P, TILES, D_MODEL], BF16)
+            nc.sync.dma_start(out=k_sb[:], in_=k[b].rearrange("(p r) c -> p r c", r=TILES))
+            stream_sb = four.tile([P, TILES, D_OUT], BF16)
             nc.sync.dma_start(
                 out=stream_sb[:], in_=pre_query[b].rearrange("(p r) c -> p r c", r=TILES)
             )
@@ -94,11 +95,6 @@ def tile_multiheadedselfattention_pa_t_kernel(
         nc.scalar.dma_start(
             out=mask_cols[:], in_=value_key_masks.rearrange("b (p a) -> p b a", a=TILES)
         )
-        mask_rows = const.tile([P, BATCH, SEQ], BF16)
-        nc.scalar.dma_start(
-            out=mask_rows[:].rearrange("p b s -> p (b s)"),
-            in_=value_key_masks.rearrange("b s -> (b s)").partition_broadcast(P),
-        )
         bv_rows = const.tile([P, D_MODEL], BF16)
         nc.scalar.dma_start(out=bv_rows[:], in_=bv.partition_broadcast(P))
         counts = const.tile([P, BATCH], BF16)
@@ -111,6 +107,12 @@ def tile_multiheadedselfattention_pa_t_kernel(
         nc.scalar.dma_start(
             out=gate_bias[:],
             in_=overall_bias.rearrange("a h c d -> (a h c d)").partition_broadcast(P),
+        )
+
+        mask_rows = const.tile([P, BATCH, SEQ], BF16)
+        nc.scalar.dma_start(
+            out=mask_rows[:].rearrange("p b s -> p (b s)"),
+            in_=value_key_masks.rearrange("b s -> (b s)").partition_broadcast(P),
         )
 
         ident_bf = const.tile([P, P], BF16)
@@ -140,20 +142,6 @@ def tile_multiheadedselfattention_pa_t_kernel(
 
         prepare_masks(0)
 
-        inv_count = const.tile([P, BATCH], F32)
-        nc.vector.reciprocal(out=inv_count[:], in_=counts[:])
-        neg_gain = const.tile([P, HEADS], F32)
-        nc.vector.tensor_scalar_mul(out=neg_gain[:], in0=gain[:], scalar1=-INV_SQRT_HEAD)
-        neg_gate_bias = const.tile([P, HEADS], F32)
-        nc.vector.tensor_scalar_mul(out=neg_gate_bias[:], in0=gate_bias[:], scalar1=-1.0)
-        neg_gain_over_count = const.tile([P, BATCH, HEADS], F32)
-        nc.vector.tensor_tensor(
-            out=neg_gain_over_count[:],
-            in0=neg_gain[:].unsqueeze(1).to_broadcast([P, BATCH, HEADS]),
-            in1=inv_count[:].unsqueeze(2).to_broadcast([P, BATCH, HEADS]),
-            op=ALU.mult,
-        )
-
         w_grouped = const.tile([P, PASSES, D_MODEL * PACK], BF16, align_bytes=64)
         w_codes = const.tile([P, PASSES, D_MODEL], U32, align_bytes=64)
         w_scales = const.tile([P, PASSES, D_MODEL], U8, align_bytes=64)
@@ -168,6 +156,20 @@ def tile_multiheadedselfattention_pa_t_kernel(
                 scales=w_scales[:, g, :],
                 in_=w_grouped[:, g, :],
             )
+
+        inv_count = const.tile([P, BATCH], F32)
+        nc.vector.reciprocal(out=inv_count[:], in_=counts[:])
+        neg_gain = const.tile([P, HEADS], F32)
+        nc.vector.tensor_scalar_mul(out=neg_gain[:], in0=gain[:], scalar1=-INV_SQRT_HEAD)
+        neg_gate_bias = const.tile([P, HEADS], F32)
+        nc.vector.tensor_scalar_mul(out=neg_gate_bias[:], in0=gate_bias[:], scalar1=-1.0)
+        neg_gain_over_count = const.tile([P, BATCH, HEADS], F32)
+        nc.vector.tensor_tensor(
+            out=neg_gain_over_count[:],
+            in0=neg_gain[:].unsqueeze(1).to_broadcast([P, BATCH, HEADS]),
+            in1=inv_count[:].unsqueeze(2).to_broadcast([P, BATCH, HEADS]),
+            op=ALU.mult,
+        )
 
         def turn_features(piece):
             b, a = piece // TILES, piece % TILES
@@ -293,6 +295,10 @@ def tile_multiheadedselfattention_pa_t_kernel(
                     scalar2=0.0,
                     op0=ALU.mult,
                     op1=ALU.add,
+                )
+                nc.sync.dma_start(
+                    out=out[b].rearrange("(p r) c -> p r c", r=TILES)[:, :, D_MODEL:D_OUT],
+                    in_=result[:, :, D_MODEL:D_OUT],
                 )
                 kept[("result", b)] = result
             one_minus_gate = three.tile([P, TILES], F32)
@@ -453,7 +459,7 @@ def tile_multiheadedselfattention_pa_t_kernel(
             kept[("gate_over_sum", u)] = gate_over_sum
 
         def blend(u):
-            b, n = u // HEADS, u % HEADS
+            b = u // HEADS
             h_gated = two.tile([P, TILES, HEAD], F32)
             for r in range(TILES):
                 nc.scalar.activation(
@@ -469,10 +475,10 @@ def tile_multiheadedselfattention_pa_t_kernel(
                 in1=h_gated[:],
                 op=ALU.add,
             )
-            if n == HEADS - 1:
-                nc.gpsimd.dma_start(
-                    out=out[b].rearrange("(p r) c -> p r c", r=TILES), in_=result[:]
-                )
+            nc.sync.dma_start(
+                out=out[b].rearrange("(p r) c -> p r c", r=TILES)[:, :, head_columns(u)],
+                in_=result[:, :, head_columns(u)],
+            )
 
         for i in range(-3, UNITS + 5):
             if live(i - 4):
@@ -480,8 +486,8 @@ def tile_multiheadedselfattention_pa_t_kernel(
             if live(i - 3):
                 quantise_e_and_v(i - 3)
                 gate_over_row_sum(i - 3)
-            if live(i - 1):
-                start_result(i - 1)
+            if live(i - 2):
+                start_result(i - 2)
             if live(i - 2):
                 turn_e(i - 2)
             if live(i + 2):
@@ -509,7 +515,7 @@ def tile_multiheadedselfattention_pa_t_kernel(
                 attend(i - 3)
             if live(i + 1):
                 pooled_sum(i + 1)
-            invert(i, i - 2)
+            invert(i - 1, i - 2)
             if live(i - 1):
                 exponentials(i - 1)
             if live(i + 1):

@@ -27,6 +27,7 @@ D_OUT = 640
 UNITS = BATCH * HEADS
 INV_SQRT_HEAD = 1.0 / math.sqrt(HEAD)
 MASKED = -1.0e30
+TENSOR_MASKS = 2
 
 FLOPS = 2 * BATCH * SEQ * D_FEAT * D_MODEL + 2 * 2 * BATCH * HEADS * SEQ * SEQ * HEAD
 
@@ -128,17 +129,17 @@ def tile_multiheadedselfattention_pa_t_kernel(
                 in1=mask_cols[:, b, :].unsqueeze(2).to_broadcast([P, TILES, P]),
                 op=ALU.mult,
             )
-            mask_bias = two.tile([P, TILES, P], BF16)
+            neg_mask_rows = two.tile([P, TILES, P], BF16)
             nc.gpsimd.tensor_scalar(
-                out=mask_bias[:],
+                out=neg_mask_rows[:],
                 in0=mask_rows[:, b, :].rearrange("p (x a) -> p a x", a=TILES),
                 scalar1=0.0,
-                scalar2=MASKED,
+                scalar2=-MASKED,
                 op0=ALU.is_equal,
                 op1=ALU.mult,
             )
             kept[("kept_keys", b)] = kept_keys
-            kept[("mask_bias", b)] = mask_bias
+            kept[("neg_mask_rows", b)] = neg_mask_rows
 
         prepare_masks(0)
 
@@ -156,6 +157,16 @@ def tile_multiheadedselfattention_pa_t_kernel(
                 scales=w_scales[:, g, :],
                 in_=w_grouped[:, g, :],
             )
+
+        mask_bias_cols = const.tile([P, BATCH, TILES], F32)
+        nc.vector.tensor_scalar(
+            out=mask_bias_cols[:],
+            in0=mask_cols[:],
+            scalar1=0.0,
+            scalar2=MASKED,
+            op0=ALU.is_equal,
+            op1=ALU.mult,
+        )
 
         inv_count = const.tile([P, BATCH], F32)
         nc.vector.reciprocal(out=inv_count[:], in_=counts[:])
@@ -318,38 +329,58 @@ def tile_multiheadedselfattention_pa_t_kernel(
             )
 
         def score_matmul(u, r):
-            scores_ps = psum_scores.tile([P, SEQ], F32, tag="scores")
+            scores_ps = psum_scores.tile([P, TILES, P], F32, tag="scores")
             nc.tensor.matmul(
-                out=scores_ps[:],
+                out=scores_ps[:].rearrange("p a x -> p (a x)"),
                 lhsT=kept[("q_turned", u)][:, r, :],
                 rhs=kept[("k_turned", u)][:].rearrange("c a x -> c (a x)"),
                 start=True,
-                stop=True,
+                stop=(r >= TENSOR_MASKS),
             )
+            if r < TENSOR_MASKS:
+                for a in range(TILES):
+                    nc.tensor.matmul(
+                        out=scores_ps[:, a, :],
+                        lhsT=mask_bias_cols[:, u // HEADS, a : a + 1].to_broadcast([P, P]),
+                        rhs=ident_f[:],
+                        is_transpose=True,
+                        start=False,
+                        stop=(a == TILES - 1),
+                    )
             kept[("scores_ps", u, r)] = scores_ps
 
-        def add_mask(u, r):
+        def negate_scores(u, r):
             if r == 0:
-                masked_scores = three.tile([P, TILES, SEQ], F32)
+                neg_scores = three.tile([P, TILES, SEQ], F32)
                 neg_max = three.tile([P, TILES], F32)
-                kept[("masked_scores", u)] = masked_scores
+                kept[("neg_scores", u)] = neg_scores
                 kept[("neg_max", u)] = neg_max
-            nc.vector.scalar_tensor_tensor(
-                out=kept[("masked_scores", u)][:, r, :],
-                in0=kept[("scores_ps", u, r)][:],
-                scalar=INV_SQRT_HEAD,
-                in1=kept[("mask_bias", u // HEADS)][:].rearrange("p a x -> p (a x)"),
-                op0=ALU.mult,
-                op1=ALU.add,
-            )
+            if r < TENSOR_MASKS:
+                nc.vector.tensor_scalar(
+                    out=kept[("neg_scores", u)][:, r, :],
+                    in0=kept[("scores_ps", u, r)][:].rearrange("p a x -> p (a x)"),
+                    scalar1=-INV_SQRT_HEAD,
+                    scalar2=None,
+                    op0=ALU.mult,
+                    op1=ALU.min,
+                    accum_out=kept[("neg_max", u)][:, r : r + 1],
+                )
+            else:
+                nc.vector.scalar_tensor_tensor(
+                    out=kept[("neg_scores", u)][:, r, :],
+                    in0=kept[("scores_ps", u, r)][:].rearrange("p a x -> p (a x)"),
+                    scalar=-INV_SQRT_HEAD,
+                    in1=kept[("neg_mask_rows", u // HEADS)][:].rearrange("p a x -> p (a x)"),
+                    op0=ALU.mult,
+                    op1=ALU.add,
+                )
 
-        def row_max(u, r):
+        def row_minima(u):
             nc.vector.tensor_reduce(
-                out=kept[("neg_max", u)][:, r : r + 1],
-                in_=kept[("masked_scores", u)][:, r, :],
+                out=kept[("neg_max", u)][:, TENSOR_MASKS:TILES],
+                in_=kept[("neg_scores", u)][:, TENSOR_MASKS:TILES, :],
                 axis=AXIS.X,
-                op=ALU.max,
-                negate=True,
+                op=ALU.min,
             )
 
         def exponentials(u):
@@ -358,12 +389,12 @@ def tile_multiheadedselfattention_pa_t_kernel(
             for r in range(TILES):
                 nc.scalar.activation(
                     out=e_sb[:, r, :].rearrange("p (u w e) -> p u w e", u=2, e=2),
-                    in_=kept[("masked_scores", u)][:, r, :].rearrange(
+                    in_=kept[("neg_scores", u)][:, r, :].rearrange(
                         "p (u e w) -> p u w e", u=2, e=2
                     ),
                     func=ACT.Exp,
                     bias=kept[("neg_max", u)][:, r : r + 1],
-                    scale=1.0,
+                    scale=-1.0,
                     accum_out=row_sum[:, r : r + 1],
                 )
             kept[("e_sb", u)] = e_sb
@@ -384,7 +415,8 @@ def tile_multiheadedselfattention_pa_t_kernel(
                             in_=e_words[:, 2 * half + rr, u2 * P : (u2 + 1) * P],
                             identity=ident_f[:],
                         )
-                nc.scalar.copy(
+                copy_out = nc.vector.tensor_copy if half == 0 else nc.scalar.copy
+                copy_out(
                     out=e_grouped_words[:, 2 * half : 2 * half + 2],
                     in_=turn_half[:].rearrange("w r u i -> w r i u"),
                 )
@@ -496,15 +528,13 @@ def tile_multiheadedselfattention_pa_t_kernel(
                 turn_features(i + 3)
             if live(i):
                 for r in range(TILES):
-                    add_mask(i, r)
+                    negate_scores(i, r)
                     if r == 0:
                         score_matmul(i, TILES - 1)
-                    else:
-                        row_max(i, r - 1)
             if live(i + 2):
                 quantise_features(i + 2)
             if live(i):
-                row_max(i, TILES - 1)
+                row_minima(i)
                 gate_denominator(i)
             if live(i + 1):
                 pooled_matmuls(i + 1)

@@ -133,9 +133,9 @@ def tile_multiheadedselfattention_pa_t_kernel(
             nc.gpsimd.tensor_scalar(
                 out=neg_mask_rows[:],
                 in0=mask_rows[:, b, :].rearrange("p (x a) -> p a x", a=TILES),
-                scalar1=0.0,
-                scalar2=-MASKED,
-                op0=ALU.is_equal,
+                scalar1=-1.0,
+                scalar2=MASKED,
+                op0=ALU.add,
                 op1=ALU.mult,
             )
             kept[("kept_keys", b)] = kept_keys
@@ -170,14 +170,14 @@ def tile_multiheadedselfattention_pa_t_kernel(
 
         inv_count = const.tile([P, BATCH], F32)
         nc.vector.reciprocal(out=inv_count[:], in_=counts[:])
-        neg_gain = const.tile([P, HEADS], F32)
-        nc.vector.tensor_scalar_mul(out=neg_gain[:], in0=gain[:], scalar1=-INV_SQRT_HEAD)
-        neg_gate_bias = const.tile([P, HEADS], F32)
-        nc.vector.tensor_scalar_mul(out=neg_gate_bias[:], in0=gate_bias[:], scalar1=-1.0)
-        neg_gain_over_count = const.tile([P, BATCH, HEADS], F32)
+        half_gain = const.tile([P, HEADS], F32)
+        nc.vector.tensor_scalar_mul(out=half_gain[:], in0=gain[:], scalar1=0.5 * INV_SQRT_HEAD)
+        half_gate_bias = const.tile([P, HEADS], F32)
+        nc.vector.tensor_scalar_mul(out=half_gate_bias[:], in0=gate_bias[:], scalar1=0.5)
+        half_gain_over_count = const.tile([P, BATCH, HEADS], F32)
         nc.vector.tensor_tensor(
-            out=neg_gain_over_count[:],
-            in0=neg_gain[:].unsqueeze(1).to_broadcast([P, BATCH, HEADS]),
+            out=half_gain_over_count[:],
+            in0=half_gain[:].unsqueeze(1).to_broadcast([P, BATCH, HEADS]),
             in1=inv_count[:].unsqueeze(2).to_broadcast([P, BATCH, HEADS]),
             op=ALU.mult,
         )
@@ -271,28 +271,43 @@ def tile_multiheadedselfattention_pa_t_kernel(
             )
             kept[("pooled", u)] = pooled
 
-        def gate_denominator(u):
+        def one_minus_gate_of(u):
             b, n = u // HEADS, u % HEADS
-            denominator = three.tile([P, TILES], F32)
+            tanh_half_z = three.tile([P, TILES], F32)
             nc.scalar.activation(
-                out=denominator[:],
+                out=tanh_half_z[:],
                 in_=kept[("pooled", u)][:],
-                func=ACT.Exp,
-                scale=neg_gain_over_count[:, b, n : n + 1],
-                bias=neg_gate_bias[:, n : n + 1],
+                func=ACT.Tanh,
+                scale=half_gain_over_count[:, b, n : n + 1],
+                bias=half_gate_bias[:, n : n + 1],
             )
-            nc.gpsimd.tensor_scalar_add(out=denominator[:], in0=denominator[:], scalar1=1.0)
-            kept[("denominator", u)] = denominator
+            one_minus_gate = five.tile([P, TILES], F32)
+            nc.gpsimd.tensor_scalar(
+                out=one_minus_gate[:],
+                in0=tanh_half_z[:],
+                scalar1=-0.5,
+                scalar2=0.5,
+                op0=ALU.mult,
+                op1=ALU.add,
+            )
+            kept[("one_minus_gate", u)] = one_minus_gate
 
-        def invert(u_gate, u_sum):
-            if live(u_gate):
-                gate = five.tile([P, TILES], F32)
-                nc.vector.reciprocal(out=gate[:], in_=kept[("denominator", u_gate)][:])
-                kept[("gate", u_gate)] = gate
-            if live(u_sum):
-                inv_sum = three.tile([P, TILES], F32)
-                nc.vector.reciprocal(out=inv_sum[:], in_=kept[("row_sum", u_sum)][:])
-                kept[("inv_sum", u_sum)] = inv_sum
+        def invert_row_sum(u):
+            inv_sum = three.tile([P, TILES], F32)
+            nc.vector.reciprocal(out=inv_sum[:], in_=kept[("row_sum", u)][:])
+            kept[("inv_sum", u)] = inv_sum
+
+        def minus_gate_over_row_sum(u):
+            minus_gate_over_sum = three.tile([P, TILES], F32)
+            nc.vector.scalar_tensor_tensor(
+                out=minus_gate_over_sum[:],
+                in0=kept[("one_minus_gate", u)][:],
+                scalar=1.0,
+                in1=kept[("inv_sum", u)][:],
+                op0=ALU.subtract,
+                op1=ALU.mult,
+            )
+            kept[("minus_gate_over_sum", u)] = minus_gate_over_sum
 
         def start_result(u):
             b, n = u // HEADS, u % HEADS
@@ -312,19 +327,10 @@ def tile_multiheadedselfattention_pa_t_kernel(
                     in_=result[:, :, D_MODEL:D_OUT],
                 )
                 kept[("result", b)] = result
-            one_minus_gate = three.tile([P, TILES], F32)
-            nc.gpsimd.tensor_scalar(
-                out=one_minus_gate[:],
-                in0=kept[("gate", u)][:],
-                scalar1=-1.0,
-                scalar2=1.0,
-                op0=ALU.mult,
-                op1=ALU.add,
-            )
             nc.gpsimd.tensor_tensor(
                 out=kept[("result", b)][:, :, head_columns(u)],
                 in0=stream_sb[:, :, head_columns(u)],
-                in1=one_minus_gate[:].unsqueeze(2).to_broadcast([P, TILES, HEAD]),
+                in1=kept[("one_minus_gate", u)][:].unsqueeze(2).to_broadcast([P, TILES, HEAD]),
                 op=ALU.mult,
             )
 
@@ -415,7 +421,7 @@ def tile_multiheadedselfattention_pa_t_kernel(
                             in_=e_words[:, 2 * half + rr, u2 * P : (u2 + 1) * P],
                             identity=ident_f[:],
                         )
-                copy_out = nc.vector.tensor_copy if half == 0 else nc.scalar.copy
+                copy_out = nc.scalar.copy if half == 0 else nc.vector.tensor_copy
                 copy_out(
                     out=e_grouped_words[:, 2 * half : 2 * half + 2],
                     in_=turn_half[:].rearrange("w r u i -> w r i u"),
@@ -480,32 +486,22 @@ def tile_multiheadedselfattention_pa_t_kernel(
                 )
             kept[("h_ps", u)] = h_ps
 
-        def gate_over_row_sum(u):
-            gate_over_sum = three.tile([P, TILES], F32)
-            nc.gpsimd.tensor_tensor(
-                out=gate_over_sum[:],
-                in0=kept[("inv_sum", u)][:],
-                in1=kept[("gate", u)][:],
-                op=ALU.mult,
-            )
-            kept[("gate_over_sum", u)] = gate_over_sum
-
         def blend(u):
             b = u // HEADS
-            h_gated = two.tile([P, TILES, HEAD], F32)
+            minus_h_gated = two.tile([P, TILES, HEAD], F32)
             for r in range(TILES):
                 nc.scalar.activation(
-                    out=h_gated[:, r, :],
+                    out=minus_h_gated[:, r, :],
                     in_=kept[("h_ps", u)][:, r, :],
                     func=ACT.Copy,
-                    scale=kept[("gate_over_sum", u)][:, r : r + 1],
+                    scale=kept[("minus_gate_over_sum", u)][:, r : r + 1],
                 )
             result = kept[("result", b)]
             nc.gpsimd.tensor_tensor(
                 out=result[:, :, head_columns(u)],
                 in0=result[:, :, head_columns(u)],
-                in1=h_gated[:],
-                op=ALU.add,
+                in1=minus_h_gated[:],
+                op=ALU.subtract,
             )
             nc.sync.dma_start(
                 out=out[b].rearrange("(p r) c -> p r c", r=TILES)[:, :, head_columns(u)],
@@ -513,15 +509,17 @@ def tile_multiheadedselfattention_pa_t_kernel(
             )
 
         for i in range(-3, UNITS + 5):
-            if live(i - 4):
-                blend(i - 4)
             if live(i - 3):
                 quantise_e_and_v(i - 3)
-                gate_over_row_sum(i - 3)
-            if live(i - 2):
-                start_result(i - 2)
+                minus_gate_over_row_sum(i - 3)
             if live(i - 2):
                 turn_e(i - 2)
+            if live(i + 1):
+                pooled_matmuls(i + 1)
+            if live(i - 4):
+                blend(i - 4)
+            if live(i - 2):
+                start_result(i - 2)
             if live(i + 2):
                 turn_q_and_k(i + 2)
             if live(i + 3):
@@ -535,9 +533,7 @@ def tile_multiheadedselfattention_pa_t_kernel(
                 quantise_features(i + 2)
             if live(i):
                 row_minima(i)
-                gate_denominator(i)
-            if live(i + 1):
-                pooled_matmuls(i + 1)
+                one_minus_gate_of(i)
             if live(i - 2):
                 project_values(i - 2)
                 add_value_bias(i - 2)
@@ -545,7 +541,8 @@ def tile_multiheadedselfattention_pa_t_kernel(
                 attend(i - 3)
             if live(i + 1):
                 pooled_sum(i + 1)
-            invert(i - 1, i - 2)
+            if live(i - 2):
+                invert_row_sum(i - 2)
             if live(i - 1):
                 exponentials(i - 1)
             if live(i + 1):

@@ -27,7 +27,6 @@ D_OUT = 640
 UNITS = BATCH * HEADS
 INV_SQRT_HEAD = 1.0 / math.sqrt(HEAD)
 MASKED = -1.0e30
-TENSOR_MASKS = 2
 
 FLOPS = 2 * BATCH * SEQ * D_FEAT * D_MODEL + 2 * 2 * BATCH * HEADS * SEQ * SEQ * HEAD
 
@@ -67,14 +66,16 @@ def tile_multiheadedselfattention_pa_t_kernel(
             return slice((u % HEADS) * HEAD, (u % HEADS + 1) * HEAD)
 
         def load_batch(b):
-            feat_sb = two.tile([P, TILES, D_FEAT], BF16)
-            nc.sync.dma_start(
-                out=feat_sb[:], in_=pre_value_key[b].rearrange("(p r) c -> p r c", r=TILES)
-            )
             q_sb = three.tile([P, TILES, D_MODEL], BF16)
             nc.sync.dma_start(out=q_sb[:], in_=q[b].rearrange("(p r) c -> p r c", r=TILES))
             k_sb = three.tile([P, TILES, D_MODEL], BF16)
             nc.sync.dma_start(out=k_sb[:], in_=k[b].rearrange("(p r) c -> p r c", r=TILES))
+            feat_sb = two.tile([P, TILES, D_FEAT], BF16)
+            nc.sync.dma_start(
+                out=feat_sb[:], in_=pre_value_key[b].rearrange("(p r) c -> p r c", r=TILES)
+            )
+            if b == 0:
+                load_weights()
             stream_sb = four.tile([P, TILES, D_OUT], BF16)
             nc.sync.dma_start(
                 out=stream_sb[:], in_=pre_query[b].rearrange("(p r) c -> p r c", r=TILES)
@@ -85,10 +86,13 @@ def tile_multiheadedselfattention_pa_t_kernel(
             kept[("stream", b)] = stream_sb
 
         w_raw = const.tile([P, PASSES, PACK, D_MODEL], BF16)
-        nc.sync.dma_start(
-            out=w_raw[:].rearrange("w g (u e) d -> w (g u) (e d)", u=2, e=2),
-            in_=Wv.rearrange("(g u w e) d -> w (g u) (e d)", g=PASSES, u=2, e=2),
-        )
+
+        def load_weights():
+            nc.sync.dma_start(
+                out=w_raw[:].rearrange("w g (u e) d -> w (g u) (e d)", u=2, e=2),
+                in_=Wv.rearrange("(g u w e) d -> w (g u) (e d)", g=PASSES, u=2, e=2),
+            )
+
         load_batch(0)
         load_batch(1)
 
@@ -110,12 +114,6 @@ def tile_multiheadedselfattention_pa_t_kernel(
             in_=overall_bias.rearrange("a h c d -> (a h c d)").partition_broadcast(P),
         )
 
-        mask_rows = const.tile([P, BATCH, SEQ], BF16)
-        nc.scalar.dma_start(
-            out=mask_rows[:].rearrange("p b s -> p (b s)"),
-            in_=value_key_masks.rearrange("b s -> (b s)").partition_broadcast(P),
-        )
-
         ident_bf = const.tile([P, P], BF16)
         make_identity(nc, ident_bf[:])
         ident_f = const.tile([P, P], F32)
@@ -129,44 +127,36 @@ def tile_multiheadedselfattention_pa_t_kernel(
                 in1=mask_cols[:, b, :].unsqueeze(2).to_broadcast([P, TILES, P]),
                 op=ALU.mult,
             )
-            neg_mask_rows = two.tile([P, TILES, P], BF16)
+            mask_bias = two.tile([P, TILES, P], F32)
             nc.gpsimd.tensor_scalar(
-                out=neg_mask_rows[:],
-                in0=mask_rows[:, b, :].rearrange("p (x a) -> p a x", a=TILES),
+                out=mask_bias[:],
+                in0=mask_cols[:, b, :].unsqueeze(2).to_broadcast([P, TILES, P]),
                 scalar1=-1.0,
-                scalar2=MASKED,
+                scalar2=-MASKED,
                 op0=ALU.add,
                 op1=ALU.mult,
             )
             kept[("kept_keys", b)] = kept_keys
-            kept[("neg_mask_rows", b)] = neg_mask_rows
+            kept[("mask_bias", b)] = mask_bias
 
         prepare_masks(0)
 
         w_grouped = const.tile([P, PASSES, D_MODEL * PACK], BF16, align_bytes=64)
         w_codes = const.tile([P, PASSES, D_MODEL], U32, align_bytes=64)
         w_scales = const.tile([P, PASSES, D_MODEL], U8, align_bytes=64)
-        for g in range(PASSES):
+
+        def group_weights(g):
             nc.vector.tensor_copy(
                 out=w_grouped[:, g, :].rearrange("w (d t) -> w d t", t=PACK),
                 in_=w_raw[:, g, :, :].rearrange("w t d -> w d t"),
             )
-        for g in range(PASSES):
+
+        def quantise_weights(g):
             nc.vector.quantize_mx(
                 out=w_codes[:, g, :].bitcast(FP8X4),
                 scales=w_scales[:, g, :],
                 in_=w_grouped[:, g, :],
             )
-
-        mask_bias_cols = const.tile([P, BATCH, TILES], F32)
-        nc.vector.tensor_scalar(
-            out=mask_bias_cols[:],
-            in0=mask_cols[:],
-            scalar1=0.0,
-            scalar2=MASKED,
-            op0=ALU.is_equal,
-            op1=ALU.mult,
-        )
 
         inv_count = const.tile([P, BATCH], F32)
         nc.vector.reciprocal(out=inv_count[:], in_=counts[:])
@@ -194,7 +184,7 @@ def tile_multiheadedselfattention_pa_t_kernel(
                         in_=feat_words[:, a, first : first + P],
                         identity=ident_f[:],
                     )
-            feat_grouped = two.tile([P, PASSES * P * PACK], BF16, align_bytes=64)
+            feat_grouped = three.tile([P, PASSES * P * PACK], BF16, align_bytes=64)
             nc.scalar.copy(
                 out=feat_grouped[:].bitcast(F32).rearrange("w (g x u) -> w g x u", g=PASSES, u=2),
                 in_=turn_f[:].rearrange("w g u x -> w g x u"),
@@ -341,18 +331,17 @@ def tile_multiheadedselfattention_pa_t_kernel(
                 lhsT=kept[("q_turned", u)][:, r, :],
                 rhs=kept[("k_turned", u)][:].rearrange("c a x -> c (a x)"),
                 start=True,
-                stop=(r >= TENSOR_MASKS),
+                stop=False,
             )
-            if r < TENSOR_MASKS:
-                for a in range(TILES):
-                    nc.tensor.matmul(
-                        out=scores_ps[:, a, :],
-                        lhsT=mask_bias_cols[:, u // HEADS, a : a + 1].to_broadcast([P, P]),
-                        rhs=ident_f[:],
-                        is_transpose=True,
-                        start=False,
-                        stop=(a == TILES - 1),
-                    )
+            for a in range(TILES):
+                nc.tensor.matmul(
+                    out=scores_ps[:, a, :],
+                    lhsT=kept[("mask_bias", u // HEADS)][:, a, :],
+                    rhs=ident_f[:],
+                    is_transpose=True,
+                    start=False,
+                    stop=(a == TILES - 1),
+                )
             kept[("scores_ps", u, r)] = scores_ps
 
         def negate_scores(u, r):
@@ -361,32 +350,14 @@ def tile_multiheadedselfattention_pa_t_kernel(
                 neg_max = three.tile([P, TILES], F32)
                 kept[("neg_scores", u)] = neg_scores
                 kept[("neg_max", u)] = neg_max
-            if r < TENSOR_MASKS:
-                nc.vector.tensor_scalar(
-                    out=kept[("neg_scores", u)][:, r, :],
-                    in0=kept[("scores_ps", u, r)][:].rearrange("p a x -> p (a x)"),
-                    scalar1=-INV_SQRT_HEAD,
-                    scalar2=None,
-                    op0=ALU.mult,
-                    op1=ALU.min,
-                    accum_out=kept[("neg_max", u)][:, r : r + 1],
-                )
-            else:
-                nc.vector.scalar_tensor_tensor(
-                    out=kept[("neg_scores", u)][:, r, :],
-                    in0=kept[("scores_ps", u, r)][:].rearrange("p a x -> p (a x)"),
-                    scalar=-INV_SQRT_HEAD,
-                    in1=kept[("neg_mask_rows", u // HEADS)][:].rearrange("p a x -> p (a x)"),
-                    op0=ALU.mult,
-                    op1=ALU.add,
-                )
-
-        def row_minima(u):
-            nc.vector.tensor_reduce(
-                out=kept[("neg_max", u)][:, TENSOR_MASKS:TILES],
-                in_=kept[("neg_scores", u)][:, TENSOR_MASKS:TILES, :],
-                axis=AXIS.X,
-                op=ALU.min,
+            nc.vector.tensor_scalar(
+                out=kept[("neg_scores", u)][:, r, :],
+                in0=kept[("scores_ps", u, r)][:].rearrange("p a x -> p (a x)"),
+                scalar1=-INV_SQRT_HEAD,
+                scalar2=None,
+                op0=ALU.mult,
+                op1=ALU.min,
+                accum_out=kept[("neg_max", u)][:, r : r + 1],
             )
 
         def exponentials(u):
@@ -508,10 +479,20 @@ def tile_multiheadedselfattention_pa_t_kernel(
                 in_=result[:, :, head_columns(u)],
             )
 
-        for i in range(-3, UNITS + 5):
+        turn_q_and_k(0)
+        for r in range(TILES - 1):
+            score_matmul(0, r)
+        pooled_matmuls(0)
+        turn_q_and_k(1)
+        turn_features(0)
+        turn_features(1)
+        pooled_sum(0)
+        for i in range(UNITS + 5):
             if live(i - 3):
                 quantise_e_and_v(i - 3)
                 minus_gate_over_row_sum(i - 3)
+            if i > 0 and live(i + 1):
+                quantise_features(i + 1)
             if live(i - 2):
                 turn_e(i - 2)
             if live(i + 1):
@@ -522,18 +503,22 @@ def tile_multiheadedselfattention_pa_t_kernel(
                 start_result(i - 2)
             if live(i + 2):
                 turn_q_and_k(i + 2)
-            if live(i + 3):
-                turn_features(i + 3)
+                turn_features(i + 2)
             if live(i):
                 for r in range(TILES):
                     negate_scores(i, r)
                     if r == 0:
                         score_matmul(i, TILES - 1)
-            if live(i + 2):
-                quantise_features(i + 2)
-            if live(i):
-                row_minima(i)
                 one_minus_gate_of(i)
+            if i == 0:
+                quantise_features(0)
+                quantise_features(1)
+            if i < PASSES:
+                group_weights(i)
+                if i > 0:
+                    quantise_weights(i - 1)
+            if i == PASSES:
+                quantise_weights(PASSES - 1)
             if live(i - 2):
                 project_values(i - 2)
                 add_value_bias(i - 2)
@@ -548,8 +533,7 @@ def tile_multiheadedselfattention_pa_t_kernel(
             if live(i + 1):
                 for r in range(TILES - 1):
                     score_matmul(i + 1, r)
-            if i >= 0 and i % HEADS == 0:
-                if i // HEADS + 1 < BATCH:
-                    prepare_masks(i // HEADS + 1)
-                if i // HEADS + 2 < BATCH:
-                    load_batch(i // HEADS + 2)
+            if i % HEADS == 0 and i // HEADS + 1 < BATCH:
+                prepare_masks(i // HEADS + 1)
+            if i % HEADS == 1 and i // HEADS + 2 < BATCH:
+                load_batch(i // HEADS + 2)

@@ -27,6 +27,8 @@ D_OUT = 640
 UNITS = BATCH * HEADS
 INV_SQRT_HEAD = 1.0 / math.sqrt(HEAD)
 MASKED = -1.0e30
+TENSOR_MASKS = 3
+PLAIN_TURNS = 3
 
 FLOPS = 2 * BATCH * SEQ * D_FEAT * D_MODEL + 2 * 2 * BATCH * HEADS * SEQ * SEQ * HEAD
 
@@ -65,43 +67,45 @@ def tile_multiheadedselfattention_pa_t_kernel(
         def head_columns(u):
             return slice((u % HEADS) * HEAD, (u % HEADS + 1) * HEAD)
 
-        def load_batch(b):
+        def load_mask_rows(b, queue):
+            mask_rows = two.tile([P, SEQ], BF16)
+            queue.dma_start(out=mask_rows[:], in_=value_key_masks[b].partition_broadcast(P))
+            kept[("mask_rows", b)] = mask_rows
+
+        def load_q_and_k(b):
             q_sb = three.tile([P, TILES, D_MODEL], BF16)
             nc.sync.dma_start(out=q_sb[:], in_=q[b].rearrange("(p r) c -> p r c", r=TILES))
             k_sb = three.tile([P, TILES, D_MODEL], BF16)
             nc.sync.dma_start(out=k_sb[:], in_=k[b].rearrange("(p r) c -> p r c", r=TILES))
+            kept[("q", b)] = q_sb
+            kept[("k", b)] = k_sb
+
+        def load_features(b):
             feat_sb = two.tile([P, TILES, D_FEAT], BF16)
             nc.sync.dma_start(
                 out=feat_sb[:], in_=pre_value_key[b].rearrange("(p r) c -> p r c", r=TILES)
             )
-            if b == 0:
-                load_weights()
+            kept[("feat", b)] = feat_sb
+
+        def load_stream(b):
             stream_sb = four.tile([P, TILES, D_OUT], BF16)
             nc.sync.dma_start(
                 out=stream_sb[:], in_=pre_query[b].rearrange("(p r) c -> p r c", r=TILES)
             )
-            kept[("q", b)] = q_sb
-            kept[("k", b)] = k_sb
-            kept[("feat", b)] = feat_sb
             kept[("stream", b)] = stream_sb
 
-        w_raw = const.tile([P, PASSES, PACK, D_MODEL], BF16)
-
-        def load_weights():
-            nc.sync.dma_start(
-                out=w_raw[:].rearrange("w g (u e) d -> w (g u) (e d)", u=2, e=2),
-                in_=Wv.rearrange("(g u w e) d -> w (g u) (e d)", g=PASSES, u=2, e=2),
-            )
-
-        load_batch(0)
-        load_batch(1)
+        def load_batch(b):
+            load_q_and_k(b)
+            load_features(b)
+            load_mask_rows(b, nc.sync)
+            load_stream(b)
 
         mask_cols = const.tile([P, BATCH, TILES], BF16)
         nc.scalar.dma_start(
             out=mask_cols[:], in_=value_key_masks.rearrange("b (p a) -> p b a", a=TILES)
         )
-        bv_rows = const.tile([P, D_MODEL], BF16)
-        nc.scalar.dma_start(out=bv_rows[:], in_=bv.partition_broadcast(P))
+        load_q_and_k(0)
+        load_mask_rows(0, nc.scalar)
         counts = const.tile([P, BATCH], BF16)
         nc.scalar.dma_start(out=counts[:], in_=value_key_counts.partition_broadcast(P))
         gain = const.tile([P, HEADS], BF16)
@@ -113,33 +117,63 @@ def tile_multiheadedselfattention_pa_t_kernel(
             out=gate_bias[:],
             in_=overall_bias.rearrange("a h c d -> (a h c d)").partition_broadcast(P),
         )
+        load_features(0)
+        w_raw = const.tile([P, PASSES, PACK, D_MODEL], BF16)
+        nc.sync.dma_start(
+            out=w_raw[:].rearrange("w g (u e) d -> w (g u) (e d)", u=2, e=2),
+            in_=Wv.rearrange("(g u w e) d -> w (g u) (e d)", g=PASSES, u=2, e=2),
+        )
+        bv_rows = const.tile([P, D_MODEL], BF16)
+        nc.scalar.dma_start(out=bv_rows[:], in_=bv.partition_broadcast(P))
+        load_stream(0)
 
         ident_bf = const.tile([P, P], BF16)
         make_identity(nc, ident_bf[:])
         ident_f = const.tile([P, P], F32)
         make_identity(nc, ident_f[:])
 
-        def prepare_masks(b):
-            kept_keys = two.tile([P, TILES, P], BF16)
-            nc.gpsimd.tensor_tensor(
-                out=kept_keys[:],
-                in0=ident_bf[:].unsqueeze(1).to_broadcast([P, TILES, P]),
-                in1=mask_cols[:, b, :].unsqueeze(2).to_broadcast([P, TILES, P]),
-                op=ALU.mult,
-            )
-            mask_bias = two.tile([P, TILES, P], F32)
+        def keep_keys(b, a):
+            if a == 0:
+                kept_keys = two.tile([P, TILES, P], BF16)
+                kept[("kept_keys", b)] = kept_keys
             nc.gpsimd.tensor_scalar(
-                out=mask_bias[:],
-                in0=mask_cols[:, b, :].unsqueeze(2).to_broadcast([P, TILES, P]),
+                out=kept[("kept_keys", b)][:, a, :],
+                in0=ident_bf[:],
+                scalar1=mask_cols[:, b, a : a + 1],
+                scalar2=0.0,
+                op0=ALU.mult,
+                op1=ALU.add,
+            )
+
+        def spread_mask_cols(b, a):
+            if a == 0:
+                mask_bias = two.tile([P, TILES, P], F32)
+                kept[("mask_bias", b)] = mask_bias
+            nc.gpsimd.tensor_scalar(
+                out=kept[("mask_bias", b)][:, a, :],
+                in0=mask_cols[:, b, a : a + 1].to_broadcast([P, P]),
                 scalar1=-1.0,
                 scalar2=-MASKED,
                 op0=ALU.add,
                 op1=ALU.mult,
             )
-            kept[("kept_keys", b)] = kept_keys
-            kept[("mask_bias", b)] = mask_bias
 
-        prepare_masks(0)
+        def order_mask_rows(b, a):
+            if a == 0:
+                neg_mask_rows = two.tile([P, TILES, P], BF16)
+                kept[("neg_mask_rows", b)] = neg_mask_rows
+            nc.gpsimd.tensor_scalar(
+                out=kept[("neg_mask_rows", b)][:, a, :],
+                in0=kept[("mask_rows", b)][:].rearrange("p (x a) -> p a x", a=TILES)[:, a, :],
+                scalar1=-1.0,
+                scalar2=MASKED,
+                op0=ALU.add,
+                op1=ALU.mult,
+            )
+
+        for prepare in (keep_keys, spread_mask_cols, order_mask_rows):
+            for a in range(TILES):
+                prepare(0, a)
 
         w_grouped = const.tile([P, PASSES, D_MODEL * PACK], BF16, align_bytes=64)
         w_codes = const.tile([P, PASSES, D_MODEL], U32, align_bytes=64)
@@ -184,6 +218,10 @@ def tile_multiheadedselfattention_pa_t_kernel(
                         in_=feat_words[:, a, first : first + P],
                         identity=ident_f[:],
                     )
+            kept[("turn_f", piece)] = turn_f
+
+        def copy_features(piece):
+            turn_f = kept[("turn_f", piece)]
             feat_grouped = three.tile([P, PASSES * P * PACK], BF16, align_bytes=64)
             nc.scalar.copy(
                 out=feat_grouped[:].bitcast(F32).rearrange("w (g x u) -> w g x u", g=PASSES, u=2),
@@ -214,11 +252,18 @@ def tile_multiheadedselfattention_pa_t_kernel(
                     identity=ident_bf[:],
                 )
             for a in range(TILES):
-                nc.tensor.transpose(
+                nc.tensor.matmul(
                     out=turn_qk[:, 1, a, :],
-                    in_=kept[("k", b)][:, a, head_columns(u)],
-                    identity=kept[("kept_keys", b)][:, a, :],
+                    lhsT=kept[("k", b)][:, a, head_columns(u)],
+                    rhs=kept[("kept_keys", b)][:, a, :],
+                    is_transpose=(a >= PLAIN_TURNS),
+                    start=True,
+                    stop=True,
                 )
+            kept[("turn_qk", u)] = turn_qk
+
+        def copy_q_and_k(u):
+            turn_qk = kept[("turn_qk", u)]
             q_turned = three.tile([P, TILES, P], BF16)
             nc.scalar.copy(out=q_turned[:], in_=turn_qk[:, 0, :, :])
             k_turned = three.tile([P, TILES, P], BF16)
@@ -261,7 +306,7 @@ def tile_multiheadedselfattention_pa_t_kernel(
             )
             kept[("pooled", u)] = pooled
 
-        def one_minus_gate_of(u):
+        def gate_minus_one_of(u):
             b, n = u // HEADS, u % HEADS
             tanh_half_z = three.tile([P, TILES], F32)
             nc.scalar.activation(
@@ -271,33 +316,33 @@ def tile_multiheadedselfattention_pa_t_kernel(
                 scale=half_gain_over_count[:, b, n : n + 1],
                 bias=half_gate_bias[:, n : n + 1],
             )
-            one_minus_gate = five.tile([P, TILES], F32)
+            gate_minus_one = five.tile([P, TILES], F32)
             nc.gpsimd.tensor_scalar(
-                out=one_minus_gate[:],
+                out=gate_minus_one[:],
                 in0=tanh_half_z[:],
-                scalar1=-0.5,
-                scalar2=0.5,
+                scalar1=0.5,
+                scalar2=-0.5,
                 op0=ALU.mult,
                 op1=ALU.add,
             )
-            kept[("one_minus_gate", u)] = one_minus_gate
+            kept[("gate_minus_one", u)] = gate_minus_one
 
         def invert_row_sum(u):
             inv_sum = three.tile([P, TILES], F32)
             nc.vector.reciprocal(out=inv_sum[:], in_=kept[("row_sum", u)][:])
             kept[("inv_sum", u)] = inv_sum
 
-        def minus_gate_over_row_sum(u):
-            minus_gate_over_sum = three.tile([P, TILES], F32)
+        def gate_over_row_sum(u):
+            gate_over_sum = three.tile([P, TILES], F32)
             nc.vector.scalar_tensor_tensor(
-                out=minus_gate_over_sum[:],
-                in0=kept[("one_minus_gate", u)][:],
+                out=gate_over_sum[:],
+                in0=kept[("gate_minus_one", u)][:],
                 scalar=1.0,
                 in1=kept[("inv_sum", u)][:],
-                op0=ALU.subtract,
+                op0=ALU.add,
                 op1=ALU.mult,
             )
-            kept[("minus_gate_over_sum", u)] = minus_gate_over_sum
+            kept[("gate_over_sum", u)] = gate_over_sum
 
         def start_result(u):
             b, n = u // HEADS, u % HEADS
@@ -317,12 +362,15 @@ def tile_multiheadedselfattention_pa_t_kernel(
                     in_=result[:, :, D_MODEL:D_OUT],
                 )
                 kept[("result", b)] = result
-            nc.gpsimd.tensor_tensor(
-                out=kept[("result", b)][:, :, head_columns(u)],
-                in0=stream_sb[:, :, head_columns(u)],
-                in1=kept[("one_minus_gate", u)][:].unsqueeze(2).to_broadcast([P, TILES, HEAD]),
-                op=ALU.mult,
-            )
+            for r in range(TILES):
+                nc.gpsimd.tensor_scalar(
+                    out=kept[("result", b)][:, r, head_columns(u)],
+                    in0=stream_sb[:, r, head_columns(u)],
+                    scalar1=kept[("gate_minus_one", u)][:, r : r + 1],
+                    scalar2=0.0,
+                    op0=ALU.mult,
+                    op1=ALU.add,
+                )
 
         def score_matmul(u, r):
             scores_ps = psum_scores.tile([P, TILES, P], F32, tag="scores")
@@ -331,17 +379,18 @@ def tile_multiheadedselfattention_pa_t_kernel(
                 lhsT=kept[("q_turned", u)][:, r, :],
                 rhs=kept[("k_turned", u)][:].rearrange("c a x -> c (a x)"),
                 start=True,
-                stop=False,
+                stop=(r >= TENSOR_MASKS),
             )
-            for a in range(TILES):
-                nc.tensor.matmul(
-                    out=scores_ps[:, a, :],
-                    lhsT=kept[("mask_bias", u // HEADS)][:, a, :],
-                    rhs=ident_f[:],
-                    is_transpose=True,
-                    start=False,
-                    stop=(a == TILES - 1),
-                )
+            if r < TENSOR_MASKS:
+                for a in range(TILES):
+                    nc.tensor.matmul(
+                        out=scores_ps[:, a, :],
+                        lhsT=kept[("mask_bias", u // HEADS)][:, a, :],
+                        rhs=ident_f[:],
+                        is_transpose=True,
+                        start=False,
+                        stop=(a == TILES - 1),
+                    )
             kept[("scores_ps", u, r)] = scores_ps
 
         def negate_scores(u, r):
@@ -350,71 +399,87 @@ def tile_multiheadedselfattention_pa_t_kernel(
                 neg_max = three.tile([P, TILES], F32)
                 kept[("neg_scores", u)] = neg_scores
                 kept[("neg_max", u)] = neg_max
-            nc.vector.tensor_scalar(
-                out=kept[("neg_scores", u)][:, r, :],
-                in0=kept[("scores_ps", u, r)][:].rearrange("p a x -> p (a x)"),
-                scalar1=-INV_SQRT_HEAD,
-                scalar2=None,
-                op0=ALU.mult,
-                op1=ALU.min,
-                accum_out=kept[("neg_max", u)][:, r : r + 1],
+            if r < TENSOR_MASKS:
+                nc.vector.tensor_scalar(
+                    out=kept[("neg_scores", u)][:, r, :],
+                    in0=kept[("scores_ps", u, r)][:].rearrange("p a x -> p (a x)"),
+                    scalar1=-INV_SQRT_HEAD,
+                    scalar2=None,
+                    op0=ALU.mult,
+                    op1=ALU.min,
+                    accum_out=kept[("neg_max", u)][:, r : r + 1],
+                )
+            else:
+                nc.vector.scalar_tensor_tensor(
+                    out=kept[("neg_scores", u)][:, r, :],
+                    in0=kept[("scores_ps", u, r)][:].rearrange("p a x -> p (a x)"),
+                    scalar=-INV_SQRT_HEAD,
+                    in1=kept[("neg_mask_rows", u // HEADS)][:].rearrange("p a x -> p (a x)"),
+                    op0=ALU.mult,
+                    op1=ALU.add,
+                )
+
+        def row_minimum(u, r):
+            nc.vector.tensor_reduce(
+                out=kept[("neg_max", u)][:, r : r + 1],
+                in_=kept[("neg_scores", u)][:, r, :],
+                axis=AXIS.X,
+                op=ALU.min,
             )
 
-        def exponentials(u):
-            e_sb = two.tile([P, TILES, SEQ], BF16)
-            row_sum = three.tile([P, TILES], F32)
-            for r in range(TILES):
-                nc.scalar.activation(
-                    out=e_sb[:, r, :].rearrange("p (u w e) -> p u w e", u=2, e=2),
-                    in_=kept[("neg_scores", u)][:, r, :].rearrange(
-                        "p (u e w) -> p u w e", u=2, e=2
-                    ),
-                    func=ACT.Exp,
-                    bias=kept[("neg_max", u)][:, r : r + 1],
-                    scale=-1.0,
-                    accum_out=row_sum[:, r : r + 1],
-                )
-            kept[("e_sb", u)] = e_sb
-            kept[("row_sum", u)] = row_sum
+        def exponential(u, r):
+            if r == 0:
+                e_sb = two.tile([P, TILES, SEQ], BF16)
+                row_sum = three.tile([P, TILES], F32)
+                kept[("e_sb", u)] = e_sb
+                kept[("row_sum", u)] = row_sum
+            nc.scalar.activation(
+                out=kept[("e_sb", u)][:, r, :].rearrange("p (u w e) -> p u w e", u=2, e=2),
+                in_=kept[("neg_scores", u)][:, r, :].rearrange("p (u e w) -> p u w e", u=2, e=2),
+                func=ACT.Exp,
+                bias=kept[("neg_max", u)][:, r : r + 1],
+                scale=-1.0,
+                accum_out=kept[("row_sum", u)][:, r : r + 1],
+            )
 
-        def turn_e(u):
+        def turn_e(u, half):
             e_words = kept[("e_sb", u)][:].bitcast(F32)
-            e_grouped = two.tile([P, SEQ * PACK], BF16, align_bytes=64)
-            e_grouped_words = (
-                e_grouped[:].bitcast(F32).rearrange("w (r i u) -> w r i u", r=TILES, u=2)
-            )
-            for half in range(TILES // 2):
-                turn_half = psum_turn.tile([P, 2, 2, P], F32, tag="turn")
-                for rr in range(2):
-                    for u2 in range(2):
-                        nc.tensor.transpose(
-                            out=turn_half[:, rr, u2, :],
-                            in_=e_words[:, 2 * half + rr, u2 * P : (u2 + 1) * P],
-                            identity=ident_f[:],
-                        )
-                copy_out = nc.scalar.copy if half == 0 else nc.vector.tensor_copy
-                copy_out(
-                    out=e_grouped_words[:, 2 * half : 2 * half + 2],
-                    in_=turn_half[:].rearrange("w r u i -> w r i u"),
-                )
-            kept[("e_grouped", u)] = e_grouped
-
-        def project_values(u):
-            b = u // HEADS
-            v_ps = psum_one.tile([P, TILES, HEAD], F32, tag="v")
-            for a in range(TILES):
-                for g in range(PASSES):
-                    key_cols = slice(g * P, (g + 1) * P)
-                    nc.tensor.matmul_mx(
-                        out=v_ps[:, a, :],
-                        lhsT=kept[("feat_codes", b)][:, a, key_cols].bitcast(FP8X4),
-                        lhsT_scale=kept[("feat_scales", b)][:, a, key_cols],
-                        rhs=w_codes[:, g, head_columns(u)].bitcast(FP8X4),
-                        rhs_scale=w_scales[:, g, head_columns(u)],
-                        start=(g == 0),
-                        stop=(g == PASSES - 1),
+            turn_half = psum_turn.tile([P, 2, 2, P], F32, tag="turn")
+            for rr in range(2):
+                for u2 in range(2):
+                    nc.tensor.transpose(
+                        out=turn_half[:, rr, u2, :],
+                        in_=e_words[:, 2 * half + rr, u2 * P : (u2 + 1) * P],
+                        identity=ident_f[:],
                     )
-            kept[("v_ps", u)] = v_ps
+            kept[("turn_half", u, half)] = turn_half
+
+        def copy_e(u, half):
+            if half == 0:
+                e_grouped = two.tile([P, SEQ * PACK], BF16, align_bytes=64)
+                kept[("e_grouped", u)] = e_grouped
+            nc.scalar.copy(
+                out=kept[("e_grouped", u)][:]
+                .bitcast(F32)
+                .rearrange("w (r i u) -> w r i u", r=TILES, u=2)[:, 2 * half : 2 * half + 2],
+                in_=kept[("turn_half", u, half)][:].rearrange("w r u i -> w r i u"),
+            )
+
+        def project_values(u, a, g):
+            b = u // HEADS
+            if a == 0 and g == 0:
+                v_ps = psum_one.tile([P, TILES, HEAD], F32, tag="v")
+                kept[("v_ps", u)] = v_ps
+            key_cols = slice(g * P, (g + 1) * P)
+            nc.tensor.matmul_mx(
+                out=kept[("v_ps", u)][:, a, :],
+                lhsT=kept[("feat_codes", b)][:, a, key_cols].bitcast(FP8X4),
+                lhsT_scale=kept[("feat_scales", b)][:, a, key_cols],
+                rhs=w_codes[:, g, head_columns(u)].bitcast(FP8X4),
+                rhs_scale=w_scales[:, g, head_columns(u)],
+                start=(g == 0),
+                stop=(g == PASSES - 1),
+            )
 
         def add_value_bias(u):
             v_grouped = two.tile([P, HEAD * PACK], BF16, align_bytes=64)
@@ -442,98 +507,128 @@ def tile_multiheadedselfattention_pa_t_kernel(
             kept[("v_codes", u)] = v_codes
             kept[("v_scales", u)] = v_scales
 
-        def attend(u):
-            h_ps = psum_one.tile([P, TILES, HEAD], F32, tag="h")
-            for r in range(TILES):
-                query_cols = slice(r * P, (r + 1) * P)
-                nc.tensor.matmul_mx(
-                    out=h_ps[:, r, :],
-                    lhsT=kept[("e_codes", u)][:, query_cols].bitcast(FP8X4),
-                    lhsT_scale=kept[("e_scales", u)][:, query_cols],
-                    rhs=kept[("v_codes", u)][:].bitcast(FP8X4),
-                    rhs_scale=kept[("v_scales", u)][:],
-                    start=True,
-                    stop=True,
-                )
-            kept[("h_ps", u)] = h_ps
-
-        def blend(u):
-            b = u // HEADS
-            minus_h_gated = two.tile([P, TILES, HEAD], F32)
-            for r in range(TILES):
-                nc.scalar.activation(
-                    out=minus_h_gated[:, r, :],
-                    in_=kept[("h_ps", u)][:, r, :],
-                    func=ACT.Copy,
-                    scale=kept[("minus_gate_over_sum", u)][:, r : r + 1],
-                )
-            result = kept[("result", b)]
-            nc.gpsimd.tensor_tensor(
-                out=result[:, :, head_columns(u)],
-                in0=result[:, :, head_columns(u)],
-                in1=minus_h_gated[:],
-                op=ALU.subtract,
+        def attend(u, r):
+            if r == 0:
+                h_ps = psum_one.tile([P, TILES, HEAD], F32, tag="h")
+                kept[("h_ps", u)] = h_ps
+            query_cols = slice(r * P, (r + 1) * P)
+            nc.tensor.matmul_mx(
+                out=kept[("h_ps", u)][:, r, :],
+                lhsT=kept[("e_codes", u)][:, query_cols].bitcast(FP8X4),
+                lhsT_scale=kept[("e_scales", u)][:, query_cols],
+                rhs=kept[("v_codes", u)][:].bitcast(FP8X4),
+                rhs_scale=kept[("v_scales", u)][:],
+                start=True,
+                stop=True,
             )
+
+        def blend(u, r):
+            result = kept[("result", u // HEADS)]
+            nc.vector.scalar_tensor_tensor(
+                out=result[:, r, head_columns(u)],
+                in0=kept[("h_ps", u)][:, r, :],
+                scalar=kept[("gate_over_sum", u)][:, r : r + 1],
+                in1=result[:, r, head_columns(u)],
+                op0=ALU.mult,
+                op1=ALU.subtract,
+            )
+
+        def store(u):
+            b = u // HEADS
             nc.sync.dma_start(
                 out=out[b].rearrange("(p r) c -> p r c", r=TILES)[:, :, head_columns(u)],
-                in_=result[:, :, head_columns(u)],
+                in_=kept[("result", b)][:, :, head_columns(u)],
             )
 
         turn_q_and_k(0)
-        for r in range(TILES - 1):
-            score_matmul(0, r)
-        pooled_matmuls(0)
+        copy_q_and_k(0)
+        score_matmul(0, 0)
+        score_matmul(0, 1)
         turn_q_and_k(1)
-        turn_features(0)
-        turn_features(1)
+        copy_q_and_k(1)
+        pooled_matmuls(0)
         pooled_sum(0)
-        for i in range(UNITS + 5):
-            if live(i - 3):
-                quantise_e_and_v(i - 3)
-                minus_gate_over_row_sum(i - 3)
-            if i > 0 and live(i + 1):
-                quantise_features(i + 1)
-            if live(i - 2):
-                turn_e(i - 2)
-            if live(i + 1):
-                pooled_matmuls(i + 1)
-            if live(i - 4):
-                blend(i - 4)
-            if live(i - 2):
-                start_result(i - 2)
-            if live(i + 2):
-                turn_q_and_k(i + 2)
-                turn_features(i + 2)
-            if live(i):
-                for r in range(TILES):
-                    negate_scores(i, r)
-                    if r == 0:
-                        score_matmul(i, TILES - 1)
-                one_minus_gate_of(i)
-            if i == 0:
-                quantise_features(0)
-                quantise_features(1)
-            if i < PASSES:
-                group_weights(i)
-                if i > 0:
-                    quantise_weights(i - 1)
-            if i == PASSES:
-                quantise_weights(PASSES - 1)
-            if live(i - 2):
-                project_values(i - 2)
-                add_value_bias(i - 2)
-            if live(i - 3):
-                attend(i - 3)
-            if live(i + 1):
-                pooled_sum(i + 1)
-            if live(i - 2):
-                invert_row_sum(i - 2)
-            if live(i - 1):
-                exponentials(i - 1)
-            if live(i + 1):
-                for r in range(TILES - 1):
-                    score_matmul(i + 1, r)
-            if i % HEADS == 0 and i // HEADS + 1 < BATCH:
-                prepare_masks(i // HEADS + 1)
-            if i % HEADS == 1 and i // HEADS + 2 < BATCH:
-                load_batch(i // HEADS + 2)
+        load_batch(1)
+        turn_features(0)
+        copy_features(0)
+        turn_features(1)
+        for i in range(UNITS + 4):
+            for j in range(TILES):
+                ahead = TILES * i + j + 2
+                if ahead < TILES * UNITS:
+                    score_matmul(ahead // TILES, ahead % TILES)
+                if j == 3 and live(i + 1):
+                    pooled_matmuls(i + 1)
+                if j == 0 and live(i - 1):
+                    turn_e(i - 1, 0)
+                if j == 2 and live(i - 1):
+                    turn_e(i - 1, 1)
+                if j == 0 and i == 0:
+                    turn_features(2)
+                if j == 1 and i > 0 and live(i + 3):
+                    turn_features(i + 3)
+                if j == 2 and i == 0:
+                    turn_features(3)
+                if j == 3 and live(i + 2):
+                    turn_q_and_k(i + 2)
+                if j < 2 and live(i - 3):
+                    attend(i - 3, 2 * j)
+                    attend(i - 3, 2 * j + 1)
+                if j >= 2 and live(i - 1):
+                    for a in (2 * j - 4, 2 * j - 3):
+                        for g in range(PASSES):
+                            project_values(i - 1, a, g)
+                if j == 0 and live(i):
+                    gate_minus_one_of(i)
+                    start_result(i)
+                if j == 0 and i > 0 and live(i + 1):
+                    copy_q_and_k(i + 1)
+                if j == 0 and i == 0:
+                    copy_features(1)
+                if j == 1 and live(i - 1):
+                    copy_e(i - 1, 0)
+                if j == 1 and i == 0:
+                    copy_features(2)
+                if j == 2 and i > 0 and live(i + 3):
+                    copy_features(i + 3)
+                if j == 3 and live(i - 1):
+                    copy_e(i - 1, 1)
+                if j == 3 and i == 0:
+                    copy_features(3)
+                before = TILES * i + j - 1
+                if 0 <= before < TILES * UNITS:
+                    exponential(before // TILES, before % TILES)
+                if live(i):
+                    negate_scores(i, j)
+                if j == 0 and live(i - 2):
+                    add_value_bias(i - 2)
+                if j == 1 and live(i - 2):
+                    quantise_e_and_v(i - 2)
+                if live(i - 3):
+                    for r in ((), (0,), (1, 2, 3), ())[j]:
+                        blend(i - 3, r)
+                    if j == 2:
+                        store(i - 3)
+                if j == 3 and i > 0 and live(i + 3):
+                    quantise_features(i + 3)
+                if j == 3 and live(i + 1):
+                    pooled_sum(i + 1)
+                if j == 3 and live(i - 1):
+                    invert_row_sum(i - 1)
+                if j == 0 and live(i - 2):
+                    gate_over_row_sum(i - 2)
+                if live(i) and j >= TENSOR_MASKS:
+                    row_minimum(i, j)
+                if i == 0:
+                    quantise_features(j)
+                    if j >= 2:
+                        group_weights(j - 2)
+                if i == 1 and j < 2:
+                    quantise_weights(j)
+                if j == 2 and i // HEADS + 1 < BATCH and i % HEADS < 2:
+                    for a in (2 * (i % HEADS), 2 * (i % HEADS) + 1):
+                        keep_keys(i // HEADS + 1, a)
+                        spread_mask_cols(i // HEADS + 1, a)
+                        order_mask_rows(i // HEADS + 1, a)
+                if j == 3 and i % HEADS == 1 and i // HEADS + 2 < BATCH:
+                    load_batch(i // HEADS + 2)

@@ -27,8 +27,7 @@ D_OUT = 640
 UNITS = BATCH * HEADS
 INV_SQRT_HEAD = 1.0 / math.sqrt(HEAD)
 MASKED = -1.0e30
-TENSOR_MASKS = 3
-PLAIN_TURNS = 3
+VECTOR_MASKS = (0,)
 
 FLOPS = 2 * BATCH * SEQ * D_FEAT * D_MODEL + 2 * 2 * BATCH * HEADS * SEQ * SEQ * HEAD
 
@@ -55,7 +54,7 @@ def tile_multiheadedselfattention_pa_t_kernel(
         three = stack.enter_context(tc.tile_pool(name="three", bufs=3))
         four = stack.enter_context(tc.tile_pool(name="four", bufs=4))
         five = stack.enter_context(tc.tile_pool(name="five", bufs=5))
-        psum_scores = stack.enter_context(tc.psum_pool(name="psum_scores", bufs=3))
+        psum_scores = stack.enter_context(tc.psum_pool(name="psum_scores", bufs=4))
         psum_turn = stack.enter_context(tc.psum_pool(name="psum_turn", bufs=2))
         psum_one = stack.enter_context(tc.psum_pool(name="psum_one", bufs=1))
 
@@ -132,57 +131,56 @@ def tile_multiheadedselfattention_pa_t_kernel(
         ident_f = const.tile([P, P], F32)
         make_identity(nc, ident_f[:])
 
-        def keep_keys(b, a):
-            if a == 0:
-                kept_keys = two.tile([P, TILES, P], BF16)
-                kept[("kept_keys", b)] = kept_keys
-            nc.gpsimd.tensor_scalar(
-                out=kept[("kept_keys", b)][:, a, :],
-                in0=ident_bf[:],
-                scalar1=mask_cols[:, b, a : a + 1],
-                scalar2=0.0,
-                op0=ALU.mult,
-                op1=ALU.add,
+        def keep_keys(b):
+            kept_keys = two.tile([P, TILES, P], BF16)
+            nc.gpsimd.tensor_tensor(
+                out=kept_keys[:],
+                in0=ident_bf[:].unsqueeze(1).to_broadcast([P, TILES, P]),
+                in1=mask_cols[:, b, :].unsqueeze(2).to_broadcast([P, TILES, P]),
+                op=ALU.mult,
             )
+            kept[("kept_keys", b)] = kept_keys
 
-        def spread_mask_cols(b, a):
-            if a == 0:
-                mask_bias = two.tile([P, TILES, P], F32)
-                kept[("mask_bias", b)] = mask_bias
+        def spread_mask_cols(b):
+            mask_bias = two.tile([P, TILES, P], F32)
             nc.gpsimd.tensor_scalar(
-                out=kept[("mask_bias", b)][:, a, :],
-                in0=mask_cols[:, b, a : a + 1].to_broadcast([P, P]),
+                out=mask_bias[:],
+                in0=mask_cols[:, b, :].unsqueeze(2).to_broadcast([P, TILES, P]),
                 scalar1=-1.0,
                 scalar2=-MASKED,
                 op0=ALU.add,
                 op1=ALU.mult,
             )
+            kept[("mask_bias", b)] = mask_bias
 
-        def order_mask_rows(b, a):
-            if a == 0:
-                neg_mask_rows = two.tile([P, TILES, P], BF16)
-                kept[("neg_mask_rows", b)] = neg_mask_rows
+        def order_mask_rows(b):
+            neg_mask_rows = two.tile([P, TILES, P], BF16)
             nc.gpsimd.tensor_scalar(
-                out=kept[("neg_mask_rows", b)][:, a, :],
-                in0=kept[("mask_rows", b)][:].rearrange("p (x a) -> p a x", a=TILES)[:, a, :],
+                out=neg_mask_rows[:],
+                in0=kept[("mask_rows", b)][:].rearrange("p (x a) -> p a x", a=TILES),
                 scalar1=-1.0,
                 scalar2=MASKED,
                 op0=ALU.add,
                 op1=ALU.mult,
             )
+            kept[("neg_mask_rows", b)] = neg_mask_rows
 
-        for prepare in (keep_keys, spread_mask_cols, order_mask_rows):
-            for a in range(TILES):
-                prepare(0, a)
+        prepare_masks = (keep_keys, spread_mask_cols, order_mask_rows)
+        for prepare in prepare_masks:
+            prepare(0)
 
         w_grouped = const.tile([P, PASSES, D_MODEL * PACK], BF16, align_bytes=64)
         w_codes = const.tile([P, PASSES, D_MODEL], U32, align_bytes=64)
         w_scales = const.tile([P, PASSES, D_MODEL], U8, align_bytes=64)
 
         def group_weights(g):
-            nc.vector.tensor_copy(
+            nc.gpsimd.tensor_scalar(
                 out=w_grouped[:, g, :].rearrange("w (d t) -> w d t", t=PACK),
-                in_=w_raw[:, g, :, :].rearrange("w t d -> w d t"),
+                in0=w_raw[:, g, :, :].rearrange("w t d -> w d t"),
+                scalar1=1.0,
+                scalar2=0.0,
+                op0=ALU.mult,
+                op1=ALU.add,
             )
 
         def quantise_weights(g):
@@ -252,13 +250,10 @@ def tile_multiheadedselfattention_pa_t_kernel(
                     identity=ident_bf[:],
                 )
             for a in range(TILES):
-                nc.tensor.matmul(
+                nc.tensor.transpose(
                     out=turn_qk[:, 1, a, :],
-                    lhsT=kept[("k", b)][:, a, head_columns(u)],
-                    rhs=kept[("kept_keys", b)][:, a, :],
-                    is_transpose=(a >= PLAIN_TURNS),
-                    start=True,
-                    stop=True,
+                    in_=kept[("k", b)][:, a, head_columns(u)],
+                    identity=kept[("kept_keys", b)][:, a, :],
                 )
             kept[("turn_qk", u)] = turn_qk
 
@@ -288,7 +283,7 @@ def tile_multiheadedselfattention_pa_t_kernel(
             kept[("key_sum", u)] = key_sum
 
         def pooled_matmuls(u):
-            pooled_ps = psum_one.tile([P, TILES, 2], F32, tag="pooled")
+            pooled_ps = psum_one.tile([P, TILES, 2], F32, tag="h")
             for r in range(TILES):
                 nc.tensor.matmul(
                     out=pooled_ps[:, r, :],
@@ -362,15 +357,12 @@ def tile_multiheadedselfattention_pa_t_kernel(
                     in_=result[:, :, D_MODEL:D_OUT],
                 )
                 kept[("result", b)] = result
-            for r in range(TILES):
-                nc.gpsimd.tensor_scalar(
-                    out=kept[("result", b)][:, r, head_columns(u)],
-                    in0=stream_sb[:, r, head_columns(u)],
-                    scalar1=kept[("gate_minus_one", u)][:, r : r + 1],
-                    scalar2=0.0,
-                    op0=ALU.mult,
-                    op1=ALU.add,
-                )
+            nc.gpsimd.tensor_tensor(
+                out=kept[("result", b)][:, :, head_columns(u)],
+                in0=stream_sb[:, :, head_columns(u)],
+                in1=kept[("gate_minus_one", u)][:].unsqueeze(2).to_broadcast([P, TILES, HEAD]),
+                op=ALU.mult,
+            )
 
         def score_matmul(u, r):
             scores_ps = psum_scores.tile([P, TILES, P], F32, tag="scores")
@@ -379,19 +371,20 @@ def tile_multiheadedselfattention_pa_t_kernel(
                 lhsT=kept[("q_turned", u)][:, r, :],
                 rhs=kept[("k_turned", u)][:].rearrange("c a x -> c (a x)"),
                 start=True,
-                stop=(r >= TENSOR_MASKS),
+                stop=(r in VECTOR_MASKS),
             )
-            if r < TENSOR_MASKS:
-                for a in range(TILES):
-                    nc.tensor.matmul(
-                        out=scores_ps[:, a, :],
-                        lhsT=kept[("mask_bias", u // HEADS)][:, a, :],
-                        rhs=ident_f[:],
-                        is_transpose=True,
-                        start=False,
-                        stop=(a == TILES - 1),
-                    )
             kept[("scores_ps", u, r)] = scores_ps
+
+        def mask_scores(u, r):
+            for a in range(TILES):
+                nc.tensor.matmul(
+                    out=kept[("scores_ps", u, r)][:, a, :],
+                    lhsT=kept[("mask_bias", u // HEADS)][:, a, :],
+                    rhs=ident_f[:],
+                    is_transpose=True,
+                    start=False,
+                    stop=(a == TILES - 1),
+                )
 
         def negate_scores(u, r):
             if r == 0:
@@ -399,7 +392,7 @@ def tile_multiheadedselfattention_pa_t_kernel(
                 neg_max = three.tile([P, TILES], F32)
                 kept[("neg_scores", u)] = neg_scores
                 kept[("neg_max", u)] = neg_max
-            if r < TENSOR_MASKS:
+            if r not in VECTOR_MASKS:
                 nc.vector.tensor_scalar(
                     out=kept[("neg_scores", u)][:, r, :],
                     in0=kept[("scores_ps", u, r)][:].rearrange("p a x -> p (a x)"),
@@ -522,113 +515,118 @@ def tile_multiheadedselfattention_pa_t_kernel(
                 stop=True,
             )
 
-        def blend(u, r):
-            result = kept[("result", u // HEADS)]
-            nc.vector.scalar_tensor_tensor(
-                out=result[:, r, head_columns(u)],
-                in0=kept[("h_ps", u)][:, r, :],
-                scalar=kept[("gate_over_sum", u)][:, r : r + 1],
-                in1=result[:, r, head_columns(u)],
-                op0=ALU.mult,
-                op1=ALU.subtract,
-            )
-
-        def store(u):
+        def blend(u):
             b = u // HEADS
+            result = kept[("result", b)]
+            for r in range(TILES):
+                nc.vector.scalar_tensor_tensor(
+                    out=result[:, r, head_columns(u)],
+                    in0=kept[("h_ps", u)][:, r, :],
+                    scalar=kept[("gate_over_sum", u)][:, r : r + 1],
+                    in1=result[:, r, head_columns(u)],
+                    op0=ALU.mult,
+                    op1=ALU.subtract,
+                )
             nc.sync.dma_start(
                 out=out[b].rearrange("(p r) c -> p r c", r=TILES)[:, :, head_columns(u)],
-                in_=kept[("result", b)][:, :, head_columns(u)],
+                in_=result[:, :, head_columns(u)],
             )
+
+        def pair(n):
+            return [(n // 2, 2 * (n % 2) + r) for r in range(2)] if 0 <= n < 2 * UNITS else []
 
         turn_q_and_k(0)
         copy_q_and_k(0)
-        score_matmul(0, 0)
-        score_matmul(0, 1)
-        turn_q_and_k(1)
-        copy_q_and_k(1)
+        for u, r in pair(0):
+            score_matmul(u, r)
+        for u, r in pair(0):
+            if r not in VECTOR_MASKS:
+                mask_scores(u, r)
         pooled_matmuls(0)
         pooled_sum(0)
+        turn_q_and_k(1)
+        copy_q_and_k(1)
         load_batch(1)
-        turn_features(0)
-        copy_features(0)
-        turn_features(1)
-        for i in range(UNITS + 4):
-            for j in range(TILES):
-                ahead = TILES * i + j + 2
-                if ahead < TILES * UNITS:
-                    score_matmul(ahead // TILES, ahead % TILES)
-                if j == 3 and live(i + 1):
-                    pooled_matmuls(i + 1)
-                if j == 0 and live(i - 1):
-                    turn_e(i - 1, 0)
-                if j == 2 and live(i - 1):
-                    turn_e(i - 1, 1)
-                if j == 0 and i == 0:
-                    turn_features(2)
-                if j == 1 and i > 0 and live(i + 3):
-                    turn_features(i + 3)
-                if j == 2 and i == 0:
-                    turn_features(3)
-                if j == 3 and live(i + 2):
-                    turn_q_and_k(i + 2)
-                if j < 2 and live(i - 3):
-                    attend(i - 3, 2 * j)
-                    attend(i - 3, 2 * j + 1)
-                if j >= 2 and live(i - 1):
-                    for a in (2 * j - 4, 2 * j - 3):
+        for piece in range(2):
+            turn_features(piece)
+            copy_features(piece)
+        for step in range(2 * UNITS + 6):
+            i, second = step // 2, step % 2 == 1
+            if second and live(i - 3):
+                blend(i - 3)
+            if second and live(i - 2):
+                quantise_e_and_v(i - 2)
+            for u, r in pair(step + 1):
+                score_matmul(u, r)
+            if second:
+                if live(i - 1):
+                    for a in range(TILES):
                         for g in range(PASSES):
                             project_values(i - 1, a, g)
-                if j == 0 and live(i):
-                    gate_minus_one_of(i)
-                    start_result(i)
-                if j == 0 and i > 0 and live(i + 1):
-                    copy_q_and_k(i + 1)
-                if j == 0 and i == 0:
-                    copy_features(1)
-                if j == 1 and live(i - 1):
-                    copy_e(i - 1, 0)
-                if j == 1 and i == 0:
-                    copy_features(2)
-                if j == 2 and i > 0 and live(i + 3):
-                    copy_features(i + 3)
-                if j == 3 and live(i - 1):
-                    copy_e(i - 1, 1)
-                if j == 3 and i == 0:
-                    copy_features(3)
-                before = TILES * i + j - 1
-                if 0 <= before < TILES * UNITS:
-                    exponential(before // TILES, before % TILES)
-                if live(i):
-                    negate_scores(i, j)
-                if j == 0 and live(i - 2):
-                    add_value_bias(i - 2)
-                if j == 1 and live(i - 2):
-                    quantise_e_and_v(i - 2)
-                if live(i - 3):
-                    for r in ((), (0,), (1, 2, 3), ())[j]:
-                        blend(i - 3, r)
-                    if j == 2:
-                        store(i - 3)
-                if j == 3 and i > 0 and live(i + 3):
-                    quantise_features(i + 3)
-                if j == 3 and live(i + 1):
+                if live(i + 1):
+                    pooled_matmuls(i + 1)
+            elif live(i - 3):
+                for r in range(TILES):
+                    attend(i - 3, r)
+            for u, r in pair(step - 3)[:1]:
+                copy_e(u, r // 2)
+            for u, r in pair(step - 1)[:1]:
+                exponential(u, r)
+            if second and live(i + 2):
+                copy_q_and_k(i + 2)
+            if not second and i > 0 and live(i + 3):
+                copy_features(i + 3)
+            if 0 < step < 3:
+                copy_features(step + 1)
+            if not second and live(i):
+                gate_minus_one_of(i)
+            for u, r in pair(step - 1)[1:]:
+                exponential(u, r)
+            for u, r in pair(step + 1):
+                if r not in VECTOR_MASKS:
+                    mask_scores(u, r)
+            for u, r in pair(step - 2)[:1]:
+                turn_e(u, r // 2)
+            if not second:
+                if live(i + 2):
+                    turn_q_and_k(i + 2)
+            elif live(i + 4):
+                turn_features(i + 4)
+            if step < 2:
+                turn_features(step + 2)
+            for u, r in pair(step):
+                negate_scores(u, r)
+            for u, r in pair(step):
+                if r in VECTOR_MASKS:
+                    row_minimum(u, r)
+            if second:
+                if live(i + 1):
                     pooled_sum(i + 1)
-                if j == 3 and live(i - 1):
-                    invert_row_sum(i - 1)
-                if j == 0 and live(i - 2):
+                if live(i - 2):
                     gate_over_row_sum(i - 2)
-                if live(i) and j >= TENSOR_MASKS:
-                    row_minimum(i, j)
-                if i == 0:
-                    quantise_features(j)
-                    if j >= 2:
-                        group_weights(j - 2)
-                if i == 1 and j < 2:
-                    quantise_weights(j)
-                if j == 2 and i // HEADS + 1 < BATCH and i % HEADS < 2:
-                    for a in (2 * (i % HEADS), 2 * (i % HEADS) + 1):
-                        keep_keys(i // HEADS + 1, a)
-                        spread_mask_cols(i // HEADS + 1, a)
-                        order_mask_rows(i // HEADS + 1, a)
-                if j == 3 and i % HEADS == 1 and i // HEADS + 2 < BATCH:
-                    load_batch(i // HEADS + 2)
+                if i > 0 and live(i + 3):
+                    quantise_features(i + 3)
+            else:
+                if live(i - 2):
+                    add_value_bias(i - 2)
+                if live(i - 2):
+                    invert_row_sum(i - 2)
+            if step == 0:
+                quantise_features(0)
+                quantise_features(1)
+            if step == 2:
+                for g in range(PASSES):
+                    quantise_weights(g)
+            if step == 1:
+                quantise_features(2)
+            if step == 2:
+                quantise_features(3)
+            if not second and live(i):
+                start_result(i)
+            if step == 0:
+                for g in range(PASSES):
+                    group_weights(g)
+            if second and i // HEADS + 1 < BATCH and i % HEADS < len(prepare_masks):
+                prepare_masks[i % HEADS](i // HEADS + 1)
+            if second and i % HEADS == 1 and i // HEADS + 2 < BATCH:
+                load_batch(i // HEADS + 2)

@@ -27,7 +27,7 @@ D_OUT = 640
 UNITS = BATCH * HEADS
 INV_SQRT_HEAD = 1.0 / math.sqrt(HEAD)
 MASKED = -1.0e30
-VECTOR_MASKS = (0,)
+MATMUL_MASK_HEADS = 3
 
 FLOPS = 2 * BATCH * SEQ * D_FEAT * D_MODEL + 2 * 2 * BATCH * HEADS * SEQ * SEQ * HEAD
 
@@ -62,6 +62,11 @@ def tile_multiheadedselfattention_pa_t_kernel(
 
         def live(u):
             return 0 <= u < UNITS
+
+        def mask_way(u, r):
+            if r > 0:
+                return "transposes"
+            return "matmul" if u % HEADS < MATMUL_MASK_HEADS else "vector"
 
         def head_columns(u):
             return slice((u % HEADS) * HEAD, (u % HEADS + 1) * HEAD)
@@ -165,6 +170,8 @@ def tile_multiheadedselfattention_pa_t_kernel(
             )
             kept[("neg_mask_rows", b)] = neg_mask_rows
 
+        minus_mean = const.tile([P, P], BF16)
+        nc.vector.memset(minus_mean[:], -1.0 / P)
         prepare_masks = (keep_keys, spread_mask_cols, order_mask_rows)
         for prepare in prepare_masks:
             prepare(0)
@@ -339,24 +346,25 @@ def tile_multiheadedselfattention_pa_t_kernel(
             )
             kept[("gate_over_sum", u)] = gate_over_sum
 
+        def pass_stream(b):
+            result = three.tile([P, TILES, D_OUT], F32)
+            nc.gpsimd.tensor_scalar(
+                out=result[:, :, D_MODEL:D_OUT],
+                in0=kept[("stream", b)][:, :, D_MODEL:D_OUT],
+                scalar1=1.0,
+                scalar2=0.0,
+                op0=ALU.mult,
+                op1=ALU.add,
+            )
+            nc.sync.dma_start(
+                out=out[b].rearrange("(p r) c -> p r c", r=TILES)[:, :, D_MODEL:D_OUT],
+                in_=result[:, :, D_MODEL:D_OUT],
+            )
+            kept[("result", b)] = result
+
         def start_result(u):
             b, n = u // HEADS, u % HEADS
             stream_sb = kept[("stream", b)]
-            if n == 0:
-                result = three.tile([P, TILES, D_OUT], F32)
-                nc.gpsimd.tensor_scalar(
-                    out=result[:, :, D_MODEL:D_OUT],
-                    in0=stream_sb[:, :, D_MODEL:D_OUT],
-                    scalar1=1.0,
-                    scalar2=0.0,
-                    op0=ALU.mult,
-                    op1=ALU.add,
-                )
-                nc.sync.dma_start(
-                    out=out[b].rearrange("(p r) c -> p r c", r=TILES)[:, :, D_MODEL:D_OUT],
-                    in_=result[:, :, D_MODEL:D_OUT],
-                )
-                kept[("result", b)] = result
             nc.gpsimd.tensor_tensor(
                 out=kept[("result", b)][:, :, head_columns(u)],
                 in0=stream_sb[:, :, head_columns(u)],
@@ -371,8 +379,16 @@ def tile_multiheadedselfattention_pa_t_kernel(
                 lhsT=kept[("q_turned", u)][:, r, :],
                 rhs=kept[("k_turned", u)][:].rearrange("c a x -> c (a x)"),
                 start=True,
-                stop=(r in VECTOR_MASKS),
+                stop=(mask_way(u, r) == "vector"),
             )
+            if mask_way(u, r) == "matmul":
+                nc.tensor.matmul(
+                    out=scores_ps[:].rearrange("p a x -> p (a x)"),
+                    lhsT=minus_mean[:],
+                    rhs=kept[("neg_mask_rows", u // HEADS)][:].rearrange("p a x -> p (a x)"),
+                    start=False,
+                    stop=True,
+                )
             kept[("scores_ps", u, r)] = scores_ps
 
         def mask_scores(u, r):
@@ -392,7 +408,7 @@ def tile_multiheadedselfattention_pa_t_kernel(
                 neg_max = three.tile([P, TILES], F32)
                 kept[("neg_scores", u)] = neg_scores
                 kept[("neg_max", u)] = neg_max
-            if r not in VECTOR_MASKS:
+            if mask_way(u, r) != "vector":
                 nc.vector.tensor_scalar(
                     out=kept[("neg_scores", u)][:, r, :],
                     in0=kept[("scores_ps", u, r)][:].rearrange("p a x -> p (a x)"),
@@ -540,7 +556,7 @@ def tile_multiheadedselfattention_pa_t_kernel(
         for u, r in pair(0):
             score_matmul(u, r)
         for u, r in pair(0):
-            if r not in VECTOR_MASKS:
+            if mask_way(u, r) == "transposes":
                 mask_scores(u, r)
         pooled_matmuls(0)
         pooled_sum(0)
@@ -550,6 +566,7 @@ def tile_multiheadedselfattention_pa_t_kernel(
         for piece in range(2):
             turn_features(piece)
             copy_features(piece)
+        prepare_batch = prepare_masks + (pass_stream,)
         for step in range(2 * UNITS + 6):
             i, second = step // 2, step % 2 == 1
             if second and live(i - 3):
@@ -583,7 +600,7 @@ def tile_multiheadedselfattention_pa_t_kernel(
             for u, r in pair(step - 1)[1:]:
                 exponential(u, r)
             for u, r in pair(step + 1):
-                if r not in VECTOR_MASKS:
+                if mask_way(u, r) == "transposes":
                     mask_scores(u, r)
             for u, r in pair(step - 2)[:1]:
                 turn_e(u, r // 2)
@@ -597,7 +614,7 @@ def tile_multiheadedselfattention_pa_t_kernel(
             for u, r in pair(step):
                 negate_scores(u, r)
             for u, r in pair(step):
-                if r in VECTOR_MASKS:
+                if mask_way(u, r) == "vector":
                     row_minimum(u, r)
             if second:
                 if live(i + 1):
@@ -621,12 +638,14 @@ def tile_multiheadedselfattention_pa_t_kernel(
                 quantise_features(2)
             if step == 2:
                 quantise_features(3)
+            if step == 0:
+                pass_stream(0)
             if not second and live(i):
                 start_result(i)
             if step == 0:
                 for g in range(PASSES):
                     group_weights(g)
-            if second and i // HEADS + 1 < BATCH and i % HEADS < len(prepare_masks):
-                prepare_masks[i % HEADS](i // HEADS + 1)
+            if second and i // HEADS + 1 < BATCH:
+                prepare_batch[i % HEADS](i // HEADS + 1)
             if second and i % HEADS == 1 and i // HEADS + 2 < BATCH:
                 load_batch(i // HEADS + 2)

@@ -76,11 +76,17 @@ def tile_multiheadedselfattention_pa_t_kernel(
             queue.dma_start(out=mask_rows[:], in_=value_key_masks[b].partition_broadcast(P))
             kept[("mask_rows", b)] = mask_rows
 
-        def load_q_and_k(b):
+        def load_q_and_k(b, pieces=1):
             q_sb = three.tile([P, TILES, D_MODEL], BF16)
-            nc.sync.dma_start(out=q_sb[:], in_=q[b].rearrange("(p r) c -> p r c", r=TILES))
             k_sb = three.tile([P, TILES, D_MODEL], BF16)
-            nc.sync.dma_start(out=k_sb[:], in_=k[b].rearrange("(p r) c -> p r c", r=TILES))
+            width = D_MODEL // pieces
+            for c0 in range(0, D_MODEL, width):
+                cols = slice(c0, c0 + width)
+                for tile_sb, dram in ((q_sb, q), (k_sb, k)):
+                    nc.sync.dma_start(
+                        out=tile_sb[:, :, cols],
+                        in_=dram[b].rearrange("(p r) c -> p r c", r=TILES)[:, :, cols],
+                    )
             kept[("q", b)] = q_sb
             kept[("k", b)] = k_sb
 
@@ -108,7 +114,7 @@ def tile_multiheadedselfattention_pa_t_kernel(
         nc.scalar.dma_start(
             out=mask_cols[:], in_=value_key_masks.rearrange("b (p a) -> p b a", a=TILES)
         )
-        load_q_and_k(0)
+        load_q_and_k(0, pieces=2)
         load_mask_rows(0, nc.scalar)
         counts = const.tile([P, BATCH], BF16)
         nc.scalar.dma_start(out=counts[:], in_=value_key_counts.partition_broadcast(P))
@@ -129,12 +135,11 @@ def tile_multiheadedselfattention_pa_t_kernel(
         )
         bv_rows = const.tile([P, D_MODEL], BF16)
         nc.scalar.dma_start(out=bv_rows[:], in_=bv.partition_broadcast(P))
+        load_features(1)
         load_stream(0)
 
         ident_bf = const.tile([P, P], BF16)
         make_identity(nc, ident_bf[:])
-        ident_f = const.tile([P, P], F32)
-        make_identity(nc, ident_f[:])
 
         def keep_keys(b):
             kept_keys = two.tile([P, TILES, P], BF16)
@@ -173,8 +178,11 @@ def tile_multiheadedselfattention_pa_t_kernel(
         minus_mean = const.tile([P, P], BF16)
         nc.vector.memset(minus_mean[:], -1.0 / P)
         prepare_masks = (keep_keys, spread_mask_cols, order_mask_rows)
-        for prepare in prepare_masks:
-            prepare(0)
+        keep_keys(0)
+        ident_f = const.tile([P, P], F32)
+        make_identity(nc, ident_f[:])
+        order_mask_rows(0)
+        spread_mask_cols(0)
 
         w_grouped = const.tile([P, PASSES, D_MODEL * PACK], BF16, align_bytes=64)
         w_codes = const.tile([P, PASSES, D_MODEL], U32, align_bytes=64)
@@ -198,18 +206,20 @@ def tile_multiheadedselfattention_pa_t_kernel(
             )
 
         inv_count = const.tile([P, BATCH], F32)
-        nc.vector.reciprocal(out=inv_count[:], in_=counts[:])
         half_gain = const.tile([P, HEADS], F32)
-        nc.vector.tensor_scalar_mul(out=half_gain[:], in0=gain[:], scalar1=0.5 * INV_SQRT_HEAD)
         half_gate_bias = const.tile([P, HEADS], F32)
-        nc.vector.tensor_scalar_mul(out=half_gate_bias[:], in0=gate_bias[:], scalar1=0.5)
         half_gain_over_count = const.tile([P, BATCH, HEADS], F32)
-        nc.vector.tensor_tensor(
-            out=half_gain_over_count[:],
-            in0=half_gain[:].unsqueeze(1).to_broadcast([P, BATCH, HEADS]),
-            in1=inv_count[:].unsqueeze(2).to_broadcast([P, BATCH, HEADS]),
-            op=ALU.mult,
-        )
+
+        def gate_constants():
+            nc.vector.reciprocal(out=inv_count[:], in_=counts[:])
+            nc.vector.tensor_scalar_mul(out=half_gain[:], in0=gain[:], scalar1=0.5 * INV_SQRT_HEAD)
+            nc.vector.tensor_scalar_mul(out=half_gate_bias[:], in0=gate_bias[:], scalar1=0.5)
+            nc.vector.tensor_tensor(
+                out=half_gain_over_count[:],
+                in0=half_gain[:].unsqueeze(1).to_broadcast([P, BATCH, HEADS]),
+                in1=inv_count[:].unsqueeze(2).to_broadcast([P, BATCH, HEADS]),
+                op=ALU.mult,
+            )
 
         def turn_features(piece):
             b, a = piece // TILES, piece % TILES
@@ -551,18 +561,18 @@ def tile_multiheadedselfattention_pa_t_kernel(
         def pair(n):
             return [(n // 2, 2 * (n % 2) + r) for r in range(2)] if 0 <= n < 2 * UNITS else []
 
-        turn_q_and_k(0)
-        copy_q_and_k(0)
+        for u in range(2):
+            turn_q_and_k(u)
+            copy_q_and_k(u)
         for u, r in pair(0):
             score_matmul(u, r)
         for u, r in pair(0):
             if mask_way(u, r) == "transposes":
                 mask_scores(u, r)
         pooled_matmuls(0)
-        pooled_sum(0)
-        turn_q_and_k(1)
-        copy_q_and_k(1)
-        load_batch(1)
+        load_q_and_k(1)
+        load_mask_rows(1, nc.sync)
+        load_stream(1)
         for piece in range(2):
             turn_features(piece)
             copy_features(piece)
@@ -585,20 +595,22 @@ def tile_multiheadedselfattention_pa_t_kernel(
             elif live(i - 3):
                 for r in range(TILES):
                     attend(i - 3, r)
+            if step == 1:
+                for u, r in pair(0):
+                    exponential(u, r)
             for u, r in pair(step - 3)[:1]:
                 copy_e(u, r // 2)
-            for u, r in pair(step - 1)[:1]:
-                exponential(u, r)
             if second and live(i + 2):
                 copy_q_and_k(i + 2)
             if not second and i > 0 and live(i + 3):
                 copy_features(i + 3)
             if 0 < step < 3:
                 copy_features(step + 1)
-            if not second and live(i):
+            if (i > 0 and not second and live(i)) or step == 1:
                 gate_minus_one_of(i)
-            for u, r in pair(step - 1)[1:]:
-                exponential(u, r)
+            if step > 1:
+                for u, r in pair(step - 1):
+                    exponential(u, r)
             for u, r in pair(step + 1):
                 if mask_way(u, r) == "transposes":
                     mask_scores(u, r)
@@ -629,6 +641,8 @@ def tile_multiheadedselfattention_pa_t_kernel(
                 if live(i - 2):
                     invert_row_sum(i - 2)
             if step == 0:
+                gate_constants()
+                pooled_sum(0)
                 quantise_features(0)
                 quantise_features(1)
             if step == 2:
@@ -638,9 +652,10 @@ def tile_multiheadedselfattention_pa_t_kernel(
                 quantise_features(2)
             if step == 2:
                 quantise_features(3)
-            if step == 0:
+            if step == 2:
                 pass_stream(0)
-            if not second and live(i):
+                start_result(0)
+            if i > 0 and not second and live(i):
                 start_result(i)
             if step == 0:
                 for g in range(PASSES):

@@ -583,18 +583,19 @@ def tile_multiheadedselfattention_pa_t_kernel(
                 blend(i - 3)
             if second and live(i - 2):
                 quantise_e_and_v(i - 2)
-            for u, r in pair(step + 1):
+            for u, r in pair(step + 1)[:1]:
                 score_matmul(u, r)
-            if second:
-                if live(i - 1):
-                    for a in range(TILES):
-                        for g in range(PASSES):
-                            project_values(i - 1, a, g)
-                if live(i + 1):
-                    pooled_matmuls(i + 1)
-            elif live(i - 3):
+            if second and live(i - 1):
+                for a in range(TILES):
+                    for g in range(PASSES):
+                        project_values(i - 1, a, g)
+            if not second and live(i - 3):
                 for r in range(TILES):
                     attend(i - 3, r)
+            for u, r in pair(step + 1)[1:]:
+                score_matmul(u, r)
+            if second and live(i + 1):
+                pooled_matmuls(i + 1)
             if step == 1:
                 for u, r in pair(0):
                     exponential(u, r)

import math
from contextlib import ExitStack

import concourse.mybir as mybir
from concourse.masks import make_identity

F32 = mybir.dt.float32
BF16 = mybir.dt.bfloat16
U32 = mybir.dt.uint32
U8 = mybir.dt.uint8
FP8X4 = mybir.dt.float8_e4m3fn_x4
ALU = mybir.AluOpType
ACT = mybir.ActivationFunctionType
AXIS = mybir.AxisListType

P = 128
PACK = 4
BATCH = 8
SEQ = 512
TILES = SEQ // P
D_FEAT = 1024
PASSES = D_FEAT // (P * PACK)
HEADS = 4
HEAD = 128
D_MODEL = HEADS * HEAD
D_OUT = 640
UNITS = BATCH * HEADS
INV_SQRT_HEAD = 1.0 / math.sqrt(HEAD)
MASKED = -1.0e30
MATMUL_MASK_HEADS = 3

FLOPS = 2 * BATCH * SEQ * D_FEAT * D_MODEL + 2 * 2 * BATCH * HEADS * SEQ * SEQ * HEAD


def tile_multiheadedselfattention_pa_t_kernel(
    tc,
    q,
    k,
    pre_value_key,
    Wv,
    bv,
    value_key_masks,
    value_key_counts,
    overall_gain,
    overall_bias,
    pre_query,
    out,
):
    nc = tc.nc
    with ExitStack() as stack:
        stack.enter_context(tc.manual_schedule())
        const = stack.enter_context(tc.tile_pool(name="const", bufs=1))
        two = stack.enter_context(tc.tile_pool(name="two", bufs=2))
        three = stack.enter_context(tc.tile_pool(name="three", bufs=3))
        four = stack.enter_context(tc.tile_pool(name="four", bufs=4))
        five = stack.enter_context(tc.tile_pool(name="five", bufs=5))
        psum_scores = stack.enter_context(tc.psum_pool(name="psum_scores", bufs=4))
        psum_turn = stack.enter_context(tc.psum_pool(name="psum_turn", bufs=2))
        psum_one = stack.enter_context(tc.psum_pool(name="psum_one", bufs=1))

        kept = {}

        def live(u):
            return 0 <= u < UNITS

        def mask_way(u, r):
            if r > 0:
                return "transposes"
            return "matmul" if u % HEADS < MATMUL_MASK_HEADS else "vector"

        def head_columns(u):
            return slice((u % HEADS) * HEAD, (u % HEADS + 1) * HEAD)

        def load_mask_rows(b, queue):
            mask_rows = two.tile([P, SEQ], BF16)
            queue.dma_start(out=mask_rows[:], in_=value_key_masks[b].partition_broadcast(P))
            kept[("mask_rows", b)] = mask_rows

        def load_q_and_k(b, pieces=1):
            q_sb = three.tile([P, TILES, D_MODEL], BF16)
            k_sb = three.tile([P, TILES, D_MODEL], BF16)
            width = D_MODEL // pieces
            for c0 in range(0, D_MODEL, width):
                cols = slice(c0, c0 + width)
                for tile_sb, dram in ((q_sb, q), (k_sb, k)):
                    nc.sync.dma_start(
                        out=tile_sb[:, :, cols],
                        in_=dram[b].rearrange("(p r) c -> p r c", r=TILES)[:, :, cols],
                    )
            kept[("q", b)] = q_sb
            kept[("k", b)] = k_sb

        def load_features(b):
            feat_sb = two.tile([P, TILES, D_FEAT], BF16)
            nc.sync.dma_start(
                out=feat_sb[:], in_=pre_value_key[b].rearrange("(p r) c -> p r c", r=TILES)
            )
            kept[("feat", b)] = feat_sb

        def load_stream(b):
            stream_sb = four.tile([P, TILES, D_OUT], BF16)
            nc.sync.dma_start(
                out=stream_sb[:], in_=pre_query[b].rearrange("(p r) c -> p r c", r=TILES)
            )
            kept[("stream", b)] = stream_sb

        def load_batch(b):
            load_q_and_k(b)
            load_features(b)
            load_mask_rows(b, nc.sync)
            load_stream(b)

        mask_cols = const.tile([P, BATCH, TILES], BF16)
        nc.scalar.dma_start(
            out=mask_cols[:], in_=value_key_masks.rearrange("b (p a) -> p b a", a=TILES)
        )
        load_q_and_k(0, pieces=2)
        load_mask_rows(0, nc.scalar)
        counts = const.tile([P, BATCH], BF16)
        nc.scalar.dma_start(out=counts[:], in_=value_key_counts.partition_broadcast(P))
        gain = const.tile([P, HEADS], BF16)
        nc.scalar.dma_start(
            out=gain[:], in_=overall_gain.rearrange("a h c d -> (a h c d)").partition_broadcast(P)
        )
        gate_bias = const.tile([P, HEADS], BF16)
        nc.scalar.dma_start(
            out=gate_bias[:],
            in_=overall_bias.rearrange("a h c d -> (a h c d)").partition_broadcast(P),
        )
        load_features(0)
        w_raw = const.tile([P, PASSES, PACK, D_MODEL], BF16)
        nc.sync.dma_start(
            out=w_raw[:].rearrange("w g (u e) d -> w (g u) (e d)", u=2, e=2),
            in_=Wv.rearrange("(g u w e) d -> w (g u) (e d)", g=PASSES, u=2, e=2),
        )
        bv_rows = const.tile([P, D_MODEL], BF16)
        nc.scalar.dma_start(out=bv_rows[:], in_=bv.partition_broadcast(P))
        load_features(1)
        load_stream(0)

        ident_bf = const.tile([P, P], BF16)
        make_identity(nc, ident_bf[:])

        def keep_keys(b):
            kept_keys = two.tile([P, TILES, P], BF16)
            nc.gpsimd.tensor_tensor(
                out=kept_keys[:],
                in0=ident_bf[:].unsqueeze(1).to_broadcast([P, TILES, P]),
                in1=mask_cols[:, b, :].unsqueeze(2).to_broadcast([P, TILES, P]),
                op=ALU.mult,
            )
            kept[("kept_keys", b)] = kept_keys

        def spread_mask_cols(b):
            mask_bias = two.tile([P, TILES, P], F32)
            nc.gpsimd.tensor_scalar(
                out=mask_bias[:],
                in0=mask_cols[:, b, :].unsqueeze(2).to_broadcast([P, TILES, P]),
                scalar1=-1.0,
                scalar2=-MASKED,
                op0=ALU.add,
                op1=ALU.mult,
            )
            kept[("mask_bias", b)] = mask_bias

        def order_mask_rows(b):
            neg_mask_rows = two.tile([P, TILES, P], BF16)
            nc.gpsimd.tensor_scalar(
                out=neg_mask_rows[:],
                in0=kept[("mask_rows", b)][:].rearrange("p (x a) -> p a x", a=TILES),
                scalar1=-1.0,
                scalar2=MASKED,
                op0=ALU.add,
                op1=ALU.mult,
            )
            kept[("neg_mask_rows", b)] = neg_mask_rows

        minus_mean = const.tile([P, P], BF16)
        nc.vector.memset(minus_mean[:], -1.0 / P)
        prepare_masks = (keep_keys, spread_mask_cols, order_mask_rows)
        keep_keys(0)
        ident_f = const.tile([P, P], F32)
        make_identity(nc, ident_f[:])
        order_mask_rows(0)
        spread_mask_cols(0)

        w_grouped = const.tile([P, PASSES, D_MODEL * PACK], BF16, align_bytes=64)
        w_codes = const.tile([P, PASSES, D_MODEL], U32, align_bytes=64)
        w_scales = const.tile([P, PASSES, D_MODEL], U8, align_bytes=64)

        def group_weights(g):
            nc.gpsimd.tensor_scalar(
                out=w_grouped[:, g, :].rearrange("w (d t) -> w d t", t=PACK),
                in0=w_raw[:, g, :, :].rearrange("w t d -> w d t"),
                scalar1=1.0,
                scalar2=0.0,
                op0=ALU.mult,
                op1=ALU.add,
            )

        def quantise_weights(g):
            nc.vector.quantize_mx(
                out=w_codes[:, g, :].bitcast(FP8X4),
                scales=w_scales[:, g, :],
                in_=w_grouped[:, g, :],
            )

        inv_count = const.tile([P, BATCH], F32)
        half_gain = const.tile([P, HEADS], F32)
        half_gate_bias = const.tile([P, HEADS], F32)
        half_gain_over_count = const.tile([P, BATCH, HEADS], F32)

        def gate_constants():
            nc.vector.reciprocal(out=inv_count[:], in_=counts[:])
            nc.vector.tensor_scalar_mul(out=half_gain[:], in0=gain[:], scalar1=0.5 * INV_SQRT_HEAD)
            nc.vector.tensor_scalar_mul(out=half_gate_bias[:], in0=gate_bias[:], scalar1=0.5)
            nc.vector.tensor_tensor(
                out=half_gain_over_count[:],
                in0=half_gain[:].unsqueeze(1).to_broadcast([P, BATCH, HEADS]),
                in1=inv_count[:].unsqueeze(2).to_broadcast([P, BATCH, HEADS]),
                op=ALU.mult,
            )

        def turn_features(piece):
            b, a = piece // TILES, piece % TILES
            feat_words = kept[("feat", b)][:].bitcast(F32)
            turn_f = psum_turn.tile([P, PASSES, 2, P], F32, tag="turn")
            for g in range(PASSES):
                for u in range(2):
                    first = (2 * g + u) * P
                    nc.tensor.transpose(
                        out=turn_f[:, g, u, :],
                        in_=feat_words[:, a, first : first + P],
                        identity=ident_f[:],
                    )
            kept[("turn_f", piece)] = turn_f

        def copy_features(piece):
            turn_f = kept[("turn_f", piece)]
            feat_grouped = three.tile([P, PASSES * P * PACK], BF16, align_bytes=64)
            nc.scalar.copy(
                out=feat_grouped[:].bitcast(F32).rearrange("w (g x u) -> w g x u", g=PASSES, u=2),
                in_=turn_f[:].rearrange("w g u x -> w g x u"),
            )
            kept[("feat_grouped", piece)] = feat_grouped

        def quantise_features(piece):
            b, a = piece // TILES, piece % TILES
            if a == 0:
                feat_codes = two.tile([P, TILES, PASSES * P], U32, align_bytes=64)
                feat_scales = two.tile([P, TILES, PASSES * P], U8, align_bytes=64)
                kept[("feat_codes", b)] = feat_codes
                kept[("feat_scales", b)] = feat_scales
            nc.vector.quantize_mx(
                out=kept[("feat_codes", b)][:, a, :].bitcast(FP8X4),
                scales=kept[("feat_scales", b)][:, a, :],
                in_=kept[("feat_grouped", piece)][:],
            )

        def turn_q_and_k(u):
            b = u // HEADS
            turn_qk = psum_turn.tile([P, 2, TILES, P], BF16, tag="turn")
            for r in range(TILES):
                nc.tensor.transpose(
                    out=turn_qk[:, 0, r, :],
                    in_=kept[("q", b)][:, r, head_columns(u)],
                    identity=ident_bf[:],
                )
            for a in range(TILES):
                nc.tensor.transpose(
                    out=turn_qk[:, 1, a, :],
                    in_=kept[("k", b)][:, a, head_columns(u)],
                    identity=kept[("kept_keys", b)][:, a, :],
                )
            kept[("turn_qk", u)] = turn_qk

        def copy_q_and_k(u):
            turn_qk = kept[("turn_qk", u)]
            q_turned = three.tile([P, TILES, P], BF16)
            nc.scalar.copy(out=q_turned[:], in_=turn_qk[:, 0, :, :])
            k_turned = three.tile([P, TILES, P], BF16)
            key_sum_f = three.tile([P, 1], F32)
            nc.scalar.activation(
                out=k_turned[:], in_=turn_qk[:, 1, :, :], func=ACT.Copy, accum_out=key_sum_f[:]
            )
            key_sum = three.tile([P, 2], BF16)
            nc.gpsimd.tensor_scalar(
                out=key_sum[:, 0:1],
                in0=key_sum_f[:],
                scalar1=1.0,
                scalar2=0.0,
                op0=ALU.mult,
                op1=ALU.add,
            )
            nc.gpsimd.tensor_tensor(
                out=key_sum[:, 1:2], in0=key_sum_f[:], in1=key_sum[:, 0:1], op=ALU.subtract
            )
            kept[("q_turned", u)] = q_turned
            kept[("k_turned", u)] = k_turned
            kept[("key_sum", u)] = key_sum

        def pooled_matmuls(u):
            pooled_ps = psum_one.tile([P, TILES, 2], F32, tag="h")
            for r in range(TILES):
                nc.tensor.matmul(
                    out=pooled_ps[:, r, :],
                    lhsT=kept[("q_turned", u)][:, r, :],
                    rhs=kept[("key_sum", u)][:],
                    start=True,
                    stop=True,
                )
            kept[("pooled_ps", u)] = pooled_ps

        def pooled_sum(u):
            pooled = three.tile([P, TILES], F32)
            nc.vector.tensor_reduce(
                out=pooled[:], in_=kept[("pooled_ps", u)][:], axis=AXIS.X, op=ALU.add
            )
            kept[("pooled", u)] = pooled

        def gate_minus_one_of(u):
            b, n = u // HEADS, u % HEADS
            tanh_half_z = three.tile([P, TILES], F32)
            nc.scalar.activation(
                out=tanh_half_z[:],
                in_=kept[("pooled", u)][:],
                func=ACT.Tanh,
                scale=half_gain_over_count[:, b, n : n + 1],
                bias=half_gate_bias[:, n : n + 1],
            )
            gate_minus_one = five.tile([P, TILES], F32)
            nc.gpsimd.tensor_scalar(
                out=gate_minus_one[:],
                in0=tanh_half_z[:],
                scalar1=0.5,
                scalar2=-0.5,
                op0=ALU.mult,
                op1=ALU.add,
            )
            kept[("gate_minus_one", u)] = gate_minus_one

        def invert_row_sum(u):
            inv_sum = three.tile([P, TILES], F32)
            nc.vector.reciprocal(out=inv_sum[:], in_=kept[("row_sum", u)][:])
            kept[("inv_sum", u)] = inv_sum

        def gate_over_row_sum(u):
            gate_over_sum = three.tile([P, TILES], F32)
            nc.vector.scalar_tensor_tensor(
                out=gate_over_sum[:],
                in0=kept[("gate_minus_one", u)][:],
                scalar=1.0,
                in1=kept[("inv_sum", u)][:],
                op0=ALU.add,
                op1=ALU.mult,
            )
            kept[("gate_over_sum", u)] = gate_over_sum

        def pass_stream(b):
            result = three.tile([P, TILES, D_OUT], F32)
            nc.gpsimd.tensor_scalar(
                out=result[:, :, D_MODEL:D_OUT],
                in0=kept[("stream", b)][:, :, D_MODEL:D_OUT],
                scalar1=1.0,
                scalar2=0.0,
                op0=ALU.mult,
                op1=ALU.add,
            )
            nc.sync.dma_start(
                out=out[b].rearrange("(p r) c -> p r c", r=TILES)[:, :, D_MODEL:D_OUT],
                in_=result[:, :, D_MODEL:D_OUT],
            )
            kept[("result", b)] = result

        def start_result(u):
            b, n = u // HEADS, u % HEADS
            stream_sb = kept[("stream", b)]
            nc.gpsimd.tensor_tensor(
                out=kept[("result", b)][:, :, head_columns(u)],
                in0=stream_sb[:, :, head_columns(u)],
                in1=kept[("gate_minus_one", u)][:].unsqueeze(2).to_broadcast([P, TILES, HEAD]),
                op=ALU.mult,
            )

        def score_matmul(u, r):
            scores_ps = psum_scores.tile([P, TILES, P], F32, tag="scores")
            nc.tensor.matmul(
                out=scores_ps[:].rearrange("p a x -> p (a x)"),
                lhsT=kept[("q_turned", u)][:, r, :],
                rhs=kept[("k_turned", u)][:].rearrange("c a x -> c (a x)"),
                start=True,
                stop=(mask_way(u, r) == "vector"),
            )
            if mask_way(u, r) == "matmul":
                nc.tensor.matmul(
                    out=scores_ps[:].rearrange("p a x -> p (a x)"),
                    lhsT=minus_mean[:],
                    rhs=kept[("neg_mask_rows", u // HEADS)][:].rearrange("p a x -> p (a x)"),
                    start=False,
                    stop=True,
                )
            kept[("scores_ps", u, r)] = scores_ps

        def mask_scores(u, r):
            for a in range(TILES):
                nc.tensor.matmul(
                    out=kept[("scores_ps", u, r)][:, a, :],
                    lhsT=kept[("mask_bias", u // HEADS)][:, a, :],
                    rhs=ident_f[:],
                    is_transpose=True,
                    start=False,
                    stop=(a == TILES - 1),
                )

        def negate_scores(u, r):
            if r == 0:
                neg_scores = three.tile([P, TILES, SEQ], F32)
                neg_max = three.tile([P, TILES], F32)
                kept[("neg_scores", u)] = neg_scores
                kept[("neg_max", u)] = neg_max
            if mask_way(u, r) != "vector":
                nc.vector.tensor_scalar(
                    out=kept[("neg_scores", u)][:, r, :],
                    in0=kept[("scores_ps", u, r)][:].rearrange("p a x -> p (a x)"),
                    scalar1=-INV_SQRT_HEAD,
                    scalar2=None,
                    op0=ALU.mult,
                    op1=ALU.min,
                    accum_out=kept[("neg_max", u)][:, r : r + 1],
                )
            else:
                nc.vector.scalar_tensor_tensor(
                    out=kept[("neg_scores", u)][:, r, :],
                    in0=kept[("scores_ps", u, r)][:].rearrange("p a x -> p (a x)"),
                    scalar=-INV_SQRT_HEAD,
                    in1=kept[("neg_mask_rows", u // HEADS)][:].rearrange("p a x -> p (a x)"),
                    op0=ALU.mult,
                    op1=ALU.add,
                )

        def row_minimum(u, r):
            nc.vector.tensor_reduce(
                out=kept[("neg_max", u)][:, r : r + 1],
                in_=kept[("neg_scores", u)][:, r, :],
                axis=AXIS.X,
                op=ALU.min,
            )

        def exponential(u, r):
            if r == 0:
                e_sb = two.tile([P, TILES, SEQ], BF16)
                row_sum = three.tile([P, TILES], F32)
                kept[("e_sb", u)] = e_sb
                kept[("row_sum", u)] = row_sum
            nc.scalar.activation(
                out=kept[("e_sb", u)][:, r, :].rearrange("p (u w e) -> p u w e", u=2, e=2),
                in_=kept[("neg_scores", u)][:, r, :].rearrange("p (u e w) -> p u w e", u=2, e=2),
                func=ACT.Exp,
                bias=kept[("neg_max", u)][:, r : r + 1],
                scale=-1.0,
                accum_out=kept[("row_sum", u)][:, r : r + 1],
            )

        def turn_e(u, half):
            e_words = kept[("e_sb", u)][:].bitcast(F32)
            turn_half = psum_turn.tile([P, 2, 2, P], F32, tag="turn")
            for rr in range(2):
                for u2 in range(2):
                    nc.tensor.transpose(
                        out=turn_half[:, rr, u2, :],
                        in_=e_words[:, 2 * half + rr, u2 * P : (u2 + 1) * P],
                        identity=ident_f[:],
                    )
            kept[("turn_half", u, half)] = turn_half

        def copy_e(u, half):
            if half == 0:
                e_grouped = two.tile([P, SEQ * PACK], BF16, align_bytes=64)
                kept[("e_grouped", u)] = e_grouped
            nc.scalar.copy(
                out=kept[("e_grouped", u)][:]
                .bitcast(F32)
                .rearrange("w (r i u) -> w r i u", r=TILES, u=2)[:, 2 * half : 2 * half + 2],
                in_=kept[("turn_half", u, half)][:].rearrange("w r u i -> w r i u"),
            )

        def project_values(u, a, g):
            b = u // HEADS
            if a == 0 and g == 0:
                v_ps = psum_one.tile([P, TILES, HEAD], F32, tag="v")
                kept[("v_ps", u)] = v_ps
            key_cols = slice(g * P, (g + 1) * P)
            nc.tensor.matmul_mx(
                out=kept[("v_ps", u)][:, a, :],
                lhsT=kept[("feat_codes", b)][:, a, key_cols].bitcast(FP8X4),
                lhsT_scale=kept[("feat_scales", b)][:, a, key_cols],
                rhs=w_codes[:, g, head_columns(u)].bitcast(FP8X4),
                rhs_scale=w_scales[:, g, head_columns(u)],
                start=(g == 0),
                stop=(g == PASSES - 1),
            )

        def add_value_bias(u):
            v_grouped = two.tile([P, HEAD * PACK], BF16, align_bytes=64)
            nc.vector.tensor_tensor(
                out=v_grouped[:].rearrange("p (d a) -> p d a", a=PACK),
                in0=kept[("v_ps", u)][:].rearrange("p a d -> p d a"),
                in1=bv_rows[:, head_columns(u)].unsqueeze(2).to_broadcast([P, HEAD, PACK]),
                op=ALU.add,
            )
            kept[("v_grouped", u)] = v_grouped

        def quantise_e_and_v(u):
            e_codes = two.tile([P, SEQ], U32, align_bytes=64)
            e_scales = two.tile([P, SEQ], U8, align_bytes=64)
            nc.vector.quantize_mx(
                out=e_codes[:].bitcast(FP8X4), scales=e_scales[:], in_=kept[("e_grouped", u)][:]
            )
            v_codes = two.tile([P, HEAD], U32, align_bytes=64)
            v_scales = two.tile([P, HEAD], U8, align_bytes=64)
            nc.vector.quantize_mx(
                out=v_codes[:].bitcast(FP8X4), scales=v_scales[:], in_=kept[("v_grouped", u)][:]
            )
            kept[("e_codes", u)] = e_codes
            kept[("e_scales", u)] = e_scales
            kept[("v_codes", u)] = v_codes
            kept[("v_scales", u)] = v_scales

        def attend(u, r):
            if r == 0:
                h_ps = psum_one.tile([P, TILES, HEAD], F32, tag="h")
                kept[("h_ps", u)] = h_ps
            query_cols = slice(r * P, (r + 1) * P)
            nc.tensor.matmul_mx(
                out=kept[("h_ps", u)][:, r, :],
                lhsT=kept[("e_codes", u)][:, query_cols].bitcast(FP8X4),
                lhsT_scale=kept[("e_scales", u)][:, query_cols],
                rhs=kept[("v_codes", u)][:].bitcast(FP8X4),
                rhs_scale=kept[("v_scales", u)][:],
                start=True,
                stop=True,
            )

        def blend(u):
            b = u // HEADS
            result = kept[("result", b)]
            for r in range(TILES):
                nc.vector.scalar_tensor_tensor(
                    out=result[:, r, head_columns(u)],
                    in0=kept[("h_ps", u)][:, r, :],
                    scalar=kept[("gate_over_sum", u)][:, r : r + 1],
                    in1=result[:, r, head_columns(u)],
                    op0=ALU.mult,
                    op1=ALU.subtract,
                )
            nc.sync.dma_start(
                out=out[b].rearrange("(p r) c -> p r c", r=TILES)[:, :, head_columns(u)],
                in_=result[:, :, head_columns(u)],
            )

        def pair(n):
            return [(n // 2, 2 * (n % 2) + r) for r in range(2)] if 0 <= n < 2 * UNITS else []

        for u in range(2):
            turn_q_and_k(u)
            copy_q_and_k(u)
        for u, r in pair(0):
            score_matmul(u, r)
        for u, r in pair(0):
            if mask_way(u, r) == "transposes":
                mask_scores(u, r)
        pooled_matmuls(0)
        load_q_and_k(1)
        load_mask_rows(1, nc.sync)
        load_stream(1)
        for piece in range(2):
            turn_features(piece)
            copy_features(piece)
        prepare_batch = prepare_masks + (pass_stream,)
        for step in range(2 * UNITS + 6):
            i, second = step // 2, step % 2 == 1
            if second and live(i - 3):
                blend(i - 3)
            if second and live(i - 2):
                quantise_e_and_v(i - 2)
            for u, r in pair(step + 1)[:1]:
                score_matmul(u, r)
            if second and live(i - 1):
                for a in range(TILES):
                    for g in range(PASSES):
                        project_values(i - 1, a, g)
            if not second and live(i - 3):
                for r in range(TILES):
                    attend(i - 3, r)
            for u, r in pair(step + 1)[1:]:
                score_matmul(u, r)
            if second and live(i + 1):
                pooled_matmuls(i + 1)
            if step == 1:
                for u, r in pair(0):
                    exponential(u, r)
            for u, r in pair(step - 3)[:1]:
                copy_e(u, r // 2)
            if second and live(i + 2):
                copy_q_and_k(i + 2)
            if not second and i > 0 and live(i + 3):
                copy_features(i + 3)
            if 0 < step < 3:
                copy_features(step + 1)
            if (i > 0 and not second and live(i)) or step == 1:
                gate_minus_one_of(i)
            if step > 1:
                for u, r in pair(step - 1):
                    exponential(u, r)
            for u, r in pair(step + 1):
                if mask_way(u, r) == "transposes":
                    mask_scores(u, r)
            for u, r in pair(step - 2)[:1]:
                turn_e(u, r // 2)
            if not second:
                if live(i + 2):
                    turn_q_and_k(i + 2)
            elif live(i + 4):
                turn_features(i + 4)
            if step < 2:
                turn_features(step + 2)
            for u, r in pair(step):
                negate_scores(u, r)
            for u, r in pair(step):
                if mask_way(u, r) == "vector":
                    row_minimum(u, r)
            if second:
                if live(i + 1):
                    pooled_sum(i + 1)
                if live(i - 2):
                    gate_over_row_sum(i - 2)
                if i > 0 and live(i + 3):
                    quantise_features(i + 3)
            else:
                if live(i - 2):
                    add_value_bias(i - 2)
                if live(i - 2):
                    invert_row_sum(i - 2)
            if step == 0:
                gate_constants()
                pooled_sum(0)
                quantise_features(0)
                quantise_features(1)
            if step == 2:
                for g in range(PASSES):
                    quantise_weights(g)
            if step == 1:
                quantise_features(2)
            if step == 2:
                quantise_features(3)
            if step == 2:
                pass_stream(0)
                start_result(0)
            if i > 0 and not second and live(i):
                start_result(i)
            if step == 0:
                for g in range(PASSES):
                    group_weights(g)
            if second and i // HEADS + 1 < BATCH:
                prepare_batch[i % HEADS](i // HEADS + 1)
            if second and i % HEADS == 1 and i // HEADS + 2 < BATCH:
                load_batch(i // HEADS + 2)
